import numpy as np
import ml_dtypes


def mxq(x, axis, fmt="e4m3"):
    dtype, down = {"e4m3": (ml_dtypes.float8_e4m3fn, 7), "e5m2": (ml_dtypes.float8_e5m2, 14)}[fmt]
    v = np.moveaxis(np.asarray(x, np.float32).astype(ml_dtypes.bfloat16).astype(np.float64), axis, -1)
    blocks = v.reshape(v.shape[:-1] + (-1, 32))
    amax = np.abs(blocks).max(-1, keepdims=True)
    byte = np.maximum(np.where(amax > 0, np.frexp(amax)[1] - 1 + 127, 0) - down, 1)
    scale = np.exp2(byte - 127.0)
    codes = (blocks / scale).astype(np.float32).astype(dtype).astype(np.float64)
    return np.moveaxis((codes * scale).reshape(v.shape), -1, axis)


WIDE = False


def mx_kscale(k):
    if not WIDE:
        return np.ones(k)
    levels = np.array([10, -10, 5, -5, 0])
    if k % 512:
        return np.exp2(np.random.permutation(np.resize(levels, k // 32))).repeat(32)
    a = np.empty((k // 512, 16))
    for p in range(k // 512):
        a[p, :8] = np.random.permutation(np.resize(levels, 8))
        for g in range(8):
            far = levels[np.abs(levels - a[p, g]) >= 10]
            a[p, g + 8] = far[np.random.randint(len(far))]
    return np.exp2(a.ravel()).repeat(32)


BF16 = ml_dtypes.bfloat16


def bf(x):
    return np.asarray(x, np.float32).astype(BF16)


def f64(x):
    return np.asarray(x).astype(np.float64)


B, N, ATTR, STATE, REL, G, NF = 4, 32, 4, 16, 9, 32, 1024


def draw0():
    rn = np.random.standard_normal
    s, u, t = mx_kscale(NF), mx_kscale(NF), mx_kscale(NF)
    rp_rows = np.concatenate([s, u, u])
    pp_rows = np.concatenate([u, t])
    pp_scale = np.concatenate([np.full(NF, 1.0 / np.sqrt(NF)), np.full(NF, 1.0 / np.sqrt(NF * N))])
    return {
        "rel_enc": bf(np.maximum(rn((B, N, N, NF)) * 1.1, 0.0) * s),
        "obj": bf(np.maximum(rn((B, N, NF)) * 1.1, 0.0) * u),
        "rp_w": bf(rn((3 * NF, NF)) * 2.0 / np.sqrt(3 * NF * N) / rp_rows[:, None] * t),
        "rp_b": bf(rn(NF) * 0.1 * t),
        "pp_w": bf(rn((2 * NF, NF)) * (pp_scale / pp_rows)[:, None]),
        "pp_b": bf(rn(NF) * 0.1),
    }


def core(rel_enc, obj, rp_w, rp_b, pp_w, pp_b):
    rp, pp = f64(rp_w), f64(pp_w)
    oq = mxq(f64(obj), 2, "e4m3")
    e_rel = mxq(f64(rel_enc), 3, "e4m3") @ mxq(rp[:NF], 0, "e4m3")
    e_recv = oq @ mxq(rp[NF:2 * NF], 0, "e4m3")
    e_send = oq @ mxq(rp[2 * NF:], 0, "e4m3")
    rel_eff = np.maximum(e_rel + e_recv[:, :, None, :] + e_send[:, None, :, :] + f64(rp_b), 0.0)
    agg = rel_eff.sum(axis=2)
    p_obj = oq @ mxq(pp[:NF], 0, "e4m3")
    p_agg = mxq(agg, 2, "e4m3") @ mxq(pp[NF:], 0, "e4m3")
    return np.maximum(p_obj + p_agg + f64(pp_b), 0.0)


def e4m3fn_bytes(y):
    return np.clip(np.asarray(y, np.float64), -448.0, 448.0).astype(np.float32).astype(ml_dtypes.float8_e4m3fn).view(np.uint8)


def e4m3fn_values(b):
    return np.asarray(b, np.uint8).view(ml_dtypes.float8_e4m3fn).astype(np.float64)


def setup_inputs():
    d = draw0()
    x0 = np.asarray(d['rel_enc']).astype(np.float64)
    s = (np.max(np.abs(x0), axis=(0, 1, 2), keepdims=True) / 448.0).astype(np.float32)
    out = {}
    for k, v in d.items():
        if k == 'rel_enc':
            out['rel_enc_bytes'] = e4m3fn_bytes(x0 / s.astype(np.float64))
            out['rel_enc_scale'] = s
        else:
            out[k] = v
    return out


def reference(rel_enc_bytes, rel_enc_scale, obj, rp_w, rp_b, pp_w, pp_b):
    return core(e4m3fn_values(rel_enc_bytes) * rel_enc_scale.astype(np.float64), obj, rp_w, rp_b, pp_w, pp_b)

@@ -1,0 +1,350 @@
+from contextlib import ExitStack
+
+import concourse.mybir as mybir
+from concourse.masks import make_identity
+
+P = 128
+NF = 1024
+K_PASS = 512
+PASSES = NF // K_PASS
+GRAPHS = 4
+N = 32
+GROUP = 256
+GROUPS = GRAPHS * N * N // GROUP
+RECV_PER_GROUP = GROUP // N
+
+F32 = mybir.dt.float32
+BF16 = mybir.dt.bfloat16
+U32 = mybir.dt.uint32
+I32 = mybir.dt.int32
+U8 = mybir.dt.uint8
+FP8 = mybir.dt.float8_e4m3fn
+FP8X4 = mybir.dt.float8_e4m3fn_x4
+ALU = mybir.AluOpType
+ACT = mybir.ActivationFunctionType
+
+FLOPS = 2 * GRAPHS * N * N * NF * NF + 4 * 2 * GRAPHS * N * NF * NF
+
+
+def tile_compositionalkoopmanoperators_pa_kernel(
+    tc, rel_bytes, rel_scale, obj, rp_w, rp_b, pp_w, pp_b, out
+):
+    nc = tc.nc
+    rel_rows = rel_bytes.rearrange("b i j k -> (b i j) k").rearrange("(g p t) k -> g p (t k)", p=P, t=2)
+    obj_rows = obj.rearrange("b n k -> (b n) k").rearrange("(x t) k -> t x k", t=2)
+    out_rows = out.rearrange("b n k -> (b n) k").rearrange("(x t) k -> t x k", t=2)
+
+    with ExitStack() as ctx:
+        keep = ctx.enter_context(tc.tile_pool(name="keep", bufs=1))
+        loads = ctx.enter_context(tc.tile_pool(name="loads", bufs=6))
+        work = ctx.enter_context(tc.tile_pool(name="work", bufs=3))
+        psum = ctx.enter_context(tc.psum_pool(name="psum", bufs=2))
+
+        def kept(shape, dtype, name):
+            return keep.tile(shape, dtype, name=name, tag=name, align_bytes=64)
+
+        ident = kept([P, P], F32, "ident")
+        make_identity(nc, ident[:])
+
+        ctx.enter_context(tc.manual_schedule())
+
+        sc8 = kept([P, NF // P], F32, "sc8")
+        nc.scalar.dma_start(out=sc8[:], in_=rel_scale.rearrange("a b c (p e) -> p (a b c e)", p=P))
+        ob = kept([P, NF], BF16, "ob")
+        for t in range(2):
+            nc.scalar.dma_start(out=ob[64 * t : 64 * t + 64, :], in_=obj_rows[t])
+        rpb = kept([P, 2, 4], BF16, "rpb")
+        with nc.allow_non_contiguous_dma(reason="bias"):
+            nc.scalar.dma_start(out=rpb[:], in_=rp_b.rearrange("(q p t) -> p q t", p=P, t=4))
+
+        raws = {}
+        rel_raw = {}
+
+        def load_rel(g):
+            rb = loads.tile([P, 2 * NF], U8, name="rb", tag="rb", align_bytes=64)
+            nc.sync.dma_start(out=rb[:], in_=rel_rows[g])
+            rel_raw[g] = rb
+
+        def load_w(key, w, row, g, q):
+            raw = loads.tile([P, 4, 512], BF16, name="raw", tag="raw", bufs=12, align_bytes=64)
+            r0 = row + K_PASS * g
+            nc.sync.dma_start(
+                out=raw[:],
+                in_=w[r0 : r0 + K_PASS, 512 * q : 512 * q + 512].rearrange("(p j) n -> p j n", j=4),
+            )
+            raws[key, g, q] = raw
+
+        rp_rows = {"r": 0, "i": NF, "s": 2 * NF}
+
+        load_rel(0)
+        for key in ("r", "s", "i"):
+            for g in range(PASSES):
+                load_w(key, rp_w, rp_rows[key], g, 0)
+        for g in range(1, 4):
+            load_rel(g)
+        for key in ("r", "s", "i"):
+            for g in range(PASSES):
+                load_w(key, rp_w, rp_rows[key], g, 1)
+
+        scale = kept([P, NF], F32, "scale")
+        scale_v = scale[:].rearrange("m (p e) -> m e p", e=8)
+        for half in range(2):
+            bank = psum.tile([P, 4, P], F32, name="misc", tag="misc")
+            for e in range(4):
+                c = 4 * half + e
+                nc.tensor.transpose(bank[:, e, :], sc8[:, c : c + 1].to_broadcast([P, P]), ident[:])
+            nc.scalar.copy(out=scale_v[:, 4 * half : 4 * half + 4, :], in_=bank[:])
+
+        og = kept([P, PASSES * P * 4], BF16, "og")
+        bank = psum.tile([P, 4, P], F32, name="misc", tag="misc")
+        words = ob[:].bitcast(F32)
+        for g in range(PASSES):
+            for u in range(2):
+                nc.tensor.transpose(bank[:, 2 * g + u, :], words[:, 256 * g + u : 256 * g + 256 : 2], ident[:])
+        nc.scalar.copy(
+            out=og[:].bitcast(F32).rearrange("p (g r u) -> p g r u", g=2, u=2),
+            in_=bank[:].rearrange("p (g u) r -> p g r u", g=2),
+        )
+        oc = kept([P, PASSES * P], U32, "oc")
+        osc = kept([P, PASSES * P], U8, "osc")
+        nc.gpsimd.memset(osc[:].bitcast(I32), 0)
+
+        codes = {}
+        scales = {}
+        rbias = {}
+        repc = {}
+        reps = {}
+
+        def weight_ig(key, g, q, h, engine):
+            wg = work.tile([P, 1024], BF16, name="wg", tag="wg", bufs=4, align_bytes=64)
+            engine(
+                out=wg[:].rearrange("p (t m j) -> p t m j", t=2, j=4),
+                in_=raws[key, g, q][:].rearrange("p j (m t) -> p t m j", t=4)[:, 2 * h : 2 * h + 2],
+            )
+            return wg
+
+        def weight_q(key, g, q, h, wg):
+            name = "w%s%d%d%d" % (key, g, q, h)
+            c = kept([P, 256], U32, name + "c")
+            s = kept([P, 256], U8, name + "s")
+            nc.vector.quantize_mx(out=c[:].bitcast(FP8X4), scales=s[:], in_=wg[:])
+            codes[key, g, q, h] = c
+            scales[key, g, q, h] = s
+
+        def weights(q, h):
+            first = q == 0 and h == 0
+            order = [(key, g) for key in ("r", "s", "i") for g in range(PASSES)]
+            pending = []
+            for key, g in order:
+                eng = nc.scalar.copy if first and key == "s" else nc.vector.tensor_copy
+                pending.append((key, g, weight_ig(key, g, q, h, eng)))
+                if len(pending) > 2:
+                    k0, g0, w0 = pending.pop(0)
+                    weight_q(k0, g0, q, h, w0)
+            for k0, g0, w0 in pending:
+                weight_q(k0, g0, q, h, w0)
+
+        def receivers(q, h):
+            bank = psum.tile([P, 2, P], F32, name="misc", tag="misc")
+            for n in range(2):
+                for g in range(PASSES):
+                    nc.tensor.matmul_mx(
+                        out=bank[:, n, :],
+                        lhsT=codes["i", g, q, h][:, 128 * n : 128 * n + 128].bitcast(FP8X4),
+                        lhsT_scale=scales["i", g, q, h][:, 128 * n : 128 * n + 128],
+                        rhs=oc[:, P * g : P * g + P].bitcast(FP8X4),
+                        rhs_scale=osc[:, P * g : P * g + P],
+                        start=(g == 0),
+                        stop=(g == PASSES - 1),
+                    )
+            rb = kept([P, 2, P], F32, "rbias%d%d" % (q, h))
+            for n in range(2):
+                t = 2 * h + n
+                nc.scalar.activation(rb[:, n, :], bank[:, n, :], ACT.Identity, bias=rpb[:, q, t : t + 1])
+            rbias[q, h] = rb
+
+        def replicate(b):
+            c = work.tile([P, PASSES * GROUP], U32, name="repc", tag="repc", bufs=4, align_bytes=64)
+            s = work.tile([P, PASSES * GROUP], U8, name="reps", tag="reps", bufs=4, align_bytes=64)
+            for dst, src, w in ((c, oc, 16), (s, osc, 4)):
+                for g in range(PASSES):
+                    nc.vector.tensor_copy(
+                        out=dst[:].bitcast(I32).rearrange("p (g t i w) -> p g t i w", g=2, t=2, i=8)[:, g],
+                        in_=src[:].bitcast(I32).rearrange("p (g t b w) -> p g t b w", g=2, t=2, b=4)[:, g, :, b, :]
+                        .unsqueeze(2)
+                        .to_broadcast([P, 2, 8, w]),
+                    )
+            repc[b] = c
+            reps[b] = s
+
+        wide = {}
+        turned = {}
+        grouped = {}
+        rel_codes = {}
+        rel_scales = {}
+
+        def widen(g):
+            for t in range(2):
+                wb = work.tile([P, NF], BF16, name="wb", tag="wb", bufs=4, align_bytes=64)
+                nc.vector.tensor_tensor(
+                    out=wb[:], in0=rel_raw[g][:, NF * t : NF * t + NF].bitcast(FP8), in1=scale[:], op=ALU.mult
+                )
+                wide[g, t] = wb
+
+        def turn(g):
+            for t in range(2):
+                bank = psum.tile([P, 4, P], F32, name="tr", tag="tr")
+                words = wide[g, t][:].bitcast(F32)
+                for kp in range(PASSES):
+                    for u in range(2):
+                        nc.tensor.transpose(
+                            bank[:, 2 * kp + u, :], words[:, 256 * kp + u : 256 * kp + 256 : 2], ident[:]
+                        )
+                turned[g, t] = bank
+
+        def empty(g):
+            grp = work.tile([P, PASSES * GROUP * 4], BF16, name="grp", tag="grp", align_bytes=64)
+            view = grp[:].bitcast(F32).rearrange("p (g t r u) -> p g t r u", g=2, t=2, u=2)
+            for t in range(2):
+                nc.scalar.copy(out=view[:, :, t], in_=turned[g, t][:].rearrange("p (g u) r -> p g r u", g=2))
+            grouped[g] = grp
+
+        def quantise(g):
+            c = kept([P, PASSES * GROUP], U32, "rc%d" % g)
+            s = kept([P, PASSES * GROUP], U8, "rs%d" % g)
+            nc.vector.quantize_mx(out=c[:].bitcast(FP8X4), scales=s[:], in_=grouped[g][:])
+            rel_codes[g] = c
+            rel_scales[g] = s
+
+        agg = [kept([P, 4, P], F32, "agg%d" % q) for q in range(2)]
+
+        def unit(g, q, h):
+            b = g // 4
+            bank = psum.tile([P, 2, GROUP], F32, name="acc", tag="acc", bufs=4)
+            for n in range(2):
+                cols = slice(128 * n, 128 * n + 128)
+                for i, (key, mc, ms) in enumerate((("s", repc[b], reps[b]), ("r", rel_codes[g], rel_scales[g]))):
+                    for kp in range(PASSES):
+                        nc.tensor.matmul_mx(
+                            out=bank[:, n, :],
+                            lhsT=codes[key, kp, q, h][:, cols].bitcast(FP8X4),
+                            lhsT_scale=scales[key, kp, q, h][:, cols],
+                            rhs=mc[:, GROUP * kp : GROUP * kp + GROUP].bitcast(FP8X4),
+                            rhs_scale=ms[:, GROUP * kp : GROUP * kp + GROUP],
+                            start=(i == 0 and kp == 0),
+                            stop=(i == 1 and kp == PASSES - 1),
+                        )
+            junk = work.tile([P, 2, RECV_PER_GROUP, N], BF16, name="junk", tag="junk", bufs=4)
+            for n in range(2):
+                view = bank[:, n, :].rearrange("p (t i w) -> p i t w", t=2, i=RECV_PER_GROUP)
+                for il in range(RECV_PER_GROUP):
+                    i = RECV_PER_GROUP * (g % 4) + il
+                    col = 64 * (i % 2) + 16 * b + i // 2
+                    nc.scalar.activation(
+                        junk[:, n, il, :].rearrange("p (t w) -> p t w", t=2),
+                        view[:, il],
+                        ACT.Relu,
+                        bias=rbias[q, h][:, n, col : col + 1],
+                        accum_out=agg[q][:, 2 * h + n, col : col + 1],
+                    )
+
+        sets = [(0, 0), (0, 1), (1, 0), (1, 1)]
+        tasks = [("r", 0), ("w", 0), ("r", 1), ("w", 1), ("r", 2), ("r", 3), ("w", 2), ("r", 4), ("r", 5), ("w", 3)]
+        tasks += [("r", g) for g in range(6, GROUPS)]
+        tasks += [("o", n) for n in range(8)]
+        cost = {"r": 2.2, "w": 4.6, "o": 1.6}
+        unit_cost = 1.05
+
+        late = [("g", g) for g in range(4, GROUPS)]
+        late += [("o", key, row, g, q) for key, row in (("o", 0), ("a", NF)) for g in range(PASSES) for q in range(2)]
+        late_n = 0
+
+        ready_groups = []
+        ready_sets = []
+        queue = []
+        budget = 0.0
+        fresh_group = None
+        last_rel = None
+
+        for kind, n in tasks + [("end", 0), ("end", 1)]:
+            new_units = []
+            for item in late[late_n : late_n + 2]:
+                if item[0] == "g":
+                    load_rel(item[1])
+                else:
+                    load_w(item[1], pp_w, item[2], item[3], item[4])
+            late_n += 2
+            if kind == "r":
+                widen(n)
+            elif kind == "w":
+                q, h = sets[n]
+                if n == 0:
+                    nc.vector.quantize_mx(out=oc[:].bitcast(FP8X4), scales=osc[:], in_=og[:])
+                weights(q, h)
+            elif kind == "o":
+                key, g, q = ("o", "a")[n // 4], (n // 2) % 2, n % 2
+                wg = work.tile([P, 512, 4], BF16, name="og4", tag="og4", bufs=2, align_bytes=64)
+                nc.vector.tensor_copy(out=wg[:], in_=raws[key, g, q][:].rearrange("p j n -> p n j"))
+                c = kept([P, 512], U32, "w%s%d%dc" % (key, g, q))
+                s = kept([P, 512], U8, "w%s%d%ds" % (key, g, q))
+                nc.vector.quantize_mx(
+                    out=c[:].bitcast(FP8X4), scales=s[:], in_=wg[:].rearrange("p n j -> p (n j)")
+                )
+                codes[key, g, q] = c
+                scales[key, g, q] = s
+            if last_rel is not None:
+                empty(last_rel)
+                if last_rel % 4 == 0:
+                    replicate(last_rel // 4)
+                quantise(last_rel)
+                new_units += [(last_rel, s) for s in ready_sets]
+                ready_groups.append(last_rel)
+                last_rel = None
+            if kind == "w":
+                receivers(q, h)
+                new_units += [(g, (q, h)) for g in ready_groups]
+                ready_sets.append((q, h))
+            budget = min(budget + cost.get(kind, 1000.0), 1000.0)
+            while queue and budget >= unit_cost:
+                g, s = queue.pop(0)
+                unit(g, s[0], s[1])
+                budget -= unit_cost
+            if not queue:
+                budget = 0.0
+            queue += new_units
+            if kind == "r":
+                turn(n)
+                last_rel = n
+
+        pb = kept([P, NF], BF16, "pb")
+        nc.sync.dma_start(out=pb[:], in_=pp_b.partition_broadcast(P))
+        ac = []
+        asc = []
+        for q in range(2):
+            ag = work.tile([P, P, 4], BF16, name="ag", tag="ag", bufs=2, align_bytes=64)
+            nc.vector.tensor_copy(out=ag[:], in_=agg[q][:].rearrange("p t c -> p c t"))
+            c = kept([P, P], U32, "ac%d" % q)
+            s = kept([P, P], U8, "as%d" % q)
+            nc.vector.quantize_mx(out=c[:].bitcast(FP8X4), scales=s[:], in_=ag[:].rearrange("p c t -> p (c t)"))
+            ac.append(c)
+            asc.append(s)
+        for h in range(2):
+            bank = psum.tile([P, 512], F32, name="misc", tag="misc")
+            terms = [("o", g, oc[:, P * g : P * g + P], osc[:, P * g : P * g + P]) for g in range(PASSES)]
+            terms += [("a", g, ac[g][:], asc[g][:]) for g in range(PASSES)]
+            for i, (key, g, lc, ls) in enumerate(terms):
+                nc.tensor.matmul_mx(
+                    out=bank[:],
+                    lhsT=lc.bitcast(FP8X4),
+                    lhsT_scale=ls,
+                    rhs=codes[key, g, h][:].bitcast(FP8X4),
+                    rhs_scale=scales[key, g, h][:],
+                    start=(i == 0),
+                    stop=(i == 3),
+                )
+            o1 = work.tile([P, 512], F32, name="o1", tag="o1", bufs=2)
+            nc.vector.tensor_tensor(out=o1[:], in0=bank[:], in1=pb[:, 512 * h : 512 * h + 512], op=ALU.add)
+            o2 = work.tile([P, 512], F32, name="o2", tag="o2", bufs=2)
+            nc.scalar.activation(o2[:], o1[:], ACT.Relu)
+            for t in range(2):
+                nc.sync.dma_start(out=out_rows[t][:, 512 * h : 512 * h + 512], in_=o2[64 * t : 64 * t + 64, :])

@@ -9,14 +9,15 @@ K_PASS = 512
 PASSES = NF // K_PASS
 GRAPHS = 4
 N = 32
-GROUP = 256
-GROUPS = GRAPHS * N * N // GROUP
-RECV_PER_GROUP = GROUP // N
+SENDERS = 4
+GROUPS = N // SENDERS
+PIECE = 256
+SETS = NF // PIECE
+AHEAD = 10
 
 F32 = mybir.dt.float32
 BF16 = mybir.dt.bfloat16
 U32 = mybir.dt.uint32
-I32 = mybir.dt.int32
 U8 = mybir.dt.uint8
 FP8 = mybir.dt.float8_e4m3fn
 FP8X4 = mybir.dt.float8_e4m3fn_x4
@@ -26,325 +27,364 @@ ACT = mybir.ActivationFunctionType
 FLOPS = 2 * GRAPHS * N * N * NF * NF + 4 * 2 * GRAPHS * N * NF * NF
 
 
+def supply_order():
+    items = []
+    for c in range(SETS):
+        pieces = [(key, kp) for key in ("r", "i", "s") for kp in range(PASSES)]
+        on_vector = 2 if c < 2 else 3
+        pieces = [("w", key, kp, c, "v" if n < on_vector else "s") for n, (key, kp) in enumerate(pieces)]
+        senders = [("r", SENDERS * c + n) for n in range(SENDERS)]
+        items += [pieces[0]]
+        for n in range(SENDERS):
+            items += [pieces[n + 1], senders[n]]
+        items += [pieces[5]]
+    late = [(key, kp, c) for key in ("o", "a") for kp in range(PASSES) for c in range(SETS)]
+    for g in range(SETS, GROUPS):
+        for n in range(SENDERS):
+            items += [("r", SENDERS * g + n)]
+            items += [("w",) + late.pop(0) + ("s",) if n % 2 == 0 else None]
+    items += [("w",) + piece + ("v",) for piece in late]
+    return items
+
+
 def tile_compositionalkoopmanoperators_pa_kernel(
     tc, rel_bytes, rel_scale, obj, rp_w, rp_b, pp_w, pp_b, out
 ):
     nc = tc.nc
-    rel_rows = rel_bytes.rearrange("b i j k -> (b i j) k").rearrange("(g p t) k -> g p (t k)", p=P, t=2)
-    obj_rows = obj.rearrange("b n k -> (b n) k").rearrange("(x t) k -> t x k", t=2)
-    out_rows = out.rearrange("b n k -> (b n) k").rearrange("(x t) k -> t x k", t=2)
+    rel_rows = rel_bytes.rearrange("b i j k -> (b i) (j k)")
+    obj_rows = obj.rearrange("b n k -> (b n) k")
+    out_rows = out.rearrange("b n k -> (b n) k")
+    source = {"r": (rp_w, 0), "i": (rp_w, NF), "s": (rp_w, 2 * NF), "o": (pp_w, 0), "a": (pp_w, NF)}
 
     with ExitStack() as ctx:
         keep = ctx.enter_context(tc.tile_pool(name="keep", bufs=1))
-        loads = ctx.enter_context(tc.tile_pool(name="loads", bufs=6))
         work = ctx.enter_context(tc.tile_pool(name="work", bufs=3))
         psum = ctx.enter_context(tc.psum_pool(name="psum", bufs=2))
 
         def kept(shape, dtype, name):
             return keep.tile(shape, dtype, name=name, tag=name, align_bytes=64)
 
+        def moving(shape, dtype, name, bufs):
+            return work.tile(shape, dtype, name=name, tag=name, bufs=bufs, align_bytes=64)
+
         ident = kept([P, P], F32, "ident")
         make_identity(nc, ident[:])
 
         ctx.enter_context(tc.manual_schedule())
 
+        items = supply_order()
+        raw = {}
+
+        def load(item):
+            if item is None:
+                return
+            if item[0] == "r":
+                j = item[1]
+                if j % 2 == 0:
+                    rb = moving([P, 2 * NF], U8, "rb", 4)
+                    nc.sync.dma_start(out=rb[:], in_=rel_rows[:, NF * j : NF * (j + 2)])
+                    raw["r", j // 2] = rb
+                return
+            key, kp, c = item[1:4]
+            w, row = source[key]
+            r0 = row + K_PASS * kp
+            wr = moving([P, 4, PIECE], BF16, "wr", 10)
+            nc.sync.dma_start(
+                out=wr[:], in_=w[r0 : r0 + K_PASS, PIECE * c : PIECE * (c + 1)].rearrange("(p t) n -> p t n", t=4)
+            )
+            raw[key, kp, c] = wr
+
         sc8 = kept([P, NF // P], F32, "sc8")
         nc.scalar.dma_start(out=sc8[:], in_=rel_scale.rearrange("a b c (p e) -> p (a b c e)", p=P))
         ob = kept([P, NF], BF16, "ob")
-        for t in range(2):
-            nc.scalar.dma_start(out=ob[64 * t : 64 * t + 64, :], in_=obj_rows[t])
-        rpb = kept([P, 2, 4], BF16, "rpb")
-        with nc.allow_non_contiguous_dma(reason="bias"):
-            nc.scalar.dma_start(out=rpb[:], in_=rp_b.rearrange("(q p t) -> p q t", p=P, t=4))
-
-        raws = {}
-        rel_raw = {}
-
-        def load_rel(g):
-            rb = loads.tile([P, 2 * NF], U8, name="rb", tag="rb", align_bytes=64)
-            nc.sync.dma_start(out=rb[:], in_=rel_rows[g])
-            rel_raw[g] = rb
-
-        def load_w(key, w, row, g, q):
-            raw = loads.tile([P, 4, 512], BF16, name="raw", tag="raw", bufs=12, align_bytes=64)
-            r0 = row + K_PASS * g
-            nc.sync.dma_start(
-                out=raw[:],
-                in_=w[r0 : r0 + K_PASS, 512 * q : 512 * q + 512].rearrange("(p j) n -> p j n", j=4),
-            )
-            raws[key, g, q] = raw
-
-        rp_rows = {"r": 0, "i": NF, "s": 2 * NF}
-
-        load_rel(0)
-        for key in ("r", "s", "i"):
-            for g in range(PASSES):
-                load_w(key, rp_w, rp_rows[key], g, 0)
-        for g in range(1, 4):
-            load_rel(g)
-        for key in ("r", "s", "i"):
-            for g in range(PASSES):
-                load_w(key, rp_w, rp_rows[key], g, 1)
+        brow = kept([P, P // 2], F32, "brow")
+        nc.vector.memset(brow[:], 0.0)
+        for n in range(AHEAD):
+            load(items[n])
+            if n == 2:
+                nc.sync.dma_start(out=ob[:], in_=obj_rows)
+        nc.scalar.dma_start(
+            out=brow[:].bitcast(BF16)[0 : NF // P, :], in_=rp_b.rearrange("(q p) -> q p", p=P)
+        )
 
         scale = kept([P, NF], F32, "scale")
-        scale_v = scale[:].rearrange("m (p e) -> m e p", e=8)
+        scale_v = scale[:].rearrange("m (p e) -> m p e", e=8)
         for half in range(2):
-            bank = psum.tile([P, 4, P], F32, name="misc", tag="misc")
+            bank = psum.tile([P, 4, P], F32, name="acc", tag="acc", bufs=4)
             for e in range(4):
                 c = 4 * half + e
                 nc.tensor.transpose(bank[:, e, :], sc8[:, c : c + 1].to_broadcast([P, P]), ident[:])
-            nc.scalar.copy(out=scale_v[:, 4 * half : 4 * half + 4, :], in_=bank[:])
+            nc.scalar.copy(out=scale_v[:, :, 4 * half : 4 * half + 4], in_=bank[:].rearrange("m e p -> m p e"))
+
+        def turn_rows(rows, bank, passes):
+            words = rows.bitcast(F32)
+            for kp in range(passes):
+                for u in range(2):
+                    nc.tensor.transpose(bank[:, 2 * kp + u, :], words[:, 256 * kp + u : 256 * (kp + 1) : 2], ident[:])
 
         og = kept([P, PASSES * P * 4], BF16, "og")
-        bank = psum.tile([P, 4, P], F32, name="misc", tag="misc")
-        words = ob[:].bitcast(F32)
-        for g in range(PASSES):
-            for u in range(2):
-                nc.tensor.transpose(bank[:, 2 * g + u, :], words[:, 256 * g + u : 256 * g + 256 : 2], ident[:])
+        bank = psum.tile([P, 4, P], F32, name="acc", tag="acc", bufs=4)
+        turn_rows(ob[:], bank, PASSES)
         nc.scalar.copy(
-            out=og[:].bitcast(F32).rearrange("p (g r u) -> p g r u", g=2, u=2),
-            in_=bank[:].rearrange("p (g u) r -> p g r u", g=2),
+            out=og[:].bitcast(F32).rearrange("p (g r u) -> p g r u", g=PASSES, u=2),
+            in_=bank[:].rearrange("p (g u) r -> p g r u", g=PASSES),
         )
         oc = kept([P, PASSES * P], U32, "oc")
         osc = kept([P, PASSES * P], U8, "osc")
-        nc.gpsimd.memset(osc[:].bitcast(I32), 0)
+
+        identb = kept([P, P], BF16, "identb")
+        nc.vector.tensor_copy(out=identb[:], in_=ident[:])
+        bcol = kept([P, NF // P], F32, "bcol")
+
+        def bias_columns():
+            bank = psum.tile([P, P], BF16, name="acc", tag="acc", bufs=4)
+            nc.tensor.transpose(bank[:], brow[:].bitcast(BF16), identb[:])
+            nc.scalar.copy(out=bcol[:], in_=bank[:, 0 : NF // P])
 
         codes = {}
         scales = {}
-        rbias = {}
-        repc = {}
-        reps = {}
+        for key in source:
+            for kp in range(PASSES):
+                for h in range(2):
+                    name = "w%s%d%d" % (key, kp, h)
+                    codes[key, kp, h] = kept([P, 2 * PIECE], U32, name + "c")
+                    scales[key, kp, h] = kept([P, 2 * PIECE], U8, name + "s")
+        laid = {}
 
-        def weight_ig(key, g, q, h, engine):
-            wg = work.tile([P, 1024], BF16, name="wg", tag="wg", bufs=4, align_bytes=64)
-            engine(
-                out=wg[:].rearrange("p (t m j) -> p t m j", t=2, j=4),
-                in_=raws[key, g, q][:].rearrange("p j (m t) -> p t m j", t=4)[:, 2 * h : 2 * h + 2],
+        def interleave(key, kp, c, engine):
+            wg = moving([P, 4 * PIECE], BF16, "wg", 4)
+            copy = nc.vector.tensor_copy if engine == "v" else nc.scalar.copy
+            copy(
+                out=wg[:].rearrange("p (c i t) -> p c t i", i=4, t=4),
+                in_=raw[key, kp, c][:].rearrange("p t (c i) -> p c t i", i=4),
             )
-            return wg
+            laid[key, kp, c] = wg
 
-        def weight_q(key, g, q, h, wg):
-            name = "w%s%d%d%d" % (key, g, q, h)
-            c = kept([P, 256], U32, name + "c")
-            s = kept([P, 256], U8, name + "s")
-            nc.vector.quantize_mx(out=c[:].bitcast(FP8X4), scales=s[:], in_=wg[:])
-            codes[key, g, q, h] = c
-            scales[key, g, q, h] = s
+        def quantise_piece(key, kp, c):
+            cols = slice(PIECE * (c % 2), PIECE * (c % 2 + 1))
+            nc.vector.quantize_mx(
+                out=codes[key, kp, c // 2][:, cols].bitcast(FP8X4),
+                scales=scales[key, kp, c // 2][:, cols],
+                in_=laid[key, kp, c][:],
+            )
 
-        def weights(q, h):
-            first = q == 0 and h == 0
-            order = [(key, g) for key in ("r", "s", "i") for g in range(PASSES)]
-            pending = []
-            for key, g in order:
-                eng = nc.scalar.copy if first and key == "s" else nc.vector.tensor_copy
-                pending.append((key, g, weight_ig(key, g, q, h, eng)))
-                if len(pending) > 2:
-                    k0, g0, w0 = pending.pop(0)
-                    weight_q(k0, g0, q, h, w0)
-            for k0, g0, w0 in pending:
-                weight_q(k0, g0, q, h, w0)
+        def stationary(key, kp, q):
+            cols = slice(P * (q % 4), P * (q % 4 + 1))
+            return codes[key, kp, q // 4][:, cols].bitcast(FP8X4), scales[key, kp, q // 4][:, cols]
 
-        def receivers(q, h):
-            bank = psum.tile([P, 2, P], F32, name="misc", tag="misc")
-            for n in range(2):
-                for g in range(PASSES):
-                    nc.tensor.matmul_mx(
-                        out=bank[:, n, :],
-                        lhsT=codes["i", g, q, h][:, 128 * n : 128 * n + 128].bitcast(FP8X4),
-                        lhsT_scale=scales["i", g, q, h][:, 128 * n : 128 * n + 128],
-                        rhs=oc[:, P * g : P * g + P].bitcast(FP8X4),
-                        rhs_scale=osc[:, P * g : P * g + P],
-                        start=(g == 0),
-                        stop=(g == PASSES - 1),
-                    )
-            rb = kept([P, 2, P], F32, "rbias%d%d" % (q, h))
-            for n in range(2):
-                t = 2 * h + n
-                nc.scalar.activation(rb[:, n, :], bank[:, n, :], ACT.Identity, bias=rpb[:, q, t : t + 1])
-            rbias[q, h] = rb
+        table_bank = {}
+        recv = {}
+        send = {}
 
-        def replicate(b):
-            c = work.tile([P, PASSES * GROUP], U32, name="repc", tag="repc", bufs=4, align_bytes=64)
-            s = work.tile([P, PASSES * GROUP], U8, name="reps", tag="reps", bufs=4, align_bytes=64)
-            for dst, src, w in ((c, oc, 16), (s, osc, 4)):
-                for g in range(PASSES):
-                    nc.vector.tensor_copy(
-                        out=dst[:].bitcast(I32).rearrange("p (g t i w) -> p g t i w", g=2, t=2, i=8)[:, g],
-                        in_=src[:].bitcast(I32).rearrange("p (g t b w) -> p g t b w", g=2, t=2, b=4)[:, g, :, b, :]
-                        .unsqueeze(2)
-                        .to_broadcast([P, 2, 8, w]),
-                    )
-            repc[b] = c
-            reps[b] = s
+        def table_products(c):
+            bank = psum.tile([P, 4, P], F32, name="acc", tag="acc", bufs=4)
+            for n, key in enumerate(("i", "s")):
+                for m in range(2):
+                    for kp in range(PASSES):
+                        wc, ws = stationary(key, kp, 2 * c + m)
+                        nc.tensor.matmul_mx(
+                            out=bank[:, 2 * n + m, :],
+                            lhsT=wc,
+                            lhsT_scale=ws,
+                            rhs=oc[:, P * kp : P * (kp + 1)].bitcast(FP8X4),
+                            rhs_scale=osc[:, P * kp : P * (kp + 1)],
+                            start=(kp == 0),
+                            stop=(kp == PASSES - 1),
+                        )
+            table_bank[c] = bank
+
+        def table_copies(c):
+            recv[c] = kept([P, 2, P], F32, "recv%d" % c)
+            send[c] = kept([P, 2, P], F32, "send%d" % c)
+            nc.scalar.copy(out=recv[c][:], in_=table_bank[c][:, 0:2, :])
+            for m in range(2):
+                q = 2 * c + m
+                nc.scalar.activation(send[c][:, m, :], table_bank[c][:, 2 + m, :], ACT.Identity, bias=bcol[:, q : q + 1])
 
         wide = {}
         turned = {}
         grouped = {}
-        rel_codes = {}
-        rel_scales = {}
+        rel_codes = [kept([P, PASSES * SENDERS * P], U32, "rc%d" % g) for g in range(GROUPS)]
+        rel_scales = [kept([P, PASSES * SENDERS * P], U8, "rs%d" % g) for g in range(GROUPS)]
 
-        def widen(g):
-            for t in range(2):
-                wb = work.tile([P, NF], BF16, name="wb", tag="wb", bufs=4, align_bytes=64)
-                nc.vector.tensor_tensor(
-                    out=wb[:], in0=rel_raw[g][:, NF * t : NF * t + NF].bitcast(FP8), in1=scale[:], op=ALU.mult
-                )
-                wide[g, t] = wb
+        def widen(j):
+            wide[j] = moving([P, NF], BF16, "wide", 3)
+            nc.vector.tensor_tensor(
+                out=wide[j][:],
+                in0=raw["r", j // 2][:, NF * (j % 2) : NF * (j % 2 + 1)].bitcast(FP8),
+                in1=scale[:],
+                op=ALU.mult,
+            )
 
-        def turn(g):
-            for t in range(2):
-                bank = psum.tile([P, 4, P], F32, name="tr", tag="tr")
-                words = wide[g, t][:].bitcast(F32)
-                for kp in range(PASSES):
-                    for u in range(2):
-                        nc.tensor.transpose(
-                            bank[:, 2 * kp + u, :], words[:, 256 * kp + u : 256 * kp + 256 : 2], ident[:]
-                        )
-                turned[g, t] = bank
+        def turn(j):
+            turned[j] = psum.tile([P, 4, P], F32, name="tr", tag="tr", bufs=2)
+            turn_rows(wide[j][:], turned[j], PASSES)
 
-        def empty(g):
-            grp = work.tile([P, PASSES * GROUP * 4], BF16, name="grp", tag="grp", align_bytes=64)
-            view = grp[:].bitcast(F32).rearrange("p (g t r u) -> p g t r u", g=2, t=2, u=2)
-            for t in range(2):
-                nc.scalar.copy(out=view[:, :, t], in_=turned[g, t][:].rearrange("p (g u) r -> p g r u", g=2))
-            grouped[g] = grp
+        def empty(j):
+            if j % 2 == 0:
+                grouped[j // 2] = moving([P, PASSES * 2 * P * 4], BF16, "grp", 3)
+            view = grouped[j // 2][:].bitcast(F32).rearrange("p (g s r u) -> p g s r u", g=PASSES, s=2, u=2)
+            nc.scalar.copy(out=view[:, :, j % 2], in_=turned[j][:].rearrange("p (g u) r -> p g r u", g=PASSES))
 
-        def quantise(g):
-            c = kept([P, PASSES * GROUP], U32, "rc%d" % g)
-            s = kept([P, PASSES * GROUP], U8, "rs%d" % g)
-            nc.vector.quantize_mx(out=c[:].bitcast(FP8X4), scales=s[:], in_=grouped[g][:])
-            rel_codes[g] = c
-            rel_scales[g] = s
-
-        agg = [kept([P, 4, P], F32, "agg%d" % q) for q in range(2)]
-
-        def unit(g, q, h):
-            b = g // 4
-            bank = psum.tile([P, 2, GROUP], F32, name="acc", tag="acc", bufs=4)
-            for n in range(2):
-                cols = slice(128 * n, 128 * n + 128)
-                for i, (key, mc, ms) in enumerate((("s", repc[b], reps[b]), ("r", rel_codes[g], rel_scales[g]))):
-                    for kp in range(PASSES):
-                        nc.tensor.matmul_mx(
-                            out=bank[:, n, :],
-                            lhsT=codes[key, kp, q, h][:, cols].bitcast(FP8X4),
-                            lhsT_scale=scales[key, kp, q, h][:, cols],
-                            rhs=mc[:, GROUP * kp : GROUP * kp + GROUP].bitcast(FP8X4),
-                            rhs_scale=ms[:, GROUP * kp : GROUP * kp + GROUP],
-                            start=(i == 0 and kp == 0),
-                            stop=(i == 1 and kp == PASSES - 1),
-                        )
-            junk = work.tile([P, 2, RECV_PER_GROUP, N], BF16, name="junk", tag="junk", bufs=4)
-            for n in range(2):
-                view = bank[:, n, :].rearrange("p (t i w) -> p i t w", t=2, i=RECV_PER_GROUP)
-                for il in range(RECV_PER_GROUP):
-                    i = RECV_PER_GROUP * (g % 4) + il
-                    col = 64 * (i % 2) + 16 * b + i // 2
-                    nc.scalar.activation(
-                        junk[:, n, il, :].rearrange("p (t w) -> p t w", t=2),
-                        view[:, il],
-                        ACT.Relu,
-                        bias=rbias[q, h][:, n, col : col + 1],
-                        accum_out=agg[q][:, 2 * h + n, col : col + 1],
-                    )
-
-        sets = [(0, 0), (0, 1), (1, 0), (1, 1)]
-        tasks = [("r", 0), ("w", 0), ("r", 1), ("w", 1), ("r", 2), ("r", 3), ("w", 2), ("r", 4), ("r", 5), ("w", 3)]
-        tasks += [("r", g) for g in range(6, GROUPS)]
-        tasks += [("o", n) for n in range(8)]
-        cost = {"r": 2.2, "w": 4.6, "o": 1.6}
-        unit_cost = 1.05
-
-        late = [("g", g) for g in range(4, GROUPS)]
-        late += [("o", key, row, g, q) for key, row in (("o", 0), ("a", NF)) for g in range(PASSES) for q in range(2)]
-        late_n = 0
-
-        ready_groups = []
-        ready_sets = []
-        queue = []
-        budget = 0.0
-        fresh_group = None
-        last_rel = None
-
-        for kind, n in tasks + [("end", 0), ("end", 1)]:
-            new_units = []
-            for item in late[late_n : late_n + 2]:
-                if item[0] == "g":
-                    load_rel(item[1])
-                else:
-                    load_w(item[1], pp_w, item[2], item[3], item[4])
-            late_n += 2
-            if kind == "r":
-                widen(n)
-            elif kind == "w":
-                q, h = sets[n]
-                if n == 0:
-                    nc.vector.quantize_mx(out=oc[:].bitcast(FP8X4), scales=osc[:], in_=og[:])
-                weights(q, h)
-            elif kind == "o":
-                key, g, q = ("o", "a")[n // 4], (n // 2) % 2, n % 2
-                wg = work.tile([P, 512, 4], BF16, name="og4", tag="og4", bufs=2, align_bytes=64)
-                nc.vector.tensor_copy(out=wg[:], in_=raws[key, g, q][:].rearrange("p j n -> p n j"))
-                c = kept([P, 512], U32, "w%s%d%dc" % (key, g, q))
-                s = kept([P, 512], U8, "w%s%d%ds" % (key, g, q))
+        def quantise_pair(m):
+            g = m // 2
+            for kp in range(PASSES):
+                first = SENDERS * P * kp + 2 * P * (m % 2)
                 nc.vector.quantize_mx(
-                    out=c[:].bitcast(FP8X4), scales=s[:], in_=wg[:].rearrange("p n j -> p (n j)")
+                    out=rel_codes[g][:, first : first + 2 * P].bitcast(FP8X4),
+                    scales=rel_scales[g][:, first : first + 2 * P],
+                    in_=grouped[m][:, 8 * P * kp : 8 * P * (kp + 1)],
                 )
-                codes[key, g, q] = c
-                scales[key, g, q] = s
-            if last_rel is not None:
-                empty(last_rel)
-                if last_rel % 4 == 0:
-                    replicate(last_rel // 4)
-                quantise(last_rel)
-                new_units += [(last_rel, s) for s in ready_sets]
-                ready_groups.append(last_rel)
-                last_rel = None
-            if kind == "w":
-                receivers(q, h)
-                new_units += [(g, (q, h)) for g in ready_groups]
-                ready_sets.append((q, h))
-            budget = min(budget + cost.get(kind, 1000.0), 1000.0)
-            while queue and budget >= unit_cost:
-                g, s = queue.pop(0)
-                unit(g, s[0], s[1])
-                budget -= unit_cost
-            if not queue:
-                budget = 0.0
-            queue += new_units
-            if kind == "r":
-                turn(n)
-                last_rel = n
+
+        agg = [psum.tile([P, 4, P], F32, name="agg%d" % h, tag="agg%d" % h, bufs=1) for h in range(2)]
+        summed = [0, 0]
+        acc = {}
+        eff = {}
+
+        def product(g, q):
+            acc[g, q] = psum.tile([P, SENDERS, P], F32, name="acc", tag="acc", bufs=4)
+            for kp in range(PASSES):
+                wc, ws = stationary("r", kp, q)
+                cols = slice(SENDERS * P * kp, SENDERS * P * (kp + 1))
+                nc.tensor.matmul_mx(
+                    out=acc[g, q][:].rearrange("p s r -> p (s r)"),
+                    lhsT=wc,
+                    lhsT_scale=ws,
+                    rhs=rel_codes[g][:, cols].bitcast(FP8X4),
+                    rhs_scale=rel_scales[g][:, cols],
+                    start=(kp == 0),
+                    stop=(kp == PASSES - 1),
+                )
+
+        def add_receivers(g, q):
+            eff[g, q] = moving([P, SENDERS, P], F32, "eff", 6)
+            nc.vector.tensor_tensor(
+                out=eff[g, q][:],
+                in0=acc[g, q][:],
+                in1=recv[q // 2][:, q % 2, :].unsqueeze(1).to_broadcast([P, SENDERS, P]),
+                op=ALU.add,
+            )
+
+        def relu_senders(g, q):
+            for s in range(SENDERS):
+                for b in range(GRAPHS):
+                    col = N * b + SENDERS * g + s
+                    part = eff[g, q][:, s, N * b : N * (b + 1)]
+                    nc.scalar.activation(part, part, ACT.Relu, bias=send[q // 2][:, q % 2, col : col + 1])
+
+        def sum_senders(g, q):
+            h = q // 4
+            for s in range(SENDERS):
+                nc.tensor.matmul(
+                    out=agg[h][:, q % 4, :],
+                    lhsT=eff[g, q][:, s, :],
+                    rhs=ident[:],
+                    is_transpose=True,
+                    start=(summed[h] == 0),
+                    stop=(summed[h] == 4 * N - 1),
+                )
+                summed[h] = summed[h] + 1
 
         pb = kept([P, NF], BF16, "pb")
-        nc.sync.dma_start(out=pb[:], in_=pp_b.partition_broadcast(P))
-        ac = []
-        asc = []
-        for q in range(2):
-            ag = work.tile([P, P, 4], BF16, name="ag", tag="ag", bufs=2, align_bytes=64)
-            nc.vector.tensor_copy(out=ag[:], in_=agg[q][:].rearrange("p t c -> p c t"))
-            c = kept([P, P], U32, "ac%d" % q)
-            s = kept([P, P], U8, "as%d" % q)
-            nc.vector.quantize_mx(out=c[:].bitcast(FP8X4), scales=s[:], in_=ag[:].rearrange("p c t -> p (c t)"))
-            ac.append(c)
-            asc.append(s)
-        for h in range(2):
-            bank = psum.tile([P, 512], F32, name="misc", tag="misc")
-            terms = [("o", g, oc[:, P * g : P * g + P], osc[:, P * g : P * g + P]) for g in range(PASSES)]
-            terms += [("a", g, ac[g][:], asc[g][:]) for g in range(PASSES)]
-            for i, (key, g, lc, ls) in enumerate(terms):
+        agg_rows = {}
+        agg_bank = {}
+        agg_laid = {}
+        agg_codes = {}
+        agg_scales = {}
+
+        def agg_round(h):
+            agg_rows[h] = kept([P, K_PASS], BF16, "ar%d" % h)
+            nc.vector.tensor_copy(out=agg_rows[h][:], in_=agg[h][:].rearrange("p q f -> p (q f)"))
+
+        def agg_turn(h):
+            agg_bank[h] = psum.tile([P, 2, P], F32, name="tr", tag="tr", bufs=2)
+            turn_rows(agg_rows[h][:], agg_bank[h], 1)
+
+        def agg_empty(h):
+            agg_laid[h] = kept([P, 4 * P], BF16, "al%d" % h)
+            nc.scalar.copy(
+                out=agg_laid[h][:].bitcast(F32).rearrange("p (r u) -> p r u", u=2),
+                in_=agg_bank[h][:].rearrange("p u r -> p r u"),
+            )
+
+        def agg_quantise(h):
+            agg_codes[h] = kept([P, P], U32, "ac%d" % h)
+            agg_scales[h] = kept([P, P], U8, "as%d" % h)
+            nc.vector.quantize_mx(out=agg_codes[h][:].bitcast(FP8X4), scales=agg_scales[h][:], in_=agg_laid[h][:])
+
+        plan = {}
+
+        def at(step, rank, fn, *args):
+            plan.setdefault(step, []).append((rank, len(plan.get(step, [])), fn, args))
+
+        group_ready = {}
+        set_ready = {}
+        for n, item in enumerate(items):
+            if n + AHEAD < len(items):
+                at(n, 0, load, items[n + AHEAD])
+            if item is None:
+                continue
+            if item[0] == "r":
+                j = item[1]
+                odd = n + 1 if n % 2 == 0 else n + 2
+                at(n, 5, widen, j)
+                at(odd, 7, turn, j)
+                at(odd + 1, 1, empty, j)
+                if j % 2 == 1:
+                    at(odd + 2, 3, quantise_pair, j // 2)
+                if j % SENDERS == SENDERS - 1:
+                    group_ready[j // SENDERS] = odd + 3
+            else:
+                key, kp, c, engine = item[1:5]
+                at(n, 5, interleave, key, kp, c, engine)
+                at(n + 2, 3, quantise_piece, key, kp, c)
+                if key == "s" and kp == PASSES - 1:
+                    even = n + 3 if n % 2 == 1 else n + 4
+                    at(even, 6, table_products, c)
+                    at(even + 1, 1, table_copies, c)
+                    set_ready[c] = even
+        at(1, 6, bias_columns)
+        at(3, 3, lambda: nc.vector.quantize_mx(out=oc[:].bitcast(FP8X4), scales=osc[:], in_=og[:]))
+        at(len(items) - AHEAD, 0, lambda: nc.sync.dma_start(out=pb[:], in_=pp_b.partition_broadcast(P)))
+
+        pairs = sorted(
+            [(max(group_ready[g], set_ready[c]), g, c) for g in range(GROUPS) for c in range(SETS)]
+        )
+        step = 0
+        for ready, g, c in pairs:
+            step = max(step + 2, ready + ready % 2)
+            for q in (2 * c, 2 * c + 1):
+                at(step, 7, product, g, q)
+                at(step + 1, 2, add_receivers, g, q)
+                at(step + 2, 4, relu_senders, g, q)
+                at(step + 3, 6, sum_senders, g, q)
+            if g == GROUPS - 1 and c % 2 == 1:
+                at(step + 4, 3, agg_round, c // 2)
+                at(step + 5, 7, agg_turn, c // 2)
+                at(step + 6, 1, agg_empty, c // 2)
+                at(step + 7, 3, agg_quantise, c // 2)
+
+        for n in sorted(plan):
+            for rank, order, fn, args in sorted(plan[n], key=lambda e: (e[0], e[1])):
+                fn(*args)
+
+        final = [psum.tile([P, K_PASS], F32, name="acc", tag="acc", bufs=4) for h in range(2)]
+        terms = [("o", kp, oc[:, P * kp : P * (kp + 1)], osc[:, P * kp : P * (kp + 1)]) for kp in range(PASSES)]
+        terms += [("a", kp, agg_codes[kp][:], agg_scales[kp][:]) for kp in range(PASSES)]
+        for i, (key, kp, lc, ls) in enumerate(terms):
+            for h in range(2):
                 nc.tensor.matmul_mx(
-                    out=bank[:],
+                    out=final[h][:],
                     lhsT=lc.bitcast(FP8X4),
                     lhsT_scale=ls,
-                    rhs=codes[key, g, h][:].bitcast(FP8X4),
-                    rhs_scale=scales[key, g, h][:],
+                    rhs=codes[key, kp, h][:].bitcast(FP8X4),
+                    rhs_scale=scales[key, kp, h][:],
                     start=(i == 0),
-                    stop=(i == 3),
+                    stop=(i == len(terms) - 1),
                 )
-            o1 = work.tile([P, 512], F32, name="o1", tag="o1", bufs=2)
-            nc.vector.tensor_tensor(out=o1[:], in0=bank[:], in1=pb[:, 512 * h : 512 * h + 512], op=ALU.add)
-            o2 = work.tile([P, 512], F32, name="o2", tag="o2", bufs=2)
-            nc.scalar.activation(o2[:], o1[:], ACT.Relu)
-            for t in range(2):
-                nc.sync.dma_start(out=out_rows[t][:, 512 * h : 512 * h + 512], in_=o2[64 * t : 64 * t + 64, :])
+        for h in range(2):
+            cols = slice(K_PASS * h, K_PASS * (h + 1))
+            o1 = moving([P, K_PASS], F32, "o1", 2)
+            nc.vector.tensor_tensor(out=o1[:], in0=final[h][:], in1=pb[:, cols], op=ALU.add)
+            nc.scalar.activation(o1[:], o1[:], ACT.Relu)
+            nc.sync.dma_start(out=out_rows[:, cols], in_=o1[:])

@@ -14,6 +14,14 @@ GROUPS = N // SENDERS
 PIECE = 256
 SETS = NF // PIECE
 AHEAD = 10
+TURN = 2
+QUANT = 3
+RELU = 3
+SUM = 7
+FOLD = 44
+SPREAD = 1
+RAMP = 4
+SHARE = 3
 
 F32 = mybir.dt.float32
 BF16 = mybir.dt.bfloat16
@@ -28,22 +36,20 @@ FLOPS = 2 * GRAPHS * N * N * NF * NF + 4 * 2 * GRAPHS * N * NF * NF
 
 
 def supply_order():
-    items = []
-    for c in range(SETS):
-        pieces = [(key, kp) for key in ("r", "i", "s") for kp in range(PASSES)]
-        on_vector = 2 if c < 2 else 3
-        pieces = [("w", key, kp, c, "v" if n < on_vector else "s") for n, (key, kp) in enumerate(pieces)]
-        senders = [("r", SENDERS * c + n) for n in range(SENDERS)]
-        items += [pieces[0]]
-        for n in range(SENDERS):
-            items += [pieces[n + 1], senders[n]]
-        items += [pieces[5]]
-    late = [(key, kp, c) for key in ("o", "a") for kp in range(PASSES) for c in range(SETS)]
+    pieces = [[("w", key, kp, c) for key in ("r", "i", "s") for kp in range(PASSES)] for c in range(SETS)]
+    senders = [[("r", SENDERS * g + n) for n in range(SENDERS)] for g in range(GROUPS)]
+    items = pieces[0][:2]
+    for n in range(SENDERS):
+        items += [senders[0][n], pieces[0][2 + n]]
+    for c in range(1, SETS):
+        items += senders[c] + pieces[c]
+    late = [("w", key, kp, c) for key in ("o", "a") for kp in range(PASSES) for c in range(SETS)]
     for g in range(SETS, GROUPS):
         for n in range(SENDERS):
-            items += [("r", SENDERS * g + n)]
-            items += [("w",) + late.pop(0) + ("s",) if n % 2 == 0 else None]
-    items += [("w",) + piece + ("v",) for piece in late]
+            items += [senders[g][n], late.pop(0) if n % 2 == 0 else None]
+        items += [late.pop(0), None]
+    for piece in late:
+        items += [piece, None]
     return items
 
 
@@ -81,7 +87,7 @@ def tile_compositionalkoopmanoperators_pa_kernel(
             if item[0] == "r":
                 j = item[1]
                 if j % 2 == 0:
-                    rb = moving([P, 2 * NF], U8, "rb", 4)
+                    rb = moving([P, 2 * NF], U8, "rb", 5)
                     nc.sync.dma_start(out=rb[:], in_=rel_rows[:, NF * j : NF * (j + 2)])
                     raw["r", j // 2] = rb
                 return
@@ -95,7 +101,7 @@ def tile_compositionalkoopmanoperators_pa_kernel(
             raw[key, kp, c] = wr
 
         sc8 = kept([P, NF // P], F32, "sc8")
-        nc.scalar.dma_start(out=sc8[:], in_=rel_scale.rearrange("a b c (p e) -> p (a b c e)", p=P))
+        nc.sync.dma_start(out=sc8[:], in_=rel_scale.rearrange("a b c (p e) -> p (a b c e)", p=P))
         ob = kept([P, NF], BF16, "ob")
         brow = kept([P, P // 2], F32, "brow")
         nc.vector.memset(brow[:], 0.0)
@@ -152,7 +158,7 @@ def tile_compositionalkoopmanoperators_pa_kernel(
         laid = {}
 
         def interleave(key, kp, c, engine):
-            wg = moving([P, 4 * PIECE], BF16, "wg", 4)
+            wg = moving([P, 4 * PIECE], BF16, "wg", 5)
             copy = nc.vector.tensor_copy if engine == "v" else nc.scalar.copy
             copy(
                 out=wg[:].rearrange("p (c i t) -> p c t i", i=4, t=4),
@@ -208,7 +214,7 @@ def tile_compositionalkoopmanoperators_pa_kernel(
         rel_scales = [kept([P, PASSES * SENDERS * P], U8, "rs%d" % g) for g in range(GROUPS)]
 
         def widen(j):
-            wide[j] = moving([P, NF], BF16, "wide", 3)
+            wide[j] = moving([P, NF], BF16, "wide", 5)
             nc.vector.tensor_tensor(
                 out=wide[j][:],
                 in0=raw["r", j // 2][:, NF * (j % 2) : NF * (j % 2 + 1)].bitcast(FP8),
@@ -222,7 +228,7 @@ def tile_compositionalkoopmanoperators_pa_kernel(
 
         def empty(j):
             if j % 2 == 0:
-                grouped[j // 2] = moving([P, PASSES * 2 * P * 4], BF16, "grp", 3)
+                grouped[j // 2] = moving([P, PASSES * 2 * P * 4], BF16, "grp", 4)
             view = grouped[j // 2][:].bitcast(F32).rearrange("p (g s r u) -> p g s r u", g=PASSES, s=2, u=2)
             nc.scalar.copy(out=view[:, :, j % 2], in_=turned[j][:].rearrange("p (g u) r -> p g r u", g=PASSES))
 
@@ -241,7 +247,7 @@ def tile_compositionalkoopmanoperators_pa_kernel(
         acc = {}
         eff = {}
 
-        def product(g, q):
+        def product(g, q, folded):
             acc[g, q] = psum.tile([P, SENDERS, P], F32, name="acc", tag="acc", bufs=4)
             for kp in range(PASSES):
                 wc, ws = stationary("r", kp, q)
@@ -253,11 +259,23 @@ def tile_compositionalkoopmanoperators_pa_kernel(
                     rhs=rel_codes[g][:, cols].bitcast(FP8X4),
                     rhs_scale=rel_scales[g][:, cols],
                     start=(kp == 0),
-                    stop=(kp == PASSES - 1),
+                    stop=(kp == PASSES - 1 and not folded),
                 )
+            for kp in range(PASSES if folded else 0):
+                wc, ws = stationary("i", kp, q)
+                for s in range(SENDERS):
+                    nc.tensor.matmul_mx(
+                        out=acc[g, q][:, s, :],
+                        lhsT=wc,
+                        lhsT_scale=ws,
+                        rhs=oc[:, P * kp : P * (kp + 1)].bitcast(FP8X4),
+                        rhs_scale=osc[:, P * kp : P * (kp + 1)],
+                        start=False,
+                        stop=(kp == PASSES - 1 and s == SENDERS - 1),
+                    )
 
         def add_receivers(g, q):
-            eff[g, q] = moving([P, SENDERS, P], F32, "eff", 6)
+            eff[g, q] = moving([P, SENDERS, P], F32, "eff", 8)
             nc.vector.tensor_tensor(
                 out=eff[g, q][:],
                 in0=acc[g, q][:],
@@ -265,12 +283,17 @@ def tile_compositionalkoopmanoperators_pa_kernel(
                 op=ALU.add,
             )
 
-        def relu_senders(g, q):
+        def relu_senders(g, q, folded):
+            if folded:
+                eff[g, q] = moving([P, SENDERS, P], F32, "eff", 8)
+            src = acc[g, q] if folded else eff[g, q]
             for s in range(SENDERS):
                 for b in range(GRAPHS):
                     col = N * b + SENDERS * g + s
-                    part = eff[g, q][:, s, N * b : N * (b + 1)]
-                    nc.scalar.activation(part, part, ACT.Relu, bias=send[q // 2][:, q % 2, col : col + 1])
+                    cols = slice(N * b, N * (b + 1))
+                    nc.scalar.activation(
+                        eff[g, q][:, s, cols], src[:, s, cols], ACT.Relu, bias=send[q // 2][:, q % 2, col : col + 1]
+                    )
 
         def sum_senders(g, q):
             h = q // 4
@@ -297,7 +320,7 @@ def tile_compositionalkoopmanoperators_pa_kernel(
             nc.vector.tensor_copy(out=agg_rows[h][:], in_=agg[h][:].rearrange("p q f -> p (q f)"))
 
         def agg_turn(h):
-            agg_bank[h] = psum.tile([P, 2, P], F32, name="tr", tag="tr", bufs=2)
+            agg_bank[h] = psum.tile([P, 2, P], F32, name="acc", tag="acc", bufs=4)
             turn_rows(agg_rows[h][:], agg_bank[h], 1)
 
         def agg_empty(h):
@@ -312,10 +335,36 @@ def tile_compositionalkoopmanoperators_pa_kernel(
             agg_scales[h] = kept([P, P], U8, "as%d" % h)
             nc.vector.quantize_mx(out=agg_codes[h][:].bitcast(FP8X4), scales=agg_scales[h][:], in_=agg_laid[h][:])
 
+        final = {}
+
+        def final_pass(key, kp):
+            if key == "o":
+                lc, ls = oc[:, P * kp : P * (kp + 1)], osc[:, P * kp : P * (kp + 1)]
+            else:
+                lc, ls = agg_codes[kp][:], agg_scales[kp][:]
+            for h in range(2):
+                if (key, kp) == ("o", 0):
+                    final[h] = psum.tile([P, K_PASS], F32, name="tr", tag="tr", bufs=2)
+                nc.tensor.matmul_mx(
+                    out=final[h][:],
+                    lhsT=lc.bitcast(FP8X4),
+                    lhsT_scale=ls,
+                    rhs=codes[key, kp, h][:].bitcast(FP8X4),
+                    rhs_scale=scales[key, kp, h][:],
+                    start=((key, kp) == ("o", 0)),
+                    stop=((key, kp) == ("a", PASSES - 1)),
+                )
+
         plan = {}
 
         def at(step, rank, fn, *args):
             plan.setdefault(step, []).append((rank, len(plan.get(step, [])), fn, args))
+
+        def odd(n):
+            return n + 1 - n % 2
+
+        def even(n):
+            return n + n % 2
 
         group_ready = {}
         set_ready = {}
@@ -326,62 +375,61 @@ def tile_compositionalkoopmanoperators_pa_kernel(
                 continue
             if item[0] == "r":
                 j = item[1]
-                odd = n + 1 if n % 2 == 0 else n + 2
+                turn_step = odd(n + TURN)
                 at(n, 5, widen, j)
-                at(odd, 7, turn, j)
-                at(odd + 1, 1, empty, j)
+                at(turn_step, 8, turn, j)
+                at(turn_step + 1, 1, empty, j)
                 if j % 2 == 1:
-                    at(odd + 2, 3, quantise_pair, j // 2)
+                    at(turn_step + 1 + QUANT, 3, quantise_pair, j // 2)
                 if j % SENDERS == SENDERS - 1:
-                    group_ready[j // SENDERS] = odd + 3
+                    group_ready[j // SENDERS] = turn_step + 2 + QUANT
+                last_turn = turn_step
             else:
-                key, kp, c, engine = item[1:5]
-                at(n, 5, interleave, key, kp, c, engine)
-                at(n + 2, 3, quantise_piece, key, kp, c)
+                key, kp, c = item[1:4]
+                at(n + QUANT, 3, quantise_piece, key, kp, c)
                 if key == "s" and kp == PASSES - 1:
-                    even = n + 3 if n % 2 == 1 else n + 4
-                    at(even, 6, table_products, c)
-                    at(even + 1, 1, table_copies, c)
-                    set_ready[c] = even
+                    at(even(n + QUANT + 1), 6, table_products, c)
+                    at(even(n + QUANT + 1) + 1, 1, table_copies, c)
+                    set_ready[c] = even(n + QUANT + 1)
         at(1, 6, bias_columns)
         at(3, 3, lambda: nc.vector.quantize_mx(out=oc[:].bitcast(FP8X4), scales=osc[:], in_=og[:]))
         at(len(items) - AHEAD, 0, lambda: nc.sync.dma_start(out=pb[:], in_=pp_b.partition_broadcast(P)))
+        for kp in range(PASSES):
+            at(even(last_turn + 2) + 2 * kp, 6, final_pass, "o", kp)
 
-        pairs = sorted(
-            [(max(group_ready[g], set_ready[c]), g, c) for g in range(GROUPS) for c in range(SETS)]
-        )
+        pairs = sorted([(max(group_ready[g], set_ready[c]), g, c) for g in range(GROUPS) for c in range(SETS)])
         step = 0
+        relu_steps = set()
         for ready, g, c in pairs:
-            step = max(step + 2, ready + ready % 2)
-            for q in (2 * c, 2 * c + 1):
-                at(step, 7, product, g, q)
-                at(step + 1, 2, add_receivers, g, q)
-                at(step + 2, 4, relu_senders, g, q)
-                at(step + 3, 6, sum_senders, g, q)
+            step = max(step + (RAMP if step < FOLD else 2), even(ready))
+            folded = step < FOLD
+            for m in range(2):
+                q = 2 * c + m
+                at(step, 6, product, g, q, folded)
+                if not folded:
+                    at(step + 1 + m * SPREAD, 2, add_receivers, g, q)
+                at(step + RELU + m, 4, relu_senders, g, q, folded)
+                relu_steps.add(step + RELU + m)
+                at(step + SUM, 7, sum_senders, g, q)
             if g == GROUPS - 1 and c % 2 == 1:
-                at(step + 4, 3, agg_round, c // 2)
-                at(step + 5, 7, agg_turn, c // 2)
-                at(step + 6, 1, agg_empty, c // 2)
-                at(step + 7, 3, agg_quantise, c // 2)
+                at(step + SUM + 1, 3, agg_round, c // 2)
+                at(step + SUM + 2, 8, agg_turn, c // 2)
+                at(step + SUM + 3, 1, agg_empty, c // 2)
+                at(step + SUM + 4, 3, agg_quantise, c // 2)
+                at(step + SUM + 5, 6, final_pass, "a", c // 2)
+
+        shared = 0
+        for n, item in enumerate(items):
+            if item is None or item[0] == "r":
+                continue
+            shared = shared + 1
+            on_vector = n < 2 or (n >= 10 and shared % SHARE != 0) or n >= len(items) - 8
+            at(n, 5, interleave, item[1], item[2], item[3], "v" if on_vector else "s")
 
         for n in sorted(plan):
             for rank, order, fn, args in sorted(plan[n], key=lambda e: (e[0], e[1])):
                 fn(*args)
 
-        final = [psum.tile([P, K_PASS], F32, name="acc", tag="acc", bufs=4) for h in range(2)]
-        terms = [("o", kp, oc[:, P * kp : P * (kp + 1)], osc[:, P * kp : P * (kp + 1)]) for kp in range(PASSES)]
-        terms += [("a", kp, agg_codes[kp][:], agg_scales[kp][:]) for kp in range(PASSES)]
-        for i, (key, kp, lc, ls) in enumerate(terms):
-            for h in range(2):
-                nc.tensor.matmul_mx(
-                    out=final[h][:],
-                    lhsT=lc.bitcast(FP8X4),
-                    lhsT_scale=ls,
-                    rhs=codes[key, kp, h][:].bitcast(FP8X4),
-                    rhs_scale=scales[key, kp, h][:],
-                    start=(i == 0),
-                    stop=(i == len(terms) - 1),
-                )
         for h in range(2):
             cols = slice(K_PASS * h, K_PASS * (h + 1))
             o1 = moving([P, K_PASS], F32, "o1", 2)

@@ -13,15 +13,31 @@ SENDERS = 4
 GROUPS = N // SENDERS
 PIECE = 256
 SETS = NF // PIECE
-AHEAD = 10
-TURN = 2
+AHEAD = 6
+TURN0 = 1
+QUANT0 = 2
+RELU0 = 2
+SUM0 = 4
+TURN = 3
 QUANT = 3
-RELU = 3
-SUM = 7
-FOLD = 44
+RELU = 1
+SUM = 2
+BEAT = 2
+ON_GPSIMD = 0
+DRAIN = 4
+WIDE = 2
+RELU_V = 2
+RUN = 4
+FOLD = 22
+RAMP = 22
 SPREAD = 1
-RAMP = 4
-SHARE = 3
+SHARE = 2
+SHARE0 = 4
+SHARE_FROM = 10
+SENDER_GAP = 2
+FAST = 24
+PIECE_GAP = 2
+PIECE_FROM = 41
 
 F32 = mybir.dt.float32
 BF16 = mybir.dt.bfloat16
@@ -35,22 +51,16 @@ ACT = mybir.ActivationFunctionType
 FLOPS = 2 * GRAPHS * N * N * NF * NF + 4 * 2 * GRAPHS * N * NF * NF
 
 
-def supply_order():
-    pieces = [[("w", key, kp, c) for key in ("r", "i", "s") for kp in range(PASSES)] for c in range(SETS)]
-    senders = [[("r", SENDERS * g + n) for n in range(SENDERS)] for g in range(GROUPS)]
-    items = pieces[0][:2]
-    for n in range(SENDERS):
-        items += [senders[0][n], pieces[0][2 + n]]
-    for c in range(1, SETS):
-        items += senders[c] + pieces[c]
+def supply_steps():
+    early = [("w", key, kp, c) for c in range(SETS) for key in ("i", "s", "r") for kp in range(PASSES)]
     late = [("w", key, kp, c) for key in ("o", "a") for kp in range(PASSES) for c in range(SETS)]
-    for g in range(SETS, GROUPS):
-        for n in range(SENDERS):
-            items += [senders[g][n], late.pop(0) if n % 2 == 0 else None]
-        items += [late.pop(0), None]
-    for piece in late:
-        items += [piece, None]
-    return items
+    ramp = len(early)
+    steps = {item: n for n, item in enumerate(early)}
+    steps.update({item: RAMP + 3 + BEAT * n for n, item in enumerate(late[:ON_GPSIMD])})
+    steps.update({item: PIECE_FROM + PIECE_GAP * n for n, item in enumerate(late[ON_GPSIMD:])})
+    for j in range(N):
+        steps["r", j] = j if j < FAST else FAST + SENDER_GAP * (j - FAST)
+    return steps
 
 
 def tile_compositionalkoopmanoperators_pa_kernel(
@@ -78,12 +88,14 @@ def tile_compositionalkoopmanoperators_pa_kernel(
 
         ctx.enter_context(tc.manual_schedule())
 
-        items = supply_order()
+        starts = supply_steps()
+        items = sorted(starts, key=lambda item: (starts[item], item[0] == "w"))
+        ramp = 3 * PASSES * SETS
+        late = [("w", key, kp, c) for key in ("o", "a") for kp in range(PASSES) for c in range(SETS)]
+        gpsimd_items = late[:ON_GPSIMD]
         raw = {}
 
         def load(item):
-            if item is None:
-                return
             if item[0] == "r":
                 j = item[1]
                 if j % 2 == 0:
@@ -105,9 +117,9 @@ def tile_compositionalkoopmanoperators_pa_kernel(
         ob = kept([P, NF], BF16, "ob")
         brow = kept([P, P // 2], F32, "brow")
         nc.vector.memset(brow[:], 0.0)
-        for n in range(AHEAD):
-            load(items[n])
-            if n == 2:
+        for n, item in enumerate([item for item in items if starts[item] < AHEAD]):
+            load(item)
+            if n == 1:
                 nc.sync.dma_start(out=ob[:], in_=obj_rows)
         nc.scalar.dma_start(
             out=brow[:].bitcast(BF16)[0 : NF // P, :], in_=rp_b.rearrange("(q p) -> q p", p=P)
@@ -120,7 +132,8 @@ def tile_compositionalkoopmanoperators_pa_kernel(
             for e in range(4):
                 c = 4 * half + e
                 nc.tensor.transpose(bank[:, e, :], sc8[:, c : c + 1].to_broadcast([P, P]), ident[:])
-            nc.scalar.copy(out=scale_v[:, :, 4 * half : 4 * half + 4], in_=bank[:].rearrange("m e p -> m p e"))
+            copy = nc.vector.tensor_copy if half else nc.scalar.copy
+            copy(out=scale_v[:, :, 4 * half : 4 * half + 4], in_=bank[:].rearrange("m e p -> m p e"))
 
         def turn_rows(rows, bank, passes):
             words = rows.bitcast(F32)
@@ -158,12 +171,23 @@ def tile_compositionalkoopmanoperators_pa_kernel(
         laid = {}
 
         def interleave(key, kp, c, engine):
-            wg = moving([P, 4 * PIECE], BF16, "wg", 5)
-            copy = nc.vector.tensor_copy if engine == "v" else nc.scalar.copy
-            copy(
-                out=wg[:].rearrange("p (c i t) -> p c t i", i=4, t=4),
-                in_=raw[key, kp, c][:].rearrange("p t (c i) -> p c t i", i=4),
-            )
+            if engine == "g":
+                wg = moving([P, 4 * PIECE], BF16, "wgg", 1)
+                nc.gpsimd.tensor_scalar(
+                    out=wg[:].rearrange("p (n t) -> p n t", t=4),
+                    in0=raw[key, kp, c][:].rearrange("p t n -> p n t"),
+                    scalar1=1.0,
+                    scalar2=0.0,
+                    op0=ALU.mult,
+                    op1=ALU.add,
+                )
+            else:
+                wg = moving([P, 4 * PIECE], BF16, "wg", 5)
+                copy = nc.vector.tensor_copy if engine == "v" else nc.scalar.copy
+                copy(
+                    out=wg[:].rearrange("p (c i t) -> p c t i", i=RUN, t=4),
+                    in_=raw[key, kp, c][:].rearrange("p t (c i) -> p c t i", i=RUN),
+                )
             laid[key, kp, c] = wg
 
         def quantise_piece(key, kp, c):
@@ -275,7 +299,7 @@ def tile_compositionalkoopmanoperators_pa_kernel(
                     )
 
         def add_receivers(g, q):
-            eff[g, q] = moving([P, SENDERS, P], F32, "eff", 8)
+            eff[g, q] = moving([P, SENDERS, P], F32, "eff", 12)
             nc.vector.tensor_tensor(
                 out=eff[g, q][:],
                 in0=acc[g, q][:],
@@ -283,17 +307,26 @@ def tile_compositionalkoopmanoperators_pa_kernel(
                 op=ALU.add,
             )
 
-        def relu_senders(g, q, folded):
+        def relu_senders(g, q, folded, engine):
             if folded:
-                eff[g, q] = moving([P, SENDERS, P], F32, "eff", 8)
+                eff[g, q] = moving([P, SENDERS, P], F32, "eff", 12)
             src = acc[g, q] if folded else eff[g, q]
             for s in range(SENDERS):
                 for b in range(GRAPHS):
                     col = N * b + SENDERS * g + s
                     cols = slice(N * b, N * (b + 1))
-                    nc.scalar.activation(
-                        eff[g, q][:, s, cols], src[:, s, cols], ACT.Relu, bias=send[q // 2][:, q % 2, col : col + 1]
-                    )
+                    bias = send[q // 2][:, q % 2, col : col + 1]
+                    if engine == "s":
+                        nc.scalar.activation(eff[g, q][:, s, cols], src[:, s, cols], ACT.Relu, bias=bias)
+                    else:
+                        nc.vector.tensor_scalar(
+                            out=eff[g, q][:, s, cols],
+                            in0=src[:, s, cols],
+                            scalar1=bias,
+                            scalar2=0.0,
+                            op0=ALU.add,
+                            op1=ALU.max,
+                        )
 
         def sum_senders(g, q):
             h = q // 4
@@ -320,7 +353,10 @@ def tile_compositionalkoopmanoperators_pa_kernel(
             nc.vector.tensor_copy(out=agg_rows[h][:], in_=agg[h][:].rearrange("p q f -> p (q f)"))
 
         def agg_turn(h):
-            agg_bank[h] = psum.tile([P, 2, P], F32, name="acc", tag="acc", bufs=4)
+            if h == 0:
+                agg_bank[h] = psum.tile([P, 2, P], F32, name="tr", tag="tr", bufs=2)
+            else:
+                agg_bank[h] = psum.tile([P, 2, P], F32, name="acc", tag="acc", bufs=4)
             turn_rows(agg_rows[h][:], agg_bank[h], 1)
 
         def agg_empty(h):
@@ -360,71 +396,91 @@ def tile_compositionalkoopmanoperators_pa_kernel(
         def at(step, rank, fn, *args):
             plan.setdefault(step, []).append((rank, len(plan.get(step, [])), fn, args))
 
-        def odd(n):
-            return n + 1 - n % 2
-
         def even(n):
             return n + n % 2
 
         group_ready = {}
         set_ready = {}
-        for n, item in enumerate(items):
-            if n + AHEAD < len(items):
-                at(n, 0, load, items[n + AHEAD])
-            if item is None:
-                continue
+        piece_ready = {}
+        for item in items:
+            n = starts[item]
+            turn_lag, quant_lag = (TURN0, QUANT0) if n < RAMP else (TURN, QUANT)
+            if n >= AHEAD:
+                at(n - AHEAD, 0, load, item)
             if item[0] == "r":
                 j = item[1]
-                turn_step = odd(n + TURN)
+                turn_step = n + turn_lag
                 at(n, 5, widen, j)
                 at(turn_step, 8, turn, j)
                 at(turn_step + 1, 1, empty, j)
                 if j % 2 == 1:
-                    at(turn_step + 1 + QUANT, 3, quantise_pair, j // 2)
+                    at(turn_step + 1 + quant_lag, 3, quantise_pair, j // 2)
                 if j % SENDERS == SENDERS - 1:
-                    group_ready[j // SENDERS] = turn_step + 2 + QUANT
+                    group_ready[j // SENDERS] = turn_step + 2 + quant_lag
                 last_turn = turn_step
             else:
                 key, kp, c = item[1:4]
-                at(n + QUANT, 3, quantise_piece, key, kp, c)
+                on_vector = n >= ramp or (n % SHARE0 == SHARE0 - 1 if n < SHARE_FROM else n % SHARE != 0)
+                if item in gpsimd_items:
+                    quant_lag = BEAT
+                    at(n, 2, interleave, key, kp, c, "g")
+                    at(n + quant_lag, 1, quantise_piece, key, kp, c)
+                else:
+                    at(n, 5, interleave, key, kp, c, "v" if on_vector else "s")
+                    at(n + quant_lag, 3, quantise_piece, key, kp, c)
+                piece_ready[key, kp] = max(piece_ready.get((key, kp), 0), n + quant_lag + 1)
                 if key == "s" and kp == PASSES - 1:
-                    at(even(n + QUANT + 1), 6, table_products, c)
-                    at(even(n + QUANT + 1) + 1, 1, table_copies, c)
-                    set_ready[c] = even(n + QUANT + 1)
+                    table_step = n + quant_lag + 1
+                    if table_step >= RAMP:
+                        table_step = table_step + (RAMP - table_step) % BEAT
+                    at(table_step, 6, table_products, c)
+                    at(table_step + 1, 1, table_copies, c)
+                    set_ready[c] = max(table_step, n + PASSES + quant_lag + 1)
         at(1, 6, bias_columns)
         at(3, 3, lambda: nc.vector.quantize_mx(out=oc[:].bitcast(FP8X4), scales=osc[:], in_=og[:]))
-        at(len(items) - AHEAD, 0, lambda: nc.sync.dma_start(out=pb[:], in_=pp_b.partition_broadcast(P)))
-        for kp in range(PASSES):
-            at(even(last_turn + 2) + 2 * kp, 6, final_pass, "o", kp)
-
-        pairs = sorted([(max(group_ready[g], set_ready[c]), g, c) for g in range(GROUPS) for c in range(SETS)])
-        step = 0
-        relu_steps = set()
-        for ready, g, c in pairs:
-            step = max(step + (RAMP if step < FOLD else 2), even(ready))
-            folded = step < FOLD
-            for m in range(2):
-                q = 2 * c + m
-                at(step, 6, product, g, q, folded)
-                if not folded:
-                    at(step + 1 + m * SPREAD, 2, add_receivers, g, q)
-                at(step + RELU + m, 4, relu_senders, g, q, folded)
-                relu_steps.add(step + RELU + m)
-                at(step + SUM, 7, sum_senders, g, q)
-            if g == GROUPS - 1 and c % 2 == 1:
-                at(step + SUM + 1, 3, agg_round, c // 2)
-                at(step + SUM + 2, 8, agg_turn, c // 2)
-                at(step + SUM + 3, 1, agg_empty, c // 2)
-                at(step + SUM + 4, 3, agg_quantise, c // 2)
-                at(step + SUM + 5, 6, final_pass, "a", c // 2)
-
-        shared = 0
-        for n, item in enumerate(items):
-            if item is None or item[0] == "r":
+        at(last_turn, 0, lambda: nc.sync.dma_start(out=pb[:], in_=pp_b.partition_broadcast(P)))
+        units = [(q // 4, g, q) for g in range(GROUPS) for q in range(2 * SETS)]
+        wide_from = last_turn + 1 + (last_turn + 1 - RAMP) % 2
+        slots = [(n, 0) for n in range(RAMP)] + [(n, m) for n in range(RAMP, wide_from, 2) for m in range(2)]
+        slots += [(n, m) for n in range(wide_from, 200, WIDE) for m in range(WIDE)]
+        left = [4 * GROUPS, 4 * GROUPS]
+        for step, m in slots:
+            ready = [u for u in units if max(group_ready[u[1]], set_ready[u[2] // 2]) <= step]
+            if not ready:
                 continue
-            shared = shared + 1
-            on_vector = n < 2 or (n >= 10 and shared % SHARE != 0) or n >= len(items) - 8
-            at(n, 5, interleave, item[1], item[2], item[3], "v" if on_vector else "s")
+            h, g, q = min(ready)
+            units.remove((h, g, q))
+            folded = step < FOLD
+            at(step, 6, product, g, q, folded)
+            if step < RAMP:
+                add_step = step + 1
+                relu_step = step + RELU0
+                sum_step = step + SUM0
+            elif step >= wide_from:
+                add_step = step + 1 + m
+                relu_step = add_step + RELU
+                sum_step = step + 2 * WIDE if len(units) >= DRAIN else relu_step + 1
+            else:
+                place = (step - RAMP) % BEAT
+                add_step = step - place + BEAT - 1 if len(units) >= DRAIN else step + 1
+                relu_step = add_step + RELU + (place + m if len(units) >= DRAIN else m)
+                sum_step = relu_step + SUM + (step + relu_step + SUM + 1) % 2
+            if not folded:
+                at(add_step, 2, add_receivers, g, q)
+            at(relu_step, 4, relu_senders, g, q, folded, "v" if len(units) < RELU_V and len(units) % 2 == 0 else "s")
+            at(sum_step, 7, sum_senders, g, q)
+            left[h] = left[h] - 1
+            if left[h] == 0:
+                at(sum_step + 1, 3, agg_round, h)
+                at(sum_step + 2, 8, agg_turn, h)
+                at(sum_step + 3, 1, agg_empty, h)
+                at(sum_step + 4, 3, agg_quantise, h)
+            if not units and left[1] == 0:
+                for kp in range(PASSES):
+                    at(step, 6, final_pass, "o", kp)
+                at(sum_step + 2, 9, final_pass, "a", 0)
+                at(sum_step + 5, 6, final_pass, "a", 1)
+                break
 
         for n in sorted(plan):
             for rank, order, fn, args in sorted(plan[n], key=lambda e: (e[0], e[1])):

@@ -27,7 +27,7 @@ ON_GPSIMD = 0
 DRAIN = 4
 WIDE = 2
 RELU_V = 2
-RUN = 4
+RUN = 8
 FOLD = 22
 RAMP = 22
 SPREAD = 1

@@ -14,30 +14,43 @@ GROUPS = N // SENDERS
 PIECE = 256
 SETS = NF // PIECE
 AHEAD = 6
-TURN0 = 1
+PRO = 6
+TURNP = 1
+QUANTP = 2
+TURN0 = 2
 QUANT0 = 2
 RELU0 = 2
 SUM0 = 4
-TURN = 3
-QUANT = 3
-RELU = 1
-SUM = 2
-BEAT = 2
-ON_GPSIMD = 0
-DRAIN = 4
-WIDE = 2
-RELU_V = 2
+TURN = 2
+QUANT = 2
+RELU = 0
+SUM = 3
+FINAL = 0
+TAPER = 0
+TAIL = 0
+TAIL_FROM = 77
+CUTS = 2
+DELAY = 2
+PDELAY = 1
+VP = 0
+OB = 2
+RV = 0
+V_EVERY = 2
+RELU_V = 4
+RELU_EVERY = 1000
 RUN = 8
-FOLD = 22
-RAMP = 22
-SPREAD = 1
-SHARE = 2
+WIDE = 3
+AGG = 3
+SETTLE = 2
+FOLD = 14
+SKIP = 4
+RAMP = 38
 SHARE0 = 4
-SHARE_FROM = 10
-SENDER_GAP = 2
-FAST = 24
-PIECE_GAP = 2
-PIECE_FROM = 41
+SHARE = 100
+FIRST = 12
+MID = 8
+MID_GAP = 5
+LATE_ENGINE = "g"
 
 F32 = mybir.dt.float32
 BF16 = mybir.dt.bfloat16
@@ -52,14 +65,15 @@ FLOPS = 2 * GRAPHS * N * N * NF * NF + 4 * 2 * GRAPHS * N * NF * NF
 
 
 def supply_steps():
-    early = [("w", key, kp, c) for c in range(SETS) for key in ("i", "s", "r") for kp in range(PASSES)]
-    late = [("w", key, kp, c) for key in ("o", "a") for kp in range(PASSES) for c in range(SETS)]
-    ramp = len(early)
-    steps = {item: n for n, item in enumerate(early)}
-    steps.update({item: RAMP + 3 + BEAT * n for n, item in enumerate(late[:ON_GPSIMD])})
-    steps.update({item: PIECE_FROM + PIECE_GAP * n for n, item in enumerate(late[ON_GPSIMD:])})
-    for j in range(N):
-        steps["r", j] = j if j < FAST else FAST + SENDER_GAP * (j - FAST)
+    pieces = [("w", key, kp, c) for c in range(SETS) for key in ("i", "s", "r") for kp in range(PASSES)]
+    pieces += [("w", key, kp, c) for key in ("o", "a") for kp in range(PASSES) for c in range(SETS)]
+    slots = [(n if n < 6 else n + PDELAY, "v" if n % SHARE0 == VP else "s") for n in range(FIRST)]
+    slots += [(FIRST + PDELAY + MID_GAP * n // 2, "v" if n % SHARE == SHARE - 1 else "s") for n in range(MID)]
+    for n in range(RAMP, RAMP + WIDE * len(pieces), WIDE):
+        slots += [(n + 1, LATE_ENGINE)] + [(n + 2, "v")] * ((n - RAMP) // WIDE % V_EVERY == 0)
+    slots = slots[: len(pieces) - TAIL] + [(TAIL_FROM + n, "s") for n in range(TAIL)]
+    steps = dict(zip(pieces, slots))
+    steps.update({("r", j): (j + 1 if j < SENDERS else j + DELAY, "v") for j in range(N)})
     return steps
 
 
@@ -88,11 +102,9 @@ def tile_compositionalkoopmanoperators_pa_kernel(
 
         ctx.enter_context(tc.manual_schedule())
 
-        starts = supply_steps()
-        items = sorted(starts, key=lambda item: (starts[item], item[0] == "w"))
-        ramp = 3 * PASSES * SETS
-        late = [("w", key, kp, c) for key in ("o", "a") for kp in range(PASSES) for c in range(SETS)]
-        gpsimd_items = late[:ON_GPSIMD]
+        supply = supply_steps()
+        starts = {item: supply[item][0] for item in supply}
+        items = sorted(starts, key=lambda item: (starts[item], item[0] == "r"))
         raw = {}
 
         def load(item):
@@ -113,13 +125,14 @@ def tile_compositionalkoopmanoperators_pa_kernel(
             raw[key, kp, c] = wr
 
         sc8 = kept([P, NF // P], F32, "sc8")
-        nc.sync.dma_start(out=sc8[:], in_=rel_scale.rearrange("a b c (p e) -> p (a b c e)", p=P))
         ob = kept([P, NF], BF16, "ob")
         brow = kept([P, P // 2], F32, "brow")
         nc.vector.memset(brow[:], 0.0)
         for n, item in enumerate([item for item in items if starts[item] < AHEAD]):
             load(item)
-            if n == 1:
+            if n == 0:
+                nc.sync.dma_start(out=sc8[:], in_=rel_scale.rearrange("a b c (p e) -> p (a b c e)", p=P))
+            if n == OB:
                 nc.sync.dma_start(out=ob[:], in_=obj_rows)
         nc.scalar.dma_start(
             out=brow[:].bitcast(BF16)[0 : NF // P, :], in_=rp_b.rearrange("(q p) -> q p", p=P)
@@ -127,8 +140,9 @@ def tile_compositionalkoopmanoperators_pa_kernel(
 
         scale = kept([P, NF], F32, "scale")
         scale_v = scale[:].rearrange("m (p e) -> m p e", e=8)
-        for half in range(2):
-            bank = psum.tile([P, 4, P], F32, name="acc", tag="acc", bufs=4)
+
+        def spread_scales(half):
+            bank = psum.tile([P, 4, P], F32, name="bank", tag="bank", bufs=6)
             for e in range(4):
                 c = 4 * half + e
                 nc.tensor.transpose(bank[:, e, :], sc8[:, c : c + 1].to_broadcast([P, P]), ident[:])
@@ -142,12 +156,15 @@ def tile_compositionalkoopmanoperators_pa_kernel(
                     nc.tensor.transpose(bank[:, 2 * kp + u, :], words[:, 256 * kp + u : 256 * (kp + 1) : 2], ident[:])
 
         og = kept([P, PASSES * P * 4], BF16, "og")
-        bank = psum.tile([P, 4, P], F32, name="acc", tag="acc", bufs=4)
-        turn_rows(ob[:], bank, PASSES)
-        nc.scalar.copy(
-            out=og[:].bitcast(F32).rearrange("p (g r u) -> p g r u", g=PASSES, u=2),
-            in_=bank[:].rearrange("p (g u) r -> p g r u", g=PASSES),
-        )
+
+        def turn_particles():
+            bank = psum.tile([P, 4, P], F32, name="bank", tag="bank", bufs=6)
+            turn_rows(ob[:], bank, PASSES)
+            nc.scalar.copy(
+                out=og[:].bitcast(F32).rearrange("p (g r u) -> p g r u", g=PASSES, u=2),
+                in_=bank[:].rearrange("p (g u) r -> p g r u", g=PASSES),
+            )
+
         oc = kept([P, PASSES * P], U32, "oc")
         osc = kept([P, PASSES * P], U8, "osc")
 
@@ -156,7 +173,7 @@ def tile_compositionalkoopmanoperators_pa_kernel(
         bcol = kept([P, NF // P], F32, "bcol")
 
         def bias_columns():
-            bank = psum.tile([P, P], BF16, name="acc", tag="acc", bufs=4)
+            bank = psum.tile([P, P], BF16, name="bank", tag="bank", bufs=6)
             nc.tensor.transpose(bank[:], brow[:].bitcast(BF16), identb[:])
             nc.scalar.copy(out=bcol[:], in_=bank[:, 0 : NF // P])
 
@@ -207,7 +224,7 @@ def tile_compositionalkoopmanoperators_pa_kernel(
         send = {}
 
         def table_products(c):
-            bank = psum.tile([P, 4, P], F32, name="acc", tag="acc", bufs=4)
+            bank = psum.tile([P, 4, P], F32, name="bank", tag="bank", bufs=6)
             for n, key in enumerate(("i", "s")):
                 for m in range(2):
                     for kp in range(PASSES):
@@ -247,7 +264,7 @@ def tile_compositionalkoopmanoperators_pa_kernel(
             )
 
         def turn(j):
-            turned[j] = psum.tile([P, 4, P], F32, name="tr", tag="tr", bufs=2)
+            turned[j] = psum.tile([P, 4, P], F32, name="bank", tag="bank", bufs=6)
             turn_rows(wide[j][:], turned[j], PASSES)
 
         def empty(j):
@@ -272,7 +289,7 @@ def tile_compositionalkoopmanoperators_pa_kernel(
         eff = {}
 
         def product(g, q, folded):
-            acc[g, q] = psum.tile([P, SENDERS, P], F32, name="acc", tag="acc", bufs=4)
+            acc[g, q] = psum.tile([P, SENDERS, P], F32, name="bank", tag="bank", bufs=6)
             for kp in range(PASSES):
                 wc, ws = stationary("r", kp, q)
                 cols = slice(SENDERS * P * kp, SENDERS * P * (kp + 1))
@@ -307,7 +324,7 @@ def tile_compositionalkoopmanoperators_pa_kernel(
                 op=ALU.add,
             )
 
-        def relu_senders(g, q, folded, engine):
+        def relu_senders(g, q, folded, on_vector):
             if folded:
                 eff[g, q] = moving([P, SENDERS, P], F32, "eff", 12)
             src = acc[g, q] if folded else eff[g, q]
@@ -316,7 +333,7 @@ def tile_compositionalkoopmanoperators_pa_kernel(
                     col = N * b + SENDERS * g + s
                     cols = slice(N * b, N * (b + 1))
                     bias = send[q // 2][:, q % 2, col : col + 1]
-                    if engine == "s":
+                    if s >= on_vector:
                         nc.scalar.activation(eff[g, q][:, s, cols], src[:, s, cols], ACT.Relu, bias=bias)
                     else:
                         nc.vector.tensor_scalar(
@@ -353,10 +370,7 @@ def tile_compositionalkoopmanoperators_pa_kernel(
             nc.vector.tensor_copy(out=agg_rows[h][:], in_=agg[h][:].rearrange("p q f -> p (q f)"))
 
         def agg_turn(h):
-            if h == 0:
-                agg_bank[h] = psum.tile([P, 2, P], F32, name="tr", tag="tr", bufs=2)
-            else:
-                agg_bank[h] = psum.tile([P, 2, P], F32, name="acc", tag="acc", bufs=4)
+            agg_bank[h] = psum.tile([P, 2, P], F32, name="bank", tag="bank", bufs=6)
             turn_rows(agg_rows[h][:], agg_bank[h], 1)
 
         def agg_empty(h):
@@ -380,7 +394,7 @@ def tile_compositionalkoopmanoperators_pa_kernel(
                 lc, ls = agg_codes[kp][:], agg_scales[kp][:]
             for h in range(2):
                 if (key, kp) == ("o", 0):
-                    final[h] = psum.tile([P, K_PASS], F32, name="tr", tag="tr", bufs=2)
+                    final[h] = psum.tile([P, K_PASS], F32, name="bank", tag="bank", bufs=6)
                 nc.tensor.matmul_mx(
                     out=final[h][:],
                     lhsT=lc.bitcast(FP8X4),
@@ -404,7 +418,7 @@ def tile_compositionalkoopmanoperators_pa_kernel(
         piece_ready = {}
         for item in items:
             n = starts[item]
-            turn_lag, quant_lag = (TURN0, QUANT0) if n < RAMP else (TURN, QUANT)
+            turn_lag, quant_lag = (TURNP, QUANTP) if n < PRO else (TURN0, QUANT0) if n < RAMP else (TURN, QUANT)
             if n >= AHEAD:
                 at(n - AHEAD, 0, load, item)
             if item[0] == "r":
@@ -420,75 +434,78 @@ def tile_compositionalkoopmanoperators_pa_kernel(
                 last_turn = turn_step
             else:
                 key, kp, c = item[1:4]
-                on_vector = n >= ramp or (n % SHARE0 == SHARE0 - 1 if n < SHARE_FROM else n % SHARE != 0)
-                if item in gpsimd_items:
-                    quant_lag = BEAT
+                if supply[item][1] == "g":
+                    quant_lag = WIDE
                     at(n, 2, interleave, key, kp, c, "g")
                     at(n + quant_lag, 1, quantise_piece, key, kp, c)
                 else:
-                    at(n, 5, interleave, key, kp, c, "v" if on_vector else "s")
+                    at(n, 5, interleave, key, kp, c, supply[item][1])
                     at(n + quant_lag, 3, quantise_piece, key, kp, c)
+                if key == "r" and kp == PASSES - 1:
+                    set_ready[c] = max(set_ready[c], n + quant_lag + 1)
                 piece_ready[key, kp] = max(piece_ready.get((key, kp), 0), n + quant_lag + 1)
                 if key == "s" and kp == PASSES - 1:
                     table_step = n + quant_lag + 1
                     if table_step >= RAMP:
-                        table_step = table_step + (RAMP - table_step) % BEAT
+                        table_step = table_step + (RAMP - table_step) % WIDE
                     at(table_step, 6, table_products, c)
                     at(table_step + 1, 1, table_copies, c)
-                    set_ready[c] = max(table_step, n + PASSES + quant_lag + 1)
-        at(1, 6, bias_columns)
-        at(3, 3, lambda: nc.vector.quantize_mx(out=oc[:].bitcast(FP8X4), scales=osc[:], in_=og[:]))
+                    set_ready[c] = table_step
+        at(0, 1, spread_scales, 0)
+        at(0, 6, spread_scales, 1)
+        at(1, 6, turn_particles)
+        at(2, 6, bias_columns)
+        at(4, 3, lambda: nc.vector.quantize_mx(out=oc[:].bitcast(FP8X4), scales=osc[:], in_=og[:]))
         at(last_turn, 0, lambda: nc.sync.dma_start(out=pb[:], in_=pp_b.partition_broadcast(P)))
         units = [(q // 4, g, q) for g in range(GROUPS) for q in range(2 * SETS)]
-        wide_from = last_turn + 1 + (last_turn + 1 - RAMP) % 2
-        slots = [(n, 0) for n in range(RAMP)] + [(n, m) for n in range(RAMP, wide_from, 2) for m in range(2)]
-        slots += [(n, m) for n in range(wide_from, 200, WIDE) for m in range(WIDE)]
-        left = [4 * GROUPS, 4 * GROUPS]
-        for step, m in slots:
-            ready = [u for u in units if max(group_ready[u[1]], set_ready[u[2] // 2]) <= step]
-            if not ready:
+        slots = [(n, 0, 1) for n in range(RAMP)]
+        slots += [(n, m, WIDE) for n in range(RAMP, RAMP + len(units), WIDE) for m in range(WIDE)]
+        placed = []
+        for step, m, burst in slots:
+            if burst > 1 and len(units) <= TAPER and m >= burst // 2:
                 continue
-            h, g, q = min(ready)
-            units.remove((h, g, q))
-            folded = step < FOLD
+            ready = [u for u in units if max(group_ready[u[1]], set_ready[u[2] // 2]) <= step]
+            if ready:
+                settled = [u for u in ready if group_ready[u[1]] + SETTLE <= step]
+                placed.append((step, m, burst) + min(settled or ready))
+                units.remove(min(settled or ready))
+        last_step = placed[-1][0]
+        last_sum = [0, 0]
+        for n, (step, m, burst, h, g, q) in enumerate(placed):
+            folded = step < FOLD or (step < RAMP and step % SKIP == 0)
             at(step, 6, product, g, q, folded)
-            if step < RAMP:
-                add_step = step + 1
-                relu_step = step + RELU0
-                sum_step = step + SUM0
-            elif step >= wide_from:
-                add_step = step + 1 + m
-                relu_step = add_step + RELU
-                sum_step = step + 2 * WIDE if len(units) >= DRAIN else relu_step + 1
+            if burst == 1:
+                add_step, relu_step, sum_step = step + 1, step + RELU0, step + SUM0
             else:
-                place = (step - RAMP) % BEAT
-                add_step = step - place + BEAT - 1 if len(units) >= DRAIN else step + 1
-                relu_step = add_step + RELU + (place + m if len(units) >= DRAIN else m)
-                sum_step = relu_step + SUM + (step + relu_step + SUM + 1) % 2
+                add_step = step + 1
+                relu_step = step + 1 + RELU + m
+                sum_step = step + SUM
+            sum_step = min(sum_step, max(relu_step + 1, last_step))
             if not folded:
                 at(add_step, 2, add_receivers, g, q)
-            at(relu_step, 4, relu_senders, g, q, folded, "v" if len(units) < RELU_V and len(units) % 2 == 0 else "s")
+            at(relu_step, 4, relu_senders, g, q, folded, SENDERS // 2 if n >= len(placed) - RELU_V else RV if burst > 1 and m == burst - 1 else 0)
             at(sum_step, 7, sum_senders, g, q)
-            left[h] = left[h] - 1
-            if left[h] == 0:
-                at(sum_step + 1, 3, agg_round, h)
-                at(sum_step + 2, 8, agg_turn, h)
-                at(sum_step + 3, 1, agg_empty, h)
-                at(sum_step + 4, 3, agg_quantise, h)
-            if not units and left[1] == 0:
-                for kp in range(PASSES):
-                    at(step, 6, final_pass, "o", kp)
-                at(sum_step + 2, 9, final_pass, "a", 0)
-                at(sum_step + 5, 6, final_pass, "a", 1)
-                break
+            last_sum[h] = max(last_sum[h], sum_step)
+        for h, gap in enumerate((AGG, 1)):
+            at(last_sum[h] + 1, 3, agg_round, h)
+            at(last_sum[h] + 1 + gap, 8, agg_turn, h)
+            at(last_sum[h] + 1 + 2 * gap, 1, agg_empty, h)
+            at(last_sum[h] + 1 + 3 * gap, 3, agg_quantise, h)
+        for kp in range(PASSES):
+            at(last_sum[1] + 1 if FINAL else last_step, 6, final_pass, "o", kp)
+        assert piece_ready["a", 0] <= last_sum[1] + 2 and piece_ready["a", 1] <= last_sum[1] + 5 and piece_ready["o", 1] <= last_step
+        at(last_sum[1] + 2, 9, final_pass, "a", 0)
+        at(last_sum[1] + 5, 6, final_pass, "a", 1)
 
         for n in sorted(plan):
             for rank, order, fn, args in sorted(plan[n], key=lambda e: (e[0], e[1])):
                 fn(*args)
 
-        for h in range(2):
-            cols = slice(K_PASS * h, K_PASS * (h + 1))
-            o1 = moving([P, K_PASS], F32, "o1", 2)
-            nc.vector.tensor_tensor(out=o1[:], in0=final[h][:], in1=pb[:, cols], op=ALU.add)
+        width = K_PASS // CUTS
+        for n in range(2 * CUTS):
+            cols = slice(width * n, width * (n + 1))
+            first = width * (n % CUTS)
+            o1 = moving([P, width], F32, "o1", 2 * CUTS)
+            nc.vector.tensor_tensor(out=o1[:], in0=final[n // CUTS][:, first : first + width], in1=pb[:, cols], op=ALU.add)
             nc.scalar.activation(o1[:], o1[:], ACT.Relu)
             nc.sync.dma_start(out=out_rows[:, cols], in_=o1[:])

@@ -13,8 +13,8 @@ SENDERS = 4
 GROUPS = N // SENDERS
 PIECE = 256
 SETS = NF // PIECE
-AHEAD = 6
-PRO = 6
+AHEAD = 4
+PRO = 0
 TURNP = 1
 QUANTP = 2
 TURN0 = 2
@@ -30,26 +30,31 @@ TAPER = 0
 TAIL = 0
 TAIL_FROM = 77
 CUTS = 2
-DELAY = 2
+DELAY = 1
 PDELAY = 1
-VP = 0
+VP = 50
 OB = 2
+NP = 12
+BRIDGE = 2
+PACE = 12
+MID_FROM = 12
+WEAVE = 1
 RV = 0
 V_EVERY = 2
-RELU_V = 4
+RELU_V = 2
 RELU_EVERY = 1000
 RUN = 8
 WIDE = 3
 AGG = 3
 SETTLE = 2
 FOLD = 14
-SKIP = 4
-RAMP = 38
-SHARE0 = 4
+SKIP = 3
+RAMP = 36
+SHARE0 = 100
 SHARE = 100
 FIRST = 12
-MID = 8
-MID_GAP = 5
+MID = 6
+MID_GAP = 7
 LATE_ENGINE = "g"
 
 F32 = mybir.dt.float32
@@ -67,8 +72,11 @@ FLOPS = 2 * GRAPHS * N * N * NF * NF + 4 * 2 * GRAPHS * N * NF * NF
 def supply_steps():
     pieces = [("w", key, kp, c) for c in range(SETS) for key in ("i", "s", "r") for kp in range(PASSES)]
     pieces += [("w", key, kp, c) for key in ("o", "a") for kp in range(PASSES) for c in range(SETS)]
-    slots = [(n if n < 6 else n + PDELAY, "v" if n % SHARE0 == VP else "s") for n in range(FIRST)]
-    slots += [(FIRST + PDELAY + MID_GAP * n // 2, "v" if n % SHARE == SHARE - 1 else "s") for n in range(MID)]
+    slots = [(n * PACE // 12, "v" if n % SHARE0 == VP else "p" if n < NP else "s") for n in range(FIRST)]
+    slots += [(MID_FROM + MID_GAP * n // 2, "v" if n % SHARE == SHARE - 1 else "s") for n in range(MID)]
+    slots += [(N + DELAY + n, "v") for n in range(BRIDGE)]
+    slots += [(RAMP + 1 - WIDE, "first")]
+    slots = sorted(slots)
     for n in range(RAMP, RAMP + WIDE * len(pieces), WIDE):
         slots += [(n + 1, LATE_ENGINE)] + [(n + 2, "v")] * ((n - RAMP) // WIDE % V_EVERY == 0)
     slots = slots[: len(pieces) - TAIL] + [(TAIL_FROM + n, "s") for n in range(TAIL)]
@@ -104,7 +112,7 @@ def tile_compositionalkoopmanoperators_pa_kernel(
 
         supply = supply_steps()
         starts = {item: supply[item][0] for item in supply}
-        items = sorted(starts, key=lambda item: (starts[item], item[0] == "r"))
+        items = sorted(starts, key=lambda item: (starts[item] - (item == ("r", 0)), item[0] == "w"))
         raw = {}
 
         def load(item):
@@ -118,7 +126,7 @@ def tile_compositionalkoopmanoperators_pa_kernel(
             key, kp, c = item[1:4]
             w, row = source[key]
             r0 = row + K_PASS * kp
-            wr = moving([P, 4, PIECE], BF16, "wr", 10)
+            wr = moving([P, 4, PIECE], BF16, "wr", 12)
             nc.sync.dma_start(
                 out=wr[:], in_=w[r0 : r0 + K_PASS, PIECE * c : PIECE * (c + 1)].rearrange("(p t) n -> p t n", t=4)
             )
@@ -129,9 +137,9 @@ def tile_compositionalkoopmanoperators_pa_kernel(
         brow = kept([P, P // 2], F32, "brow")
         nc.vector.memset(brow[:], 0.0)
         for n, item in enumerate([item for item in items if starts[item] < AHEAD]):
-            load(item)
             if n == 0:
                 nc.sync.dma_start(out=sc8[:], in_=rel_scale.rearrange("a b c (p e) -> p (a b c e)", p=P))
+            load(item)
             if n == OB:
                 nc.sync.dma_start(out=ob[:], in_=obj_rows)
         nc.scalar.dma_start(
@@ -187,6 +195,21 @@ def tile_compositionalkoopmanoperators_pa_kernel(
                     scales[key, kp, h] = kept([P, 2 * PIECE], U8, name + "s")
         laid = {}
 
+        woven = {}
+
+        def weave(key, kp, c):
+            bank = psum.tile([P, 4 * PIECE], BF16, name="bank", tag="bank", bufs=6)
+            half = PIECE // 2
+            for m in range(2):
+                nc.tensor.matmul(
+                    out=bank[:, 4 * half * m : 4 * half * (m + 1)],
+                    lhsT=identb[:],
+                    rhs=raw[key, kp, c][:, :, half * m : half * (m + 1)].rearrange("p t n -> p n t"),
+                    start=True,
+                    stop=True,
+                )
+            woven[key, kp, c] = bank
+
         def interleave(key, kp, c, engine):
             if engine == "g":
                 wg = moving([P, 4 * PIECE], BF16, "wgg", 1)
@@ -198,8 +221,11 @@ def tile_compositionalkoopmanoperators_pa_kernel(
                     op0=ALU.mult,
                     op1=ALU.add,
                 )
-            else:
+            elif engine == "p":
                 wg = moving([P, 4 * PIECE], BF16, "wg", 5)
+                nc.scalar.copy(out=wg[:], in_=woven[key, kp, c][:])
+            else:
+                wg = moving([P, 4 * PIECE], BF16, "wgg", 1) if engine == "first" else moving([P, 4 * PIECE], BF16, "wg", 5)
                 copy = nc.vector.tensor_copy if engine == "v" else nc.scalar.copy
                 copy(
                     out=wg[:].rearrange("p (c i t) -> p c t i", i=RUN, t=4),
@@ -268,20 +294,14 @@ def tile_compositionalkoopmanoperators_pa_kernel(
             turn_rows(wide[j][:], turned[j], PASSES)
 
         def empty(j):
-            if j % 2 == 0:
-                grouped[j // 2] = moving([P, PASSES * 2 * P * 4], BF16, "grp", 4)
-            view = grouped[j // 2][:].bitcast(F32).rearrange("p (g s r u) -> p g s r u", g=PASSES, s=2, u=2)
-            nc.scalar.copy(out=view[:, :, j % 2], in_=turned[j][:].rearrange("p (g u) r -> p g r u", g=PASSES))
+            g = j // SENDERS
+            if j % SENDERS == 0:
+                grouped[g] = moving([P, PASSES * SENDERS * P * 4], BF16, "grp", 2)
+            view = grouped[g][:].bitcast(F32).rearrange("p (g s r u) -> p g s r u", g=PASSES, s=SENDERS, u=2)
+            nc.scalar.copy(out=view[:, :, j % SENDERS], in_=turned[j][:].rearrange("p (g u) r -> p g r u", g=PASSES))
 
-        def quantise_pair(m):
-            g = m // 2
-            for kp in range(PASSES):
-                first = SENDERS * P * kp + 2 * P * (m % 2)
-                nc.vector.quantize_mx(
-                    out=rel_codes[g][:, first : first + 2 * P].bitcast(FP8X4),
-                    scales=rel_scales[g][:, first : first + 2 * P],
-                    in_=grouped[m][:, 8 * P * kp : 8 * P * (kp + 1)],
-                )
+        def quantise_group(g):
+            nc.vector.quantize_mx(out=rel_codes[g][:].bitcast(FP8X4), scales=rel_scales[g][:], in_=grouped[g][:])
 
         agg = [psum.tile([P, 4, P], F32, name="agg%d" % h, tag="agg%d" % h, bufs=1) for h in range(2)]
         summed = [0, 0]
@@ -427,17 +447,21 @@ def tile_compositionalkoopmanoperators_pa_kernel(
                 at(n, 5, widen, j)
                 at(turn_step, 8, turn, j)
                 at(turn_step + 1, 1, empty, j)
-                if j % 2 == 1:
-                    at(turn_step + 1 + quant_lag, 3, quantise_pair, j // 2)
                 if j % SENDERS == SENDERS - 1:
+                    at(turn_step + 1 + quant_lag, 3, quantise_group, j // SENDERS)
                     group_ready[j // SENDERS] = turn_step + 2 + quant_lag
                 last_turn = turn_step
             else:
                 key, kp, c = item[1:4]
-                if supply[item][1] == "g":
+                if supply[item][1] in ("g", "first"):
                     quant_lag = WIDE
-                    at(n, 2, interleave, key, kp, c, "g")
+                    at(n, 2, interleave, key, kp, c, supply[item][1])
                     at(n + quant_lag, 1, quantise_piece, key, kp, c)
+                elif supply[item][1] == "p":
+                    quant_lag = quant_lag + WEAVE
+                    at(n, 9, weave, key, kp, c)
+                    at(n + WEAVE, 5, interleave, key, kp, c, "p")
+                    at(n + quant_lag, 3, quantise_piece, key, kp, c)
                 else:
                     at(n, 5, interleave, key, kp, c, supply[item][1])
                     at(n + quant_lag, 3, quantise_piece, key, kp, c)

@@ -13,49 +13,17 @@ SENDERS = 4
 GROUPS = N // SENDERS
 PIECE = 256
 SETS = NF // PIECE
+CHUNKS = NF // P
+
 AHEAD = 4
-PRO = 0
-TURNP = 1
-QUANTP = 2
-TURN0 = 2
-QUANT0 = 2
-RELU0 = 2
-SUM0 = 4
-TURN = 2
-QUANT = 2
-RELU = 0
-SUM = 3
-FINAL = 0
-TAPER = 0
-TAIL = 0
-TAIL_FROM = 77
-CUTS = 2
-DELAY = 1
-PDELAY = 1
-VP = 50
-OB = 2
-NP = 12
-BRIDGE = 2
-PACE = 12
-MID_FROM = 12
-WEAVE = 1
-RV = 0
-V_EVERY = 2
-RELU_V = 2
-RELU_EVERY = 1000
+LAG = 2
+RAMP = N + 2 * LAG
+FOLD_EVERY = 3
+BURST = 3
+MID_GAP = 3
 RUN = 8
-WIDE = 3
-AGG = 3
-SETTLE = 2
-FOLD = 14
-SKIP = 3
-RAMP = 36
-SHARE0 = 100
-SHARE = 100
-FIRST = 12
-MID = 6
-MID_GAP = 7
-LATE_ENGINE = "g"
+OUT_PARTS = 4
+BANKS = 6
 
 F32 = mybir.dt.float32
 BF16 = mybir.dt.bfloat16
@@ -68,21 +36,19 @@ ACT = mybir.ActivationFunctionType
 
 FLOPS = 2 * GRAPHS * N * N * NF * NF + 4 * 2 * GRAPHS * N * NF * NF
 
+LOAD, FREE, ADD, QUANTISE, RELU, SUPPLY, MULTIPLY, SUM, TURN, WEAVE = range(10)
 
-def supply_steps():
-    pieces = [("w", key, kp, c) for c in range(SETS) for key in ("i", "s", "r") for kp in range(PASSES)]
-    pieces += [("w", key, kp, c) for key in ("o", "a") for kp in range(PASSES) for c in range(SETS)]
-    slots = [(n * PACE // 12, "v" if n % SHARE0 == VP else "p" if n < NP else "s") for n in range(FIRST)]
-    slots += [(MID_FROM + MID_GAP * n // 2, "v" if n % SHARE == SHARE - 1 else "s") for n in range(MID)]
-    slots += [(N + DELAY + n, "v") for n in range(BRIDGE)]
-    slots += [(RAMP + 1 - WIDE, "first")]
-    slots = sorted(slots)
-    for n in range(RAMP, RAMP + WIDE * len(pieces), WIDE):
-        slots += [(n + 1, LATE_ENGINE)] + [(n + 2, "v")] * ((n - RAMP) // WIDE % V_EVERY == 0)
-    slots = slots[: len(pieces) - TAIL] + [(TAIL_FROM + n, "s") for n in range(TAIL)]
-    steps = dict(zip(pieces, slots))
-    steps.update({("r", j): (j + 1 if j < SENDERS else j + DELAY, "v") for j in range(N)})
-    return steps
+
+def piece_plan():
+    pieces = [(key, kp, c) for c in range(SETS) for key in ("i", "s", "r") for kp in range(PASSES)]
+    pieces += [(key, kp, c) for key in ("o", "a") for kp in range(PASSES) for c in range(SETS)]
+    per_set = 3 * PASSES
+    slots = [(n, "scalar" if n % 2 else "tensor") for n in range(2 * per_set)]
+    slots += [(2 * per_set + MID_GAP * n, "scalar") for n in range(per_set)]
+    slots += [(N + 1, "vector"), (RAMP + 1 - BURST, "lead"), (N + 2, "vector")]
+    for n, step in enumerate(range(RAMP, RAMP + BURST * len(pieces), BURST)):
+        slots += [(step + 1, "gpsimd")] + [(step + 2, "vector")] * (n % 2 == 0)
+    return dict(zip(pieces, slots))
 
 
 def tile_compositionalkoopmanoperators_pa_kernel(
@@ -96,66 +62,70 @@ def tile_compositionalkoopmanoperators_pa_kernel(
 
     with ExitStack() as ctx:
         keep = ctx.enter_context(tc.tile_pool(name="keep", bufs=1))
-        work = ctx.enter_context(tc.tile_pool(name="work", bufs=3))
-        psum = ctx.enter_context(tc.psum_pool(name="psum", bufs=2))
+        work = ctx.enter_context(tc.tile_pool(name="work", bufs=1))
+        psum = ctx.enter_context(tc.psum_pool(name="psum", bufs=1))
 
         def kept(shape, dtype, name):
             return keep.tile(shape, dtype, name=name, tag=name, align_bytes=64)
 
-        def moving(shape, dtype, name, bufs):
+        def rotating(shape, dtype, name, bufs):
             return work.tile(shape, dtype, name=name, tag=name, bufs=bufs, align_bytes=64)
+
+        def bank_tile(shape, dtype):
+            return psum.tile(shape, dtype, name="bank", tag="bank", bufs=BANKS)
 
         ident = kept([P, P], F32, "ident")
         make_identity(nc, ident[:])
 
         ctx.enter_context(tc.manual_schedule())
 
-        supply = supply_steps()
-        starts = {item: supply[item][0] for item in supply}
-        items = sorted(starts, key=lambda item: (starts[item] - (item == ("r", 0)), item[0] == "w"))
-        raw = {}
+        pieces = piece_plan()
+        rel_raw = {}
+        w_raw = {}
 
-        def load(item):
-            if item[0] == "r":
-                j = item[1]
-                if j % 2 == 0:
-                    rb = moving([P, 2 * NF], U8, "rb", 5)
-                    nc.sync.dma_start(out=rb[:], in_=rel_rows[:, NF * j : NF * (j + 2)])
-                    raw["r", j // 2] = rb
-                return
-            key, kp, c = item[1:4]
+        def load_pair(m):
+            rel_raw[m] = rotating([P, 2 * NF], U8, "rel_raw", 5)
+            nc.sync.dma_start(out=rel_raw[m][:], in_=rel_rows[:, 2 * NF * m : 2 * NF * (m + 1)])
+
+        def load_piece(key, kp, c):
             w, row = source[key]
-            r0 = row + K_PASS * kp
-            wr = moving([P, 4, PIECE], BF16, "wr", 12)
+            rows = slice(row + K_PASS * kp, row + K_PASS * (kp + 1))
+            w_raw[key, kp, c] = rotating([P, 4, PIECE], BF16, "w_raw", 12)
             nc.sync.dma_start(
-                out=wr[:], in_=w[r0 : r0 + K_PASS, PIECE * c : PIECE * (c + 1)].rearrange("(p t) n -> p t n", t=4)
+                out=w_raw[key, kp, c][:], in_=w[rows, PIECE * c : PIECE * (c + 1)].rearrange("(p t) n -> p t n", t=4)
             )
-            raw[key, kp, c] = wr
 
-        sc8 = kept([P, NF // P], F32, "sc8")
-        ob = kept([P, NF], BF16, "ob")
-        brow = kept([P, P // 2], F32, "brow")
-        nc.vector.memset(brow[:], 0.0)
-        for n, item in enumerate([item for item in items if starts[item] < AHEAD]):
-            if n == 0:
-                nc.sync.dma_start(out=sc8[:], in_=rel_scale.rearrange("a b c (p e) -> p (a b c e)", p=P))
-            load(item)
-            if n == OB:
-                nc.sync.dma_start(out=ob[:], in_=obj_rows)
-        nc.scalar.dma_start(
-            out=brow[:].bitcast(BF16)[0 : NF // P, :], in_=rp_b.rearrange("(q p) -> q p", p=P)
-        )
+        scale_rows = kept([P, NF // P], F32, "scale_rows")
+        obj_sb = kept([P, NF], BF16, "obj_sb")
+        bias_rows = kept([P, P // 2], F32, "bias_rows")
+        out_bias = kept([P, NF], BF16, "out_bias")
+
+        def load_scales():
+            nc.sync.dma_start(out=scale_rows[:], in_=rel_scale.rearrange("a b c (p e) -> p (a b c e)", p=P))
+
+        def load_particles():
+            nc.sync.dma_start(out=obj_sb[:], in_=obj_rows)
+
+        def load_out_bias():
+            nc.sync.dma_start(out=out_bias[:], in_=pp_b.partition_broadcast(P))
+
+        nc.vector.memset(bias_rows[:], 0.0)
+        nc.scalar.dma_start(out=bias_rows[:].bitcast(BF16)[0:CHUNKS, :], in_=rp_b.rearrange("(q p) -> q p", p=P))
+        ident_bf = kept([P, P], BF16, "ident_bf")
+        nc.vector.tensor_copy(out=ident_bf[:], in_=ident[:])
 
         scale = kept([P, NF], F32, "scale")
-        scale_v = scale[:].rearrange("m (p e) -> m p e", e=8)
 
         def spread_scales(half):
-            bank = psum.tile([P, 4, P], F32, name="bank", tag="bank", bufs=6)
+            bank = bank_tile([P, 4, P], F32)
             for e in range(4):
-                c = 4 * half + e
-                nc.tensor.transpose(bank[:, e, :], sc8[:, c : c + 1].to_broadcast([P, P]), ident[:])
+                col = 4 * half + e
+                nc.tensor.transpose(bank[:, e, :], scale_rows[:, col : col + 1].to_broadcast([P, P]), ident[:])
             copy = nc.vector.tensor_copy if half else nc.scalar.copy
-            copy(out=scale_v[:, :, 4 * half : 4 * half + 4], in_=bank[:].rearrange("m e p -> m p e"))
+            copy(
+                out=scale[:].rearrange("m (p e) -> m p e", e=8)[:, :, 4 * half : 4 * half + 4],
+                in_=bank[:].rearrange("m e p -> m p e"),
+            )
 
         def turn_rows(rows, bank, passes):
             words = rows.bitcast(F32)
@@ -163,155 +133,157 @@ def tile_compositionalkoopmanoperators_pa_kernel(
                 for u in range(2):
                     nc.tensor.transpose(bank[:, 2 * kp + u, :], words[:, 256 * kp + u : 256 * (kp + 1) : 2], ident[:])
 
-        og = kept([P, PASSES * P * 4], BF16, "og")
+        obj_laid = kept([P, PASSES * P * 4], BF16, "obj_laid")
+        obj_codes = kept([P, PASSES * P], U32, "obj_codes")
+        obj_scales = kept([P, PASSES * P], U8, "obj_scales")
 
         def turn_particles():
-            bank = psum.tile([P, 4, P], F32, name="bank", tag="bank", bufs=6)
-            turn_rows(ob[:], bank, PASSES)
+            bank = bank_tile([P, 4, P], F32)
+            turn_rows(obj_sb[:], bank, PASSES)
             nc.scalar.copy(
-                out=og[:].bitcast(F32).rearrange("p (g r u) -> p g r u", g=PASSES, u=2),
+                out=obj_laid[:].bitcast(F32).rearrange("p (g r u) -> p g r u", g=PASSES, u=2),
                 in_=bank[:].rearrange("p (g u) r -> p g r u", g=PASSES),
             )
 
-        oc = kept([P, PASSES * P], U32, "oc")
-        osc = kept([P, PASSES * P], U8, "osc")
+        def quantise_particles():
+            nc.vector.quantize_mx(out=obj_codes[:].bitcast(FP8X4), scales=obj_scales[:], in_=obj_laid[:])
 
-        identb = kept([P, P], BF16, "identb")
-        nc.vector.tensor_copy(out=identb[:], in_=ident[:])
-        bcol = kept([P, NF // P], F32, "bcol")
+        def particles(kp):
+            return obj_codes[:, P * kp : P * (kp + 1)].bitcast(FP8X4), obj_scales[:, P * kp : P * (kp + 1)]
 
-        def bias_columns():
-            bank = psum.tile([P, P], BF16, name="bank", tag="bank", bufs=6)
-            nc.tensor.transpose(bank[:], brow[:].bitcast(BF16), identb[:])
-            nc.scalar.copy(out=bcol[:], in_=bank[:, 0 : NF // P])
+        bias_cols = kept([P, CHUNKS], F32, "bias_cols")
 
-        codes = {}
-        scales = {}
+        def turn_bias():
+            bank = bank_tile([P, P], BF16)
+            nc.tensor.transpose(bank[:], bias_rows[:].bitcast(BF16), ident_bf[:])
+            nc.scalar.copy(out=bias_cols[:], in_=bank[:, 0:CHUNKS])
+
+        w_codes = {}
+        w_scales = {}
         for key in source:
             for kp in range(PASSES):
                 for h in range(2):
-                    name = "w%s%d%d" % (key, kp, h)
-                    codes[key, kp, h] = kept([P, 2 * PIECE], U32, name + "c")
-                    scales[key, kp, h] = kept([P, 2 * PIECE], U8, name + "s")
+                    w_codes[key, kp, h] = kept([P, 2 * PIECE], U32, "codes_%s%d%d" % (key, kp, h))
+                    w_scales[key, kp, h] = kept([P, 2 * PIECE], U8, "scales_%s%d%d" % (key, kp, h))
+        woven = {}
         laid = {}
 
-        woven = {}
-
         def weave(key, kp, c):
-            bank = psum.tile([P, 4 * PIECE], BF16, name="bank", tag="bank", bufs=6)
-            half = PIECE // 2
+            woven[key, kp, c] = bank_tile([P, 4 * PIECE], BF16)
             for m in range(2):
                 nc.tensor.matmul(
-                    out=bank[:, 4 * half * m : 4 * half * (m + 1)],
-                    lhsT=identb[:],
-                    rhs=raw[key, kp, c][:, :, half * m : half * (m + 1)].rearrange("p t n -> p n t"),
+                    out=woven[key, kp, c][:, K_PASS * m : K_PASS * (m + 1)],
+                    lhsT=ident_bf[:],
+                    rhs=w_raw[key, kp, c][:, :, P * m : P * (m + 1)].rearrange("p t n -> p n t"),
                     start=True,
                     stop=True,
                 )
-            woven[key, kp, c] = bank
 
         def interleave(key, kp, c, engine):
-            if engine == "g":
-                wg = moving([P, 4 * PIECE], BF16, "wgg", 1)
+            if engine in ("gpsimd", "lead"):
+                laid[key, kp, c] = rotating([P, 4 * PIECE], BF16, "laid_gpsimd", 1)
+            else:
+                laid[key, kp, c] = rotating([P, 4 * PIECE], BF16, "laid", 5)
+            dst, src = laid[key, kp, c][:], w_raw[key, kp, c][:]
+            if engine == "tensor":
+                nc.scalar.copy(out=dst, in_=woven[key, kp, c][:])
+            elif engine == "gpsimd":
                 nc.gpsimd.tensor_scalar(
-                    out=wg[:].rearrange("p (n t) -> p n t", t=4),
-                    in0=raw[key, kp, c][:].rearrange("p t n -> p n t"),
+                    out=dst.rearrange("p (n t) -> p n t", t=4),
+                    in0=src.rearrange("p t n -> p n t"),
                     scalar1=1.0,
                     scalar2=0.0,
                     op0=ALU.mult,
                     op1=ALU.add,
                 )
-            elif engine == "p":
-                wg = moving([P, 4 * PIECE], BF16, "wg", 5)
-                nc.scalar.copy(out=wg[:], in_=woven[key, kp, c][:])
             else:
-                wg = moving([P, 4 * PIECE], BF16, "wgg", 1) if engine == "first" else moving([P, 4 * PIECE], BF16, "wg", 5)
-                copy = nc.vector.tensor_copy if engine == "v" else nc.scalar.copy
+                copy = nc.scalar.copy if engine == "scalar" else nc.vector.tensor_copy
                 copy(
-                    out=wg[:].rearrange("p (c i t) -> p c t i", i=RUN, t=4),
-                    in_=raw[key, kp, c][:].rearrange("p t (c i) -> p c t i", i=RUN),
+                    out=dst.rearrange("p (c i t) -> p c t i", i=RUN, t=4),
+                    in_=src.rearrange("p t (c i) -> p c t i", i=RUN),
                 )
-            laid[key, kp, c] = wg
 
         def quantise_piece(key, kp, c):
             cols = slice(PIECE * (c % 2), PIECE * (c % 2 + 1))
             nc.vector.quantize_mx(
-                out=codes[key, kp, c // 2][:, cols].bitcast(FP8X4),
-                scales=scales[key, kp, c // 2][:, cols],
+                out=w_codes[key, kp, c // 2][:, cols].bitcast(FP8X4),
+                scales=w_scales[key, kp, c // 2][:, cols],
                 in_=laid[key, kp, c][:],
             )
 
-        def stationary(key, kp, q):
+        def chunk_weights(key, kp, q):
             cols = slice(P * (q % 4), P * (q % 4 + 1))
-            return codes[key, kp, q // 4][:, cols].bitcast(FP8X4), scales[key, kp, q // 4][:, cols]
+            return w_codes[key, kp, q // 4][:, cols].bitcast(FP8X4), w_scales[key, kp, q // 4][:, cols]
 
-        table_bank = {}
+        term_bank = {}
         recv = {}
         send = {}
 
-        def table_products(c):
-            bank = psum.tile([P, 4, P], F32, name="bank", tag="bank", bufs=6)
+        def term_products(c):
+            term_bank[c] = bank_tile([P, 4, P], F32)
             for n, key in enumerate(("i", "s")):
                 for m in range(2):
                     for kp in range(PASSES):
-                        wc, ws = stationary(key, kp, 2 * c + m)
+                        wc, ws = chunk_weights(key, kp, 2 * c + m)
+                        oc, osc = particles(kp)
                         nc.tensor.matmul_mx(
-                            out=bank[:, 2 * n + m, :],
+                            out=term_bank[c][:, 2 * n + m, :],
                             lhsT=wc,
                             lhsT_scale=ws,
-                            rhs=oc[:, P * kp : P * (kp + 1)].bitcast(FP8X4),
-                            rhs_scale=osc[:, P * kp : P * (kp + 1)],
+                            rhs=oc,
+                            rhs_scale=osc,
                             start=(kp == 0),
                             stop=(kp == PASSES - 1),
                         )
-            table_bank[c] = bank
 
-        def table_copies(c):
+        def term_copies(c):
             recv[c] = kept([P, 2, P], F32, "recv%d" % c)
             send[c] = kept([P, 2, P], F32, "send%d" % c)
-            nc.scalar.copy(out=recv[c][:], in_=table_bank[c][:, 0:2, :])
+            nc.scalar.copy(out=recv[c][:], in_=term_bank[c][:, 0:2, :])
             for m in range(2):
                 q = 2 * c + m
-                nc.scalar.activation(send[c][:, m, :], table_bank[c][:, 2 + m, :], ACT.Identity, bias=bcol[:, q : q + 1])
+                nc.scalar.activation(
+                    send[c][:, m, :], term_bank[c][:, 2 + m, :], ACT.Identity, bias=bias_cols[:, q : q + 1]
+                )
 
         wide = {}
         turned = {}
-        grouped = {}
-        rel_codes = [kept([P, PASSES * SENDERS * P], U32, "rc%d" % g) for g in range(GROUPS)]
-        rel_scales = [kept([P, PASSES * SENDERS * P], U8, "rs%d" % g) for g in range(GROUPS)]
+        rel_laid = {}
+        rel_codes = [kept([P, PASSES * SENDERS * P], U32, "rel_codes%d" % g) for g in range(GROUPS)]
+        rel_scales = [kept([P, PASSES * SENDERS * P], U8, "rel_scales%d" % g) for g in range(GROUPS)]
 
         def widen(j):
-            wide[j] = moving([P, NF], BF16, "wide", 5)
+            wide[j] = rotating([P, NF], BF16, "wide", 5)
             nc.vector.tensor_tensor(
                 out=wide[j][:],
-                in0=raw["r", j // 2][:, NF * (j % 2) : NF * (j % 2 + 1)].bitcast(FP8),
+                in0=rel_raw[j // 2][:, NF * (j % 2) : NF * (j % 2 + 1)].bitcast(FP8),
                 in1=scale[:],
                 op=ALU.mult,
             )
 
         def turn(j):
-            turned[j] = psum.tile([P, 4, P], F32, name="bank", tag="bank", bufs=6)
+            turned[j] = bank_tile([P, 4, P], F32)
             turn_rows(wide[j][:], turned[j], PASSES)
 
         def empty(j):
             g = j // SENDERS
             if j % SENDERS == 0:
-                grouped[g] = moving([P, PASSES * SENDERS * P * 4], BF16, "grp", 2)
-            view = grouped[g][:].bitcast(F32).rearrange("p (g s r u) -> p g s r u", g=PASSES, s=SENDERS, u=2)
+                rel_laid[g] = rotating([P, PASSES * SENDERS * P * 4], BF16, "rel_laid", 2)
+            view = rel_laid[g][:].bitcast(F32).rearrange("p (g s r u) -> p g s r u", g=PASSES, s=SENDERS, u=2)
             nc.scalar.copy(out=view[:, :, j % SENDERS], in_=turned[j][:].rearrange("p (g u) r -> p g r u", g=PASSES))
 
         def quantise_group(g):
-            nc.vector.quantize_mx(out=rel_codes[g][:].bitcast(FP8X4), scales=rel_scales[g][:], in_=grouped[g][:])
+            nc.vector.quantize_mx(out=rel_codes[g][:].bitcast(FP8X4), scales=rel_scales[g][:], in_=rel_laid[g][:])
 
-        agg = [psum.tile([P, 4, P], F32, name="agg%d" % h, tag="agg%d" % h, bufs=1) for h in range(2)]
+        agg = [psum.tile([P, 4, P], F32, name="agg%d" % h, tag="agg%d" % h) for h in range(2)]
         summed = [0, 0]
         acc = {}
         eff = {}
 
         def product(g, q, folded):
-            acc[g, q] = psum.tile([P, SENDERS, P], F32, name="bank", tag="bank", bufs=6)
+            acc[g, q] = bank_tile([P, SENDERS, P], F32)
             for kp in range(PASSES):
-                wc, ws = stationary("r", kp, q)
+                wc, ws = chunk_weights("r", kp, q)
                 cols = slice(SENDERS * P * kp, SENDERS * P * (kp + 1))
                 nc.tensor.matmul_mx(
                     out=acc[g, q][:].rearrange("p s r -> p (s r)"),
@@ -323,20 +295,21 @@ def tile_compositionalkoopmanoperators_pa_kernel(
                     stop=(kp == PASSES - 1 and not folded),
                 )
             for kp in range(PASSES if folded else 0):
-                wc, ws = stationary("i", kp, q)
+                wc, ws = chunk_weights("i", kp, q)
+                oc, osc = particles(kp)
                 for s in range(SENDERS):
                     nc.tensor.matmul_mx(
                         out=acc[g, q][:, s, :],
                         lhsT=wc,
                         lhsT_scale=ws,
-                        rhs=oc[:, P * kp : P * (kp + 1)].bitcast(FP8X4),
-                        rhs_scale=osc[:, P * kp : P * (kp + 1)],
+                        rhs=oc,
+                        rhs_scale=osc,
                         start=False,
                         stop=(kp == PASSES - 1 and s == SENDERS - 1),
                     )
 
         def add_receivers(g, q):
-            eff[g, q] = moving([P, SENDERS, P], F32, "eff", 12)
+            eff[g, q] = rotating([P, SENDERS, P], F32, "eff", 12)
             nc.vector.tensor_tensor(
                 out=eff[g, q][:],
                 in0=acc[g, q][:],
@@ -346,16 +319,14 @@ def tile_compositionalkoopmanoperators_pa_kernel(
 
         def relu_senders(g, q, folded, on_vector):
             if folded:
-                eff[g, q] = moving([P, SENDERS, P], F32, "eff", 12)
+                eff[g, q] = rotating([P, SENDERS, P], F32, "eff", 12)
             src = acc[g, q] if folded else eff[g, q]
             for s in range(SENDERS):
                 for b in range(GRAPHS):
-                    col = N * b + SENDERS * g + s
+                    sender = N * b + SENDERS * g + s
+                    bias = send[q // 2][:, q % 2, sender : sender + 1]
                     cols = slice(N * b, N * (b + 1))
-                    bias = send[q // 2][:, q % 2, col : col + 1]
-                    if s >= on_vector:
-                        nc.scalar.activation(eff[g, q][:, s, cols], src[:, s, cols], ACT.Relu, bias=bias)
-                    else:
+                    if s < on_vector:
                         nc.vector.tensor_scalar(
                             out=eff[g, q][:, s, cols],
                             in0=src[:, s, cols],
@@ -364,6 +335,8 @@ def tile_compositionalkoopmanoperators_pa_kernel(
                             op0=ALU.add,
                             op1=ALU.max,
                         )
+                    else:
+                        nc.scalar.activation(eff[g, q][:, s, cols], src[:, s, cols], ACT.Relu, bias=bias)
 
         def sum_senders(g, q):
             h = q // 4
@@ -378,158 +351,145 @@ def tile_compositionalkoopmanoperators_pa_kernel(
                 )
                 summed[h] = summed[h] + 1
 
-        pb = kept([P, NF], BF16, "pb")
         agg_rows = {}
         agg_bank = {}
         agg_laid = {}
         agg_codes = {}
         agg_scales = {}
+        final = {}
 
         def agg_round(h):
-            agg_rows[h] = kept([P, K_PASS], BF16, "ar%d" % h)
+            agg_rows[h] = kept([P, K_PASS], BF16, "agg_rows%d" % h)
             nc.vector.tensor_copy(out=agg_rows[h][:], in_=agg[h][:].rearrange("p q f -> p (q f)"))
 
         def agg_turn(h):
-            agg_bank[h] = psum.tile([P, 2, P], F32, name="bank", tag="bank", bufs=6)
+            agg_bank[h] = bank_tile([P, 2, P], F32)
             turn_rows(agg_rows[h][:], agg_bank[h], 1)
 
         def agg_empty(h):
-            agg_laid[h] = kept([P, 4 * P], BF16, "al%d" % h)
+            agg_laid[h] = kept([P, 4 * P], BF16, "agg_laid%d" % h)
             nc.scalar.copy(
                 out=agg_laid[h][:].bitcast(F32).rearrange("p (r u) -> p r u", u=2),
                 in_=agg_bank[h][:].rearrange("p u r -> p r u"),
             )
 
         def agg_quantise(h):
-            agg_codes[h] = kept([P, P], U32, "ac%d" % h)
-            agg_scales[h] = kept([P, P], U8, "as%d" % h)
+            agg_codes[h] = kept([P, P], U32, "agg_codes%d" % h)
+            agg_scales[h] = kept([P, P], U8, "agg_scales%d" % h)
             nc.vector.quantize_mx(out=agg_codes[h][:].bitcast(FP8X4), scales=agg_scales[h][:], in_=agg_laid[h][:])
 
-        final = {}
-
         def final_pass(key, kp):
-            if key == "o":
-                lc, ls = oc[:, P * kp : P * (kp + 1)], osc[:, P * kp : P * (kp + 1)]
-            else:
-                lc, ls = agg_codes[kp][:], agg_scales[kp][:]
+            lc, ls = particles(kp) if key == "o" else (agg_codes[kp][:].bitcast(FP8X4), agg_scales[kp][:])
             for h in range(2):
                 if (key, kp) == ("o", 0):
-                    final[h] = psum.tile([P, K_PASS], F32, name="bank", tag="bank", bufs=6)
+                    final[h] = bank_tile([P, K_PASS], F32)
                 nc.tensor.matmul_mx(
                     out=final[h][:],
-                    lhsT=lc.bitcast(FP8X4),
+                    lhsT=lc,
                     lhsT_scale=ls,
-                    rhs=codes[key, kp, h][:].bitcast(FP8X4),
-                    rhs_scale=scales[key, kp, h][:],
+                    rhs=w_codes[key, kp, h][:].bitcast(FP8X4),
+                    rhs_scale=w_scales[key, kp, h][:],
                     start=((key, kp) == ("o", 0)),
                     stop=((key, kp) == ("a", PASSES - 1)),
                 )
 
+        def finish(n):
+            width = NF // OUT_PARTS
+            cols = slice(width * n, width * (n + 1))
+            h, first = divmod(width * n, K_PASS)
+            result = rotating([P, width], F32, "result", OUT_PARTS)
+            nc.vector.tensor_tensor(
+                out=result[:], in0=final[h][:, first : first + width], in1=out_bias[:, cols], op=ALU.add
+            )
+            nc.scalar.activation(result[:], result[:], ACT.Relu)
+            nc.sync.dma_start(out=out_rows[:, cols], in_=result[:])
+
         plan = {}
 
         def at(step, rank, fn, *args):
-            plan.setdefault(step, []).append((rank, len(plan.get(step, [])), fn, args))
+            plan.setdefault((step, rank), []).append((fn, args))
 
-        def even(n):
-            return n + n % 2
+        at(-AHEAD - 1, LOAD, load_scales)
+        at(-AHEAD - 1, LOAD, load_pair, 0)
+        at(0, FREE, spread_scales, 0)
+        at(0, MULTIPLY, spread_scales, 1)
+        at(1, MULTIPLY, turn_particles)
+        at(2, MULTIPLY, turn_bias)
+        at(2 + LAG, QUANTISE, quantise_particles)
 
         group_ready = {}
+        for j in range(N):
+            step = j + 1
+            if j % 2 == 0 and j > 0:
+                at(step - AHEAD, LOAD, load_pair, j // 2)
+            at(step, SUPPLY, widen, j)
+            at(step + LAG, TURN, turn, j)
+            at(step + LAG + 1, FREE, empty, j)
+            if j % SENDERS == SENDERS - 1:
+                at(step + 2 * LAG + 1, QUANTISE, quantise_group, j // SENDERS)
+                group_ready[j // SENDERS] = step + 2 * LAG + 2
+
         set_ready = {}
-        piece_ready = {}
-        for item in items:
-            n = starts[item]
-            turn_lag, quant_lag = (TURNP, QUANTP) if n < PRO else (TURN0, QUANT0) if n < RAMP else (TURN, QUANT)
-            if n >= AHEAD:
-                at(n - AHEAD, 0, load, item)
-            if item[0] == "r":
-                j = item[1]
-                turn_step = n + turn_lag
-                at(n, 5, widen, j)
-                at(turn_step, 8, turn, j)
-                at(turn_step + 1, 1, empty, j)
-                if j % SENDERS == SENDERS - 1:
-                    at(turn_step + 1 + quant_lag, 3, quantise_group, j // SENDERS)
-                    group_ready[j // SENDERS] = turn_step + 2 + quant_lag
-                last_turn = turn_step
+        for (key, kp, c), (step, engine) in pieces.items():
+            at(step - AHEAD, LOAD, load_piece, key, kp, c)
+            if engine in ("gpsimd", "lead"):
+                done = step + BURST
+                at(step, ADD, interleave, key, kp, c, engine)
+                at(done, FREE, quantise_piece, key, kp, c)
             else:
-                key, kp, c = item[1:4]
-                if supply[item][1] in ("g", "first"):
-                    quant_lag = WIDE
-                    at(n, 2, interleave, key, kp, c, supply[item][1])
-                    at(n + quant_lag, 1, quantise_piece, key, kp, c)
-                elif supply[item][1] == "p":
-                    quant_lag = quant_lag + WEAVE
-                    at(n, 9, weave, key, kp, c)
-                    at(n + WEAVE, 5, interleave, key, kp, c, "p")
-                    at(n + quant_lag, 3, quantise_piece, key, kp, c)
-                else:
-                    at(n, 5, interleave, key, kp, c, supply[item][1])
-                    at(n + quant_lag, 3, quantise_piece, key, kp, c)
-                if key == "r" and kp == PASSES - 1:
-                    set_ready[c] = max(set_ready[c], n + quant_lag + 1)
-                piece_ready[key, kp] = max(piece_ready.get((key, kp), 0), n + quant_lag + 1)
-                if key == "s" and kp == PASSES - 1:
-                    table_step = n + quant_lag + 1
-                    if table_step >= RAMP:
-                        table_step = table_step + (RAMP - table_step) % WIDE
-                    at(table_step, 6, table_products, c)
-                    at(table_step + 1, 1, table_copies, c)
-                    set_ready[c] = table_step
-        at(0, 1, spread_scales, 0)
-        at(0, 6, spread_scales, 1)
-        at(1, 6, turn_particles)
-        at(2, 6, bias_columns)
-        at(4, 3, lambda: nc.vector.quantize_mx(out=oc[:].bitcast(FP8X4), scales=osc[:], in_=og[:]))
-        at(last_turn, 0, lambda: nc.sync.dma_start(out=pb[:], in_=pp_b.partition_broadcast(P)))
-        units = [(q // 4, g, q) for g in range(GROUPS) for q in range(2 * SETS)]
-        slots = [(n, 0, 1) for n in range(RAMP)]
-        slots += [(n, m, WIDE) for n in range(RAMP, RAMP + len(units), WIDE) for m in range(WIDE)]
+                laid_step = step + (engine == "tensor")
+                done = laid_step + LAG
+                if engine == "tensor":
+                    at(step, WEAVE, weave, key, kp, c)
+                at(laid_step, SUPPLY, interleave, key, kp, c, engine)
+                at(done, QUANTISE, quantise_piece, key, kp, c)
+            if (key, kp) == ("s", PASSES - 1):
+                term_step = done + 1 + (RAMP - done - 1) % BURST * (done + 1 >= RAMP)
+                at(term_step, MULTIPLY, term_products, c)
+                at(term_step + 1, FREE, term_copies, c)
+                set_ready[c] = term_step
+            if (key, kp) == ("r", PASSES - 1):
+                set_ready[c] = max(set_ready[c], done + 1)
+        at(1 - AHEAD, LOAD, load_particles)
+        at(N + LAG, LOAD, load_out_bias)
+
+        units = [(g, q) for h in range(2) for g in range(GROUPS) for q in range(4 * h, 4 * h + 4)]
+        early = [(0, 4), (0, 5)]
+        units = [unit for unit in units if unit not in early]
+        units = units[: 4 * (GROUPS - 1)] + early + units[4 * (GROUPS - 1) :]
+        places = [(step, 0) for step in range(RAMP)]
+        places += [(step, m) for step in range(RAMP, RAMP + len(units), BURST) for m in range(BURST)]
         placed = []
-        for step, m, burst in slots:
-            if burst > 1 and len(units) <= TAPER and m >= burst // 2:
-                continue
-            ready = [u for u in units if max(group_ready[u[1]], set_ready[u[2] // 2]) <= step]
-            if ready:
-                settled = [u for u in ready if group_ready[u[1]] + SETTLE <= step]
-                placed.append((step, m, burst) + min(settled or ready))
-                units.remove(min(settled or ready))
+        for g, q in units:
+            ready = max(group_ready[g], set_ready[q // 2])
+            places = [place for place in places if place[0] >= ready]
+            placed.append(places.pop(0))
         last_step = placed[-1][0]
         last_sum = [0, 0]
-        for n, (step, m, burst, h, g, q) in enumerate(placed):
-            folded = step < FOLD or (step < RAMP and step % SKIP == 0)
-            at(step, 6, product, g, q, folded)
-            if burst == 1:
-                add_step, relu_step, sum_step = step + 1, step + RELU0, step + SUM0
-            else:
-                add_step = step + 1
-                relu_step = step + 1 + RELU + m
-                sum_step = step + SUM
-            sum_step = min(sum_step, max(relu_step + 1, last_step))
+        for n, ((g, q), (step, m)) in enumerate(zip(units, placed)):
+            in_ramp = step < RAMP
+            folded = in_ramp and (n < CHUNKS // SETS or step % FOLD_EVERY == 0)
+            relu_step = step + LAG if in_ramp else step + 1 + m
+            sum_step = step + 2 * LAG if in_ramp else min(step + BURST, max(relu_step + 1, last_step))
+            at(step, MULTIPLY, product, g, q, folded)
             if not folded:
-                at(add_step, 2, add_receivers, g, q)
-            at(relu_step, 4, relu_senders, g, q, folded, SENDERS // 2 if n >= len(placed) - RELU_V else RV if burst > 1 and m == burst - 1 else 0)
-            at(sum_step, 7, sum_senders, g, q)
-            last_sum[h] = max(last_sum[h], sum_step)
-        for h, gap in enumerate((AGG, 1)):
-            at(last_sum[h] + 1, 3, agg_round, h)
-            at(last_sum[h] + 1 + gap, 8, agg_turn, h)
-            at(last_sum[h] + 1 + 2 * gap, 1, agg_empty, h)
-            at(last_sum[h] + 1 + 3 * gap, 3, agg_quantise, h)
-        for kp in range(PASSES):
-            at(last_sum[1] + 1 if FINAL else last_step, 6, final_pass, "o", kp)
-        assert piece_ready["a", 0] <= last_sum[1] + 2 and piece_ready["a", 1] <= last_sum[1] + 5 and piece_ready["o", 1] <= last_step
-        at(last_sum[1] + 2, 9, final_pass, "a", 0)
-        at(last_sum[1] + 5, 6, final_pass, "a", 1)
+                at(step + 1, ADD, add_receivers, g, q)
+            at(relu_step, RELU, relu_senders, g, q, folded, SENDERS // 2 if n >= len(units) - 2 else 0)
+            at(sum_step, SUM, sum_senders, g, q)
+            last_sum[q // 4] = max(last_sum[q // 4], sum_step)
 
-        for n in sorted(plan):
-            for rank, order, fn, args in sorted(plan[n], key=lambda e: (e[0], e[1])):
+        for h, gap in enumerate((BURST, 1)):
+            at(last_sum[h] + 1, QUANTISE, agg_round, h)
+            at(last_sum[h] + 1 + gap, TURN, agg_turn, h)
+            at(last_sum[h] + 1 + 2 * gap, FREE, agg_empty, h)
+            at(last_sum[h] + 1 + 3 * gap, QUANTISE, agg_quantise, h)
+        at(last_step, MULTIPLY, final_pass, "o", 0)
+        at(last_sum[1] + 1, MULTIPLY, final_pass, "o", 1)
+        at(last_sum[1] + 2, WEAVE, final_pass, "a", 0)
+        at(last_sum[1] + 5, MULTIPLY, final_pass, "a", 1)
+        for n in range(OUT_PARTS):
+            at(last_sum[1] + 6, ADD, finish, n)
+
+        for place in sorted(plan):
+            for fn, args in plan[place]:
                 fn(*args)
-
-        width = K_PASS // CUTS
-        for n in range(2 * CUTS):
-            cols = slice(width * n, width * (n + 1))
-            first = width * (n % CUTS)
-            o1 = moving([P, width], F32, "o1", 2 * CUTS)
-            nc.vector.tensor_tensor(out=o1[:], in0=final[n // CUTS][:, first : first + width], in1=pb[:, cols], op=ALU.add)
-            nc.scalar.activation(o1[:], o1[:], ACT.Relu)
-            nc.sync.dma_start(out=out_rows[:, cols], in_=o1[:])

@@ -15,12 +15,18 @@ PIECE = 256
 SETS = NF // PIECE
 CHUNKS = NF // P
 
-AHEAD = 4
-LAG = 2
-RAMP = N + 2 * LAG
-FOLD_EVERY = 3
+ROUND = 5
+JOB = 4
+PER_BEAT = 2
 BURST = 3
-MID_GAP = 3
+AHEAD = 3
+SUM_LAG = 2
+TURN_LEAD = 2
+FRESH = 1
+FOLDED = (0, 1, 4, 5)
+SHARES = ((4, 2, 0), (6, 0, 0), (6, 0, 0))
+FAST_ROUNDS = 2
+LAY_AT = 2
 RUN = 8
 OUT_PARTS = 4
 BANKS = 6
@@ -36,19 +42,7 @@ ACT = mybir.ActivationFunctionType
 
 FLOPS = 2 * GRAPHS * N * N * NF * NF + 4 * 2 * GRAPHS * N * NF * NF
 
-LOAD, FREE, ADD, QUANTISE, RELU, SUPPLY, MULTIPLY, SUM, TURN, WEAVE = range(10)
-
-
-def piece_plan():
-    pieces = [(key, kp, c) for c in range(SETS) for key in ("i", "s", "r") for kp in range(PASSES)]
-    pieces += [(key, kp, c) for key in ("o", "a") for kp in range(PASSES) for c in range(SETS)]
-    per_set = 3 * PASSES
-    slots = [(n, "scalar" if n % 2 else "tensor") for n in range(2 * per_set)]
-    slots += [(2 * per_set + MID_GAP * n, "scalar") for n in range(per_set)]
-    slots += [(N + 1, "vector"), (RAMP + 1 - BURST, "lead"), (N + 2, "vector")]
-    for n, step in enumerate(range(RAMP, RAMP + BURST * len(pieces), BURST)):
-        slots += [(step + 1, "gpsimd")] + [(step + 2, "vector")] * (n % 2 == 0)
-    return dict(zip(pieces, slots))
+LOAD, FREE, WIDEN, SCALE, MULTIPLY, TERMS, ADD, RELU, TERM_COPIES, LAY, QUANTISE, JOBS, TURN, SUM, LAST = range(15)
 
 
 def tile_compositionalkoopmanoperators_pa_kernel(
@@ -79,29 +73,34 @@ def tile_compositionalkoopmanoperators_pa_kernel(
 
         ctx.enter_context(tc.manual_schedule())
 
-        pieces = piece_plan()
         rel_raw = {}
         w_raw = {}
 
         def load_pair(m):
-            rel_raw[m] = rotating([P, 2 * NF], U8, "rel_raw", 5)
+            rel_raw[m] = rotating([P, 2 * NF], U8, "rel_raw", 3)
             nc.sync.dma_start(out=rel_raw[m][:], in_=rel_rows[:, 2 * NF * m : 2 * NF * (m + 1)])
 
-        def load_piece(key, kp, c):
+        def piece_rows(key, kp, c):
             w, row = source[key]
             rows = slice(row + K_PASS * kp, row + K_PASS * (kp + 1))
-            w_raw[key, kp, c] = rotating([P, 4, PIECE], BF16, "w_raw", 12)
-            nc.sync.dma_start(
-                out=w_raw[key, kp, c][:], in_=w[rows, PIECE * c : PIECE * (c + 1)].rearrange("(p t) n -> p t n", t=4)
-            )
+            return w[rows, PIECE * c : PIECE * (c + 1)].rearrange("(p t) n -> p t n", t=4)
 
-        scale_rows = kept([P, NF // P], F32, "scale_rows")
+        def load_piece(piece):
+            w_raw[piece] = rotating([P, 4, PIECE], BF16, "w_raw", 5)
+            nc.sync.dma_start(out=w_raw[piece][:], in_=piece_rows(*piece))
+
+        def load_job(job):
+            w_raw[job] = rotating([P, len(job), 4, PIECE], BF16, "job_raw", 2)
+            for x, piece in enumerate(job):
+                nc.sync.dma_start(out=w_raw[job][:, x], in_=piece_rows(*piece))
+
+        scale = kept([P, PASSES, 4], F32, "scale")
         obj_sb = kept([P, NF], BF16, "obj_sb")
         bias_rows = kept([P, P // 2], F32, "bias_rows")
         out_bias = kept([P, NF], BF16, "out_bias")
 
         def load_scales():
-            nc.sync.dma_start(out=scale_rows[:], in_=rel_scale.rearrange("a b c (p e) -> p (a b c e)", p=P))
+            nc.sync.dma_start(out=scale[:], in_=rel_scale.rearrange("a b c (g p t) -> p (a b c g) t", p=P, t=4))
 
         def load_particles():
             nc.sync.dma_start(out=obj_sb[:], in_=obj_rows)
@@ -110,22 +109,11 @@ def tile_compositionalkoopmanoperators_pa_kernel(
             nc.sync.dma_start(out=out_bias[:], in_=pp_b.partition_broadcast(P))
 
         nc.vector.memset(bias_rows[:], 0.0)
-        nc.scalar.dma_start(out=bias_rows[:].bitcast(BF16)[0:CHUNKS, :], in_=rp_b.rearrange("(q p) -> q p", p=P))
         ident_bf = kept([P, P], BF16, "ident_bf")
-        nc.vector.tensor_copy(out=ident_bf[:], in_=ident[:])
+        nc.scalar.activation(ident_bf[:], ident[:], ACT.Relu)
 
-        scale = kept([P, NF], F32, "scale")
-
-        def spread_scales(half):
-            bank = bank_tile([P, 4, P], F32)
-            for e in range(4):
-                col = 4 * half + e
-                nc.tensor.transpose(bank[:, e, :], scale_rows[:, col : col + 1].to_broadcast([P, P]), ident[:])
-            copy = nc.vector.tensor_copy if half else nc.scalar.copy
-            copy(
-                out=scale[:].rearrange("m (p e) -> m p e", e=8)[:, :, 4 * half : 4 * half + 4],
-                in_=bank[:].rearrange("m e p -> m p e"),
-            )
+        def load_bias():
+            nc.sync.dma_start(out=bias_rows[:].bitcast(BF16)[0:CHUNKS, :], in_=rp_b.rearrange("(q p) -> q p", p=P))
 
         def turn_rows(rows, bank, passes):
             words = rows.bitcast(F32)
@@ -136,13 +124,16 @@ def tile_compositionalkoopmanoperators_pa_kernel(
         obj_laid = kept([P, PASSES * P * 4], BF16, "obj_laid")
         obj_codes = kept([P, PASSES * P], U32, "obj_codes")
         obj_scales = kept([P, PASSES * P], U8, "obj_scales")
+        obj_bank = {}
 
         def turn_particles():
-            bank = bank_tile([P, 4, P], F32)
-            turn_rows(obj_sb[:], bank, PASSES)
+            obj_bank[0] = bank_tile([P, 4, P], F32)
+            turn_rows(obj_sb[:], obj_bank[0], PASSES)
+
+        def empty_particles():
             nc.scalar.copy(
                 out=obj_laid[:].bitcast(F32).rearrange("p (g r u) -> p g r u", g=PASSES, u=2),
-                in_=bank[:].rearrange("p (g u) r -> p g r u", g=PASSES),
+                in_=obj_bank[0][:].rearrange("p (g u) r -> p g r u", g=PASSES),
             )
 
         def quantise_particles():
@@ -152,68 +143,60 @@ def tile_compositionalkoopmanoperators_pa_kernel(
             return obj_codes[:, P * kp : P * (kp + 1)].bitcast(FP8X4), obj_scales[:, P * kp : P * (kp + 1)]
 
         bias_cols = kept([P, CHUNKS], F32, "bias_cols")
+        bias_bank = {}
 
         def turn_bias():
-            bank = bank_tile([P, P], BF16)
-            nc.tensor.transpose(bank[:], bias_rows[:].bitcast(BF16), ident_bf[:])
-            nc.scalar.copy(out=bias_cols[:], in_=bank[:, 0:CHUNKS])
+            bias_bank[0] = bank_tile([P, P], BF16)
+            nc.tensor.transpose(bias_bank[0][:], bias_rows[:].bitcast(BF16), ident_bf[:])
 
-        w_codes = {}
-        w_scales = {}
-        for key in source:
-            for kp in range(PASSES):
-                for h in range(2):
-                    w_codes[key, kp, h] = kept([P, 2 * PIECE], U32, "codes_%s%d%d" % (key, kp, h))
-                    w_scales[key, kp, h] = kept([P, 2 * PIECE], U8, "scales_%s%d%d" % (key, kp, h))
-        woven = {}
+        def empty_bias():
+            nc.scalar.copy(out=bias_cols[:], in_=bias_bank[0][:, 0:CHUNKS])
+
         laid = {}
+        w_codes = {}
 
-        def weave(key, kp, c):
-            woven[key, kp, c] = bank_tile([P, 4 * PIECE], BF16)
-            for m in range(2):
-                nc.tensor.matmul(
-                    out=woven[key, kp, c][:, K_PASS * m : K_PASS * (m + 1)],
-                    lhsT=ident_bf[:],
-                    rhs=w_raw[key, kp, c][:, :, P * m : P * (m + 1)].rearrange("p t n -> p n t"),
-                    start=True,
-                    stop=True,
-                )
-
-        def interleave(key, kp, c, engine):
-            if engine in ("gpsimd", "lead"):
-                laid[key, kp, c] = rotating([P, 4 * PIECE], BF16, "laid_gpsimd", 1)
-            else:
-                laid[key, kp, c] = rotating([P, 4 * PIECE], BF16, "laid", 5)
-            dst, src = laid[key, kp, c][:], w_raw[key, kp, c][:]
-            if engine == "tensor":
-                nc.scalar.copy(out=dst, in_=woven[key, kp, c][:])
-            elif engine == "gpsimd":
-                nc.gpsimd.tensor_scalar(
-                    out=dst.rearrange("p (n t) -> p n t", t=4),
-                    in0=src.rearrange("p t n -> p n t"),
-                    scalar1=1.0,
-                    scalar2=0.0,
-                    op0=ALU.mult,
-                    op1=ALU.add,
-                )
-            else:
-                copy = nc.scalar.copy if engine == "scalar" else nc.vector.tensor_copy
-                copy(
-                    out=dst.rearrange("p (c i t) -> p c t i", i=RUN, t=4),
-                    in_=src.rearrange("p t (c i) -> p c t i", i=RUN),
-                )
-
-        def quantise_piece(key, kp, c):
-            cols = slice(PIECE * (c % 2), PIECE * (c % 2 + 1))
-            nc.vector.quantize_mx(
-                out=w_codes[key, kp, c // 2][:, cols].bitcast(FP8X4),
-                scales=w_scales[key, kp, c // 2][:, cols],
-                in_=laid[key, kp, c][:],
+        def interleave(batch, x, engine):
+            if x == 0:
+                laid[batch] = rotating([P, len(batch), 4 * PIECE], BF16, "laid", 2)[:]
+            copy = nc.scalar.copy if engine == "scalar" else nc.vector.tensor_copy
+            copy(
+                out=laid[batch][:, x].rearrange("p (c i t) -> p c t i", i=RUN, t=4),
+                in_=w_raw[batch[x]][:].rearrange("p t (c i) -> p c t i", i=RUN),
             )
 
+        def run_job(job):
+            whole = rotating([P, len(job), 4 * PIECE], BF16, "job_laid", 1)
+            laid[job[:4]] = whole[:, 0 : len(job[:4])]
+            if len(job) > 4:
+                laid[job[4:]] = whole[:, 4 : len(job)]
+            nc.gpsimd.tensor_scalar(
+                out=whole[:].rearrange("p x (n t) -> p x n t", t=4),
+                in0=w_raw[job][:].rearrange("p x t n -> p x n t"),
+                scalar1=1.0,
+                scalar2=0.0,
+                op0=ALU.mult,
+                op1=ALU.add,
+            )
+
+        def quantise_batch(batch):
+            name = "%s%d%d" % batch[0]
+            codes = kept([P, len(batch) * PIECE], U32, "codes_" + name)
+            scales = kept([P, len(batch) * PIECE], U8, "scales_" + name)
+            nc.vector.quantize_mx(
+                out=codes[:].bitcast(FP8X4),
+                scales=scales[:],
+                in_=laid[batch].rearrange("p x n -> p (x n)"),
+            )
+            for x, piece in enumerate(batch):
+                w_codes[piece] = (codes, scales, PIECE * x)
+
+        def piece_weights(piece, first, width):
+            codes, scales, base = w_codes[piece]
+            cols = slice(base + first, base + first + width)
+            return codes[:, cols].bitcast(FP8X4), scales[:, cols]
+
         def chunk_weights(key, kp, q):
-            cols = slice(P * (q % 4), P * (q % 4 + 1))
-            return w_codes[key, kp, q // 4][:, cols].bitcast(FP8X4), w_scales[key, kp, q // 4][:, cols]
+            return piece_weights((key, kp, q // 2), P * (q % 2), P)
 
         term_bank = {}
         recv = {}
@@ -239,12 +222,12 @@ def tile_compositionalkoopmanoperators_pa_kernel(
         def term_copies(c):
             recv[c] = kept([P, 2, P], F32, "recv%d" % c)
             send[c] = kept([P, 2, P], F32, "send%d" % c)
-            nc.scalar.copy(out=recv[c][:], in_=term_bank[c][:, 0:2, :])
             for m in range(2):
                 q = 2 * c + m
                 nc.scalar.activation(
                     send[c][:, m, :], term_bank[c][:, 2 + m, :], ACT.Identity, bias=bias_cols[:, q : q + 1]
                 )
+            nc.scalar.copy(out=recv[c][:], in_=term_bank[c][:, 0:2, :])
 
         wide = {}
         turned = {}
@@ -252,28 +235,37 @@ def tile_compositionalkoopmanoperators_pa_kernel(
         rel_codes = [kept([P, PASSES * SENDERS * P], U32, "rel_codes%d" % g) for g in range(GROUPS)]
         rel_scales = [kept([P, PASSES * SENDERS * P], U8, "rel_scales%d" % g) for g in range(GROUPS)]
 
-        def widen(j):
-            wide[j] = rotating([P, NF], BF16, "wide", 5)
+        def widen(m):
+            wide[m] = rotating([P, 2 * NF], BF16, "wide", 3)
+            nc.scalar.copy(out=wide[m][:], in_=rel_raw[m][:].bitcast(FP8))
+
+        def turn(m, kp):
+            turned[m, kp] = bank_tile([P, 2, 2, P], F32)
+            words = wide[m][:].bitcast(F32)
+            for u in range(2):
+                for s in range(2):
+                    first = K_PASS * s + 256 * kp
+                    nc.tensor.transpose(turned[m, kp][:, u, s, :], words[:, first + u : first + 256 : 2], ident[:])
+
+        def scale_out(m, kp):
+            g = m // 2
+            if (m % 2, kp) == (0, 0):
+                rel_laid[g] = rotating([P, PASSES, 2, 2 * P * 4], BF16, "rel_laid", 2)
+            values = turned[m, kp][:].rearrange("p u s r -> p (u s r)").bitcast(BF16)
+            factors = scale[:, kp, :].rearrange("p (u e) -> p u e", u=2)
             nc.vector.tensor_tensor(
-                out=wide[j][:],
-                in0=rel_raw[j // 2][:, NF * (j % 2) : NF * (j % 2 + 1)].bitcast(FP8),
-                in1=scale[:],
+                out=rel_laid[g][:, kp, m % 2, :].rearrange("p (x u e) -> p x u e", u=2, e=2),
+                in0=values.rearrange("p (u x e) -> p x u e", u=2, e=2),
+                in1=factors.unsqueeze(1).to_broadcast([P, 2 * P, 2, 2]),
                 op=ALU.mult,
             )
 
-        def turn(j):
-            turned[j] = bank_tile([P, 4, P], F32)
-            turn_rows(wide[j][:], turned[j], PASSES)
-
-        def empty(j):
-            g = j // SENDERS
-            if j % SENDERS == 0:
-                rel_laid[g] = rotating([P, PASSES * SENDERS * P * 4], BF16, "rel_laid", 2)
-            view = rel_laid[g][:].bitcast(F32).rearrange("p (g s r u) -> p g s r u", g=PASSES, s=SENDERS, u=2)
-            nc.scalar.copy(out=view[:, :, j % SENDERS], in_=turned[j][:].rearrange("p (g u) r -> p g r u", g=PASSES))
-
         def quantise_group(g):
-            nc.vector.quantize_mx(out=rel_codes[g][:].bitcast(FP8X4), scales=rel_scales[g][:], in_=rel_laid[g][:])
+            nc.vector.quantize_mx(
+                out=rel_codes[g][:].bitcast(FP8X4),
+                scales=rel_scales[g][:],
+                in_=rel_laid[g][:].rearrange("p g m x -> p (g m x)"),
+            )
 
         agg = [psum.tile([P, 4, P], F32, name="agg%d" % h, tag="agg%d" % h) for h in range(2)]
         summed = [0, 0]
@@ -380,17 +372,19 @@ def tile_compositionalkoopmanoperators_pa_kernel(
 
         def final_pass(key, kp):
             lc, ls = particles(kp) if key == "o" else (agg_codes[kp][:].bitcast(FP8X4), agg_scales[kp][:])
-            for h in range(2):
-                if (key, kp) == ("o", 0):
+            for c in range(SETS):
+                h, m = divmod(c, 2)
+                if (key, kp, m) == ("o", 0, 0):
                     final[h] = bank_tile([P, K_PASS], F32)
+                wc, ws = piece_weights((key, kp, c), 0, PIECE)
                 nc.tensor.matmul_mx(
-                    out=final[h][:],
+                    out=final[h][:, PIECE * m : PIECE * (m + 1)],
                     lhsT=lc,
                     lhsT_scale=ls,
-                    rhs=w_codes[key, kp, h][:].bitcast(FP8X4),
-                    rhs_scale=w_scales[key, kp, h][:],
-                    start=((key, kp) == ("o", 0)),
-                    stop=((key, kp) == ("a", PASSES - 1)),
+                    rhs=wc,
+                    rhs_scale=ws,
+                    start=((key, kp, m) == ("o", 0, 0)),
+                    stop=((key, kp, m) == ("a", PASSES - 1, 1)),
                 )
 
         def finish(n):
@@ -404,88 +398,136 @@ def tile_compositionalkoopmanoperators_pa_kernel(
             nc.scalar.activation(result[:], result[:], ACT.Relu)
             nc.sync.dma_start(out=out_rows[:, cols], in_=result[:])
 
+        def both_passes(key, c):
+            return tuple((key, kp, c) for kp in range(PASSES))
+
+        first_i, first_r, first_s = both_passes("i", 0), both_passes("r", 0), both_passes("s", 0)
+        load_pair(0)
+        load_scales()
+        for piece in first_r:
+            load_piece(piece)
+        load_pair(1)
+        load_particles()
+        load_bias()
+        load_pair(2)
+        load_job(first_s)
+        for piece in first_i:
+            load_piece(piece)
+        widen(0)
+        interleave(first_r, 0, "vector")
+        interleave(first_r, 1, "vector")
+        turn(0, 0)
+        turn(0, 1)
+        widen(1)
+        scale_out(0, 0)
+        quantise_batch(first_r)
+        turn(1, 0)
+        turn(1, 1)
+        turn_particles()
+        turn_bias()
+        widen(2)
+        run_job(first_s)
+        scale_out(0, 1)
+        scale_out(1, 0)
+        turn(2, 0)
+        interleave(first_i, 0, "scalar")
+        empty_particles()
+        scale_out(1, 1)
+        turn(2, 1)
+        interleave(first_i, 1, "scalar")
+        empty_bias()
+        quantise_particles()
+
         plan = {}
 
         def at(step, rank, fn, *args):
             plan.setdefault((step, rank), []).append((fn, args))
 
-        at(-AHEAD - 1, LOAD, load_scales)
-        at(-AHEAD - 1, LOAD, load_pair, 0)
-        at(0, FREE, spread_scales, 0)
-        at(0, MULTIPLY, spread_scales, 1)
-        at(1, MULTIPLY, turn_particles)
-        at(2, MULTIPLY, turn_bias)
-        at(2 + LAG, QUANTISE, quantise_particles)
+        at(-1, QUANTISE, quantise_group, 0)
+        at(-1, QUANTISE, quantise_batch, first_i)
+        at(-1, QUANTISE, quantise_batch, first_s)
+        group_ready = {0: 0}
+        banks = [(m, kp) for m in range(2, N // 2) for kp in range(PASSES)]
+        steps = []
+        for rnd in range(GROUPS):
+            count = 6 if rnd < FAST_ROUNDS else 4
+            steps += [ROUND * rnd + max(0, n - max(0, count - ROUND)) for n in range(count)]
+        for (m, kp), step in zip(banks, steps):
+            if m > 2:
+                if kp == 0:
+                    at(step - TURN_LEAD - 1 - AHEAD, LOAD, load_pair, m)
+                    at(step - TURN_LEAD - 1, WIDEN, widen, m)
+                at(step - TURN_LEAD, TURN, turn, m, kp)
+            at(step, SCALE, scale_out, m, kp)
+            if (m % 2, kp) == (1, 1):
+                end = step // ROUND * ROUND + ROUND - 1
+                at(end, QUANTISE, quantise_group, m // 2)
+                group_ready[m // 2] = end + 1
 
-        group_ready = {}
-        for j in range(N):
-            step = j + 1
-            if j % 2 == 0 and j > 0:
-                at(step - AHEAD, LOAD, load_pair, j // 2)
-            at(step, SUPPLY, widen, j)
-            at(step + LAG, TURN, turn, j)
-            at(step + LAG + 1, FREE, empty, j)
-            if j % SENDERS == SENDERS - 1:
-                at(step + 2 * LAG + 1, QUANTISE, quantise_group, j // SENDERS)
-                group_ready[j // SENDERS] = step + 2 * LAG + 2
-
+        pieces = [(key, kp, c) for c in range(1, SETS) for key in ("i", "s", "r") for kp in range(PASSES)]
+        pieces += [(key, kp, c) for key in ("o", "a") for kp in range(PASSES) for c in range(SETS)]
+        done = {piece: -1 for piece in first_i + first_r + first_s}
+        rnd = 0
+        while pieces:
+            start = ROUND * rnd
+            on_gpsimd, on_scalar, on_vector = SHARES[rnd] if rnd < len(SHARES) else (JOB, 0, 0)
+            job, pieces = tuple(pieces[:on_gpsimd]), pieces[on_gpsimd:]
+            at(start - AHEAD, LOAD, load_job, job)
+            at(start - 1, JOBS, run_job, job)
+            engines = ["scalar"] * on_scalar + ["vector"] * on_vector
+            batches = []
+            for n in range(0, len(engines), 2):
+                batch, pieces = tuple(pieces[:2]), pieces[2:]
+                for x, piece in enumerate(batch):
+                    step = start + (n + x + LAY_AT if engines[n + x] == "scalar" else ROUND - 1)
+                    at(start - AHEAD + 1, LOAD, load_piece, piece)
+                    at(step, LAY, interleave, batch, x, engines[n + x])
+                batches.append(batch)
+            for batch in batches + [job[:4], job[4:]]:
+                if batch:
+                    at(start + ROUND - 1, QUANTISE, quantise_batch, batch)
+                for piece in batch:
+                    done[piece] = start + ROUND - 1
+            rnd = rnd + 1
         set_ready = {}
-        for (key, kp, c), (step, engine) in pieces.items():
-            at(step - AHEAD, LOAD, load_piece, key, kp, c)
-            if engine in ("gpsimd", "lead"):
-                done = step + BURST
-                at(step, ADD, interleave, key, kp, c, engine)
-                at(done, FREE, quantise_piece, key, kp, c)
-            else:
-                laid_step = step + (engine == "tensor")
-                done = laid_step + LAG
-                if engine == "tensor":
-                    at(step, WEAVE, weave, key, kp, c)
-                at(laid_step, SUPPLY, interleave, key, kp, c, engine)
-                at(done, QUANTISE, quantise_piece, key, kp, c)
-            if (key, kp) == ("s", PASSES - 1):
-                term_step = done + 1 + (RAMP - done - 1) % BURST * (done + 1 >= RAMP)
-                at(term_step, MULTIPLY, term_products, c)
-                at(term_step + 1, FREE, term_copies, c)
-                set_ready[c] = term_step
-            if (key, kp) == ("r", PASSES - 1):
-                set_ready[c] = max(set_ready[c], done + 1)
-        at(1 - AHEAD, LOAD, load_particles)
-        at(N + LAG, LOAD, load_out_bias)
+        for c in range(SETS):
+            step = max(done[key, kp, c] for key in ("i", "s", "r") for kp in range(PASSES)) + 1
+            at(step, TERMS if c else FREE, term_products, c)
+            at(step, TERM_COPIES if c else WIDEN, term_copies, c)
+            set_ready[c] = step + (c > 0)
+        at(ROUND * (GROUPS - 1), LOAD, load_out_bias)
 
         units = [(g, q) for h in range(2) for g in range(GROUPS) for q in range(4 * h, 4 * h + 4)]
-        early = [(0, 4), (0, 5)]
-        units = [unit for unit in units if unit not in early]
-        units = units[: 4 * (GROUPS - 1)] + early + units[4 * (GROUPS - 1) :]
-        places = [(step, 0) for step in range(RAMP)]
-        places += [(step, m) for step in range(RAMP, RAMP + len(units), BURST) for m in range(BURST)]
+        supplied = group_ready[GROUPS - 1]
         placed = []
-        for g, q in units:
-            ready = max(group_ready[g], set_ready[q // 2])
-            places = [place for place in places if place[0] >= ready]
-            placed.append(places.pop(0))
-        last_step = placed[-1][0]
+        step = 0
+        while units:
+            ready = [(g, q) for g, q in units if max(group_ready[g], set_ready[q // 2]) <= step - FRESH]
+            ready += [(g, q) for g, q in units if step - FRESH < max(group_ready[g], set_ready[q // 2]) <= step]
+            now = ready[: PER_BEAT if step < supplied else BURST]
+            units = [unit for unit in units if unit not in now]
+            placed += [(step, unit) for unit in now]
+            step = step + 1
+        last_step = step - 1
         last_sum = [0, 0]
-        for n, ((g, q), (step, m)) in enumerate(zip(units, placed)):
-            in_ramp = step < RAMP
-            folded = in_ramp and (n < CHUNKS // SETS or step % FOLD_EVERY == 0)
-            relu_step = step + LAG if in_ramp else step + 1 + m
-            sum_step = step + 2 * LAG if in_ramp else min(step + BURST, max(relu_step + 1, last_step))
+        for n, (step, (g, q)) in enumerate(placed):
+            folded = n in FOLDED
+            sum_step = step + (SUM_LAG if step < supplied else 2)
             at(step, MULTIPLY, product, g, q, folded)
             if not folded:
-                at(step + 1, ADD, add_receivers, g, q)
-            at(relu_step, RELU, relu_senders, g, q, folded, SENDERS // 2 if n >= len(units) - 2 else 0)
+                at(step, ADD, add_receivers, g, q)
+            at(step + 1, RELU, relu_senders, g, q, folded, SENDERS // 2 if n >= len(placed) - 2 else 0)
             at(sum_step, SUM, sum_senders, g, q)
             last_sum[q // 4] = max(last_sum[q // 4], sum_step)
 
-        for h, gap in enumerate((BURST, 1)):
-            at(last_sum[h] + 1, QUANTISE, agg_round, h)
-            at(last_sum[h] + 1 + gap, TURN, agg_turn, h)
-            at(last_sum[h] + 1 + 2 * gap, FREE, agg_empty, h)
-            at(last_sum[h] + 1 + 3 * gap, QUANTISE, agg_quantise, h)
-        at(last_step, MULTIPLY, final_pass, "o", 0)
+        for h in range(2):
+            at(last_sum[h] + 1, SCALE, agg_round, h)
+            at(last_sum[h] + 2, TURN, agg_turn, h)
+            at(last_sum[h] + 3, WIDEN, agg_empty, h)
+            at(last_sum[h] + 4, QUANTISE, agg_quantise, h)
+        at(last_step + 1, MULTIPLY, final_pass, "o", 0)
         at(last_sum[1] + 1, MULTIPLY, final_pass, "o", 1)
-        at(last_sum[1] + 2, WEAVE, final_pass, "a", 0)
+        at(max(last_sum[1] + 2, last_sum[0] + 4), LAST, final_pass, "a", 0)
         at(last_sum[1] + 5, MULTIPLY, final_pass, "a", 1)
         for n in range(OUT_PARTS):
             at(last_sum[1] + 6, ADD, finish, n)

@@ -19,14 +19,23 @@ ROUND = 5
 JOB = 4
 PER_BEAT = 2
 BURST = 3
-AHEAD = 3
+AHEAD = 2
 SUM_LAG = 2
-TURN_LEAD = 2
+TURN_LEAD = 1
+EARLY = 2
+EDGE = 1
+TURN_FIRST = 5
+JOB_AHEAD = 4
+EAGER = 5
+SPARE = 1
+PAIRED = 0
+SHARED = 0
+LATE = 2
 FRESH = 1
 FOLDED = (0, 1, 4, 5)
 SHARES = ((4, 2, 0), (6, 0, 0), (6, 0, 0))
-FAST_ROUNDS = 2
-LAY_AT = 2
+EXITS = (6, 6)
+LAY_AT = 1
 RUN = 8
 OUT_PARTS = 4
 BANKS = 6
@@ -42,7 +51,7 @@ ACT = mybir.ActivationFunctionType
 
 FLOPS = 2 * GRAPHS * N * N * NF * NF + 4 * 2 * GRAPHS * N * NF * NF
 
-LOAD, FREE, WIDEN, SCALE, MULTIPLY, TERMS, ADD, RELU, TERM_COPIES, LAY, QUANTISE, JOBS, TURN, SUM, LAST = range(15)
+LOAD, FREE, WIDEN, SCALE, MULTIPLY, TERMS, ADD, PAIR, LAY, RELU, TERM_COPIES, QUANTISE, JOBS, TURN, SUM, LAST = range(16)
 
 
 def tile_compositionalkoopmanoperators_pa_kernel(
@@ -77,7 +86,7 @@ def tile_compositionalkoopmanoperators_pa_kernel(
         w_raw = {}
 
         def load_pair(m):
-            rel_raw[m] = rotating([P, 2 * NF], U8, "rel_raw", 3)
+            rel_raw[m] = rotating([P, 2 * NF], U8, "rel_raw", 4)
             nc.sync.dma_start(out=rel_raw[m][:], in_=rel_rows[:, 2 * NF * m : 2 * NF * (m + 1)])
 
         def piece_rows(key, kp, c):
@@ -330,18 +339,23 @@ def tile_compositionalkoopmanoperators_pa_kernel(
                     else:
                         nc.scalar.activation(eff[g, q][:, s, cols], src[:, s, cols], ACT.Relu, bias=bias)
 
-        def sum_senders(g, q):
+        def pair_senders(g, q):
+            nc.vector.tensor_tensor(
+                out=eff[g, q][:, 0:2, :], in0=eff[g, q][:, 0:2, :], in1=eff[g, q][:, 2:4, :], op=ALU.add
+            )
+
+        def sum_senders(g, q, terms):
             h = q // 4
-            for s in range(SENDERS):
+            for s in range(terms):
                 nc.tensor.matmul(
                     out=agg[h][:, q % 4, :],
                     lhsT=eff[g, q][:, s, :],
                     rhs=ident[:],
                     is_transpose=True,
                     start=(summed[h] == 0),
-                    stop=(summed[h] == 4 * N - 1),
+                    stop=(summed[h] == 4 * N - SENDERS // terms),
                 )
-                summed[h] = summed[h] + 1
+                summed[h] = summed[h] + SENDERS // terms
 
         agg_rows = {}
         agg_bank = {}
@@ -409,10 +423,10 @@ def tile_compositionalkoopmanoperators_pa_kernel(
         load_pair(1)
         load_particles()
         load_bias()
-        load_pair(2)
         load_job(first_s)
         for piece in first_i:
             load_piece(piece)
+        load_pair(2)
         widen(0)
         interleave(first_r, 0, "vector")
         interleave(first_r, 1, "vector")
@@ -422,20 +436,20 @@ def tile_compositionalkoopmanoperators_pa_kernel(
         scale_out(0, 0)
         quantise_batch(first_r)
         turn(1, 0)
-        turn(1, 1)
         turn_particles()
+        turn(1, 1)
         turn_bias()
-        widen(2)
         run_job(first_s)
         scale_out(0, 1)
         scale_out(1, 0)
-        turn(2, 0)
-        interleave(first_i, 0, "scalar")
         empty_particles()
+        interleave(first_i, 0, "scalar")
         scale_out(1, 1)
-        turn(2, 1)
         interleave(first_i, 1, "scalar")
         empty_bias()
+        widen(2)
+        turn(2, 0)
+        turn(2, 1)
         quantise_particles()
 
         plan = {}
@@ -450,14 +464,15 @@ def tile_compositionalkoopmanoperators_pa_kernel(
         banks = [(m, kp) for m in range(2, N // 2) for kp in range(PASSES)]
         steps = []
         for rnd in range(GROUPS):
-            count = 6 if rnd < FAST_ROUNDS else 4
+            count = EXITS[rnd] if rnd < len(EXITS) else 4
             steps += [ROUND * rnd + max(0, n - max(0, count - ROUND)) for n in range(count)]
         for (m, kp), step in zip(banks, steps):
+            lead = TURN_LEAD + (EARLY if step < ROUND else EDGE if step == ROUND else 0)
             if m > 2:
                 if kp == 0:
-                    at(step - TURN_LEAD - 1 - AHEAD, LOAD, load_pair, m)
-                    at(step - TURN_LEAD - 1, WIDEN, widen, m)
-                at(step - TURN_LEAD, TURN, turn, m, kp)
+                    at(step - lead - 1 - AHEAD, LOAD, load_pair, m)
+                    at(step - lead - 1, WIDEN, widen, m)
+                at(step - lead, FREE if 0 < step - lead < TURN_FIRST else TURN, turn, m, kp)
             at(step, SCALE, scale_out, m, kp)
             if (m % 2, kp) == (1, 1):
                 end = step // ROUND * ROUND + ROUND - 1
@@ -472,23 +487,25 @@ def tile_compositionalkoopmanoperators_pa_kernel(
             start = ROUND * rnd
             on_gpsimd, on_scalar, on_vector = SHARES[rnd] if rnd < len(SHARES) else (JOB, 0, 0)
             job, pieces = tuple(pieces[:on_gpsimd]), pieces[on_gpsimd:]
-            at(start - AHEAD, LOAD, load_job, job)
+            at(start - JOB_AHEAD, LOAD, load_job, job)
             at(start - 1, JOBS, run_job, job)
             engines = ["scalar"] * on_scalar + ["vector"] * on_vector
             batches = []
             for n in range(0, len(engines), 2):
-                batch, pieces = tuple(pieces[:2]), pieces[2:]
+                size = len(engines[n : n + 2])
+                batch, pieces = tuple(pieces[:size]), pieces[size:]
                 for x, piece in enumerate(batch):
-                    step = start + (n + x + LAY_AT if engines[n + x] == "scalar" else ROUND - 1)
+                    step = start + (LAY_AT if engines[n + x] == "scalar" else ROUND - 1)
                     at(start - AHEAD + 1, LOAD, load_piece, piece)
                     at(step, LAY, interleave, batch, x, engines[n + x])
                 batches.append(batch)
             for batch in batches + [job[:4], job[4:]]:
-                if batch:
+                if batch and pieces:
                     at(start + ROUND - 1, QUANTISE, quantise_batch, batch)
                 for piece in batch:
                     done[piece] = start + ROUND - 1
             rnd = rnd + 1
+        last_job = job
         set_ready = {}
         for c in range(SETS):
             step = max(done[key, kp, c] for key in ("i", "s", "r") for kp in range(PASSES)) + 1
@@ -504,7 +521,8 @@ def tile_compositionalkoopmanoperators_pa_kernel(
         while units:
             ready = [(g, q) for g, q in units if max(group_ready[g], set_ready[q // 2]) <= step - FRESH]
             ready += [(g, q) for g, q in units if step - FRESH < max(group_ready[g], set_ready[q // 2]) <= step]
-            now = ready[: PER_BEAT if step < supplied else BURST]
+            spread = (len(ready) + EAGER) // (ROUND - step % ROUND + SPARE)
+            now = ready[: min(PER_BEAT, spread) if step < supplied else BURST]
             units = [unit for unit in units if unit not in now]
             placed += [(step, unit) for unit in now]
             step = step + 1
@@ -516,19 +534,29 @@ def tile_compositionalkoopmanoperators_pa_kernel(
             at(step, MULTIPLY, product, g, q, folded)
             if not folded:
                 at(step, ADD, add_receivers, g, q)
-            at(step + 1, RELU, relu_senders, g, q, folded, SENDERS // 2 if n >= len(placed) - 2 else 0)
-            at(sum_step, SUM, sum_senders, g, q)
+            late = supplied + LATE <= step and n < len(placed) - 2
+            paired = late and n % 4 < PAIRED
+            shared = SENDERS // 2 if n >= len(placed) - 2 else 1 if late and n % 4 < SHARED else 0
+            at(step + 1, SCALE if shared else RELU, relu_senders, g, q, folded, shared)
+            if paired:
+                at(sum_step, PAIR, pair_senders, g, q)
+            at(sum_step, SUM, sum_senders, g, q, 2 if paired else SENDERS)
             last_sum[q // 4] = max(last_sum[q // 4], sum_step)
 
-        for h in range(2):
-            at(last_sum[h] + 1, SCALE, agg_round, h)
-            at(last_sum[h] + 2, TURN, agg_turn, h)
-            at(last_sum[h] + 3, WIDEN, agg_empty, h)
-            at(last_sum[h] + 4, QUANTISE, agg_quantise, h)
+        end = last_sum[1]
+        at(last_sum[0] + 1, SCALE, agg_round, 0)
+        at(end, QUANTISE, quantise_batch, last_job)
+        at(end + 1, SCALE, agg_round, 1)
+        at(end + 1, FREE, agg_turn, 0)
         at(last_step + 1, MULTIPLY, final_pass, "o", 0)
-        at(last_sum[1] + 1, MULTIPLY, final_pass, "o", 1)
-        at(max(last_sum[1] + 2, last_sum[0] + 4), LAST, final_pass, "a", 0)
-        at(last_sum[1] + 5, MULTIPLY, final_pass, "a", 1)
+        at(end + 1, MULTIPLY, final_pass, "o", 1)
+        at(end + 1, RELU, agg_empty, 0)
+        at(end + 1, QUANTISE, agg_quantise, 0)
+        at(end + 2, FREE, agg_turn, 1)
+        at(end + 2, MULTIPLY, final_pass, "a", 0)
+        at(end + 3, WIDEN, agg_empty, 1)
+        at(end + 4, QUANTISE, agg_quantise, 1)
+        at(end + 5, MULTIPLY, final_pass, "a", 1)
         for n in range(OUT_PARTS):
             at(last_sum[1] + 6, ADD, finish, n)
 

@@ -26,16 +26,19 @@ EARLY = 2
 EDGE = 1
 TURN_FIRST = 5
 JOB_AHEAD = 4
-EAGER = 5
-SPARE = 1
-PAIRED = 0
+FIRST_BEATS = (1, 1, 0, 0, 0, 1, 1, 1, 1, 2)
+PAIRED = 2
+PAIR_FROM = 10
 SHARED = 0
 LATE = 2
 FRESH = 1
-FOLDED = (0, 1, 4, 5)
-SHARES = ((4, 2, 0), (6, 0, 0), (6, 0, 0))
+FOLDED = (0, 1, 6, 7)
+SHARES = ((4, 2, 0), (4, 2, 0), (4, 2, 0), (4, 0, 0), (2, 0, 0), (2, 0, 0))
 EXITS = (6, 6)
-LAY_AT = 1
+HELPED = {1: 1, 2: 1, 3: 1, 4: 2, 5: 2}
+LATE_ROUND = 3
+TERMS_LATE = 2
+LAY_AT = 0
 RUN = 8
 OUT_PARTS = 4
 BANKS = 6
@@ -269,6 +272,26 @@ def tile_compositionalkoopmanoperators_pa_kernel(
                 op=ALU.mult,
             )
 
+        plain = {}
+
+        def copy_out(m, kp, count):
+            if (m % 2, kp) == (0, 0):
+                rel_laid[m // 2] = rotating([P, PASSES, 2, 2 * P * 4], BF16, "rel_laid", 2)
+            if kp == 0:
+                plain[m] = rotating([P, count, 2 * P * 4], BF16, "plain", 1)
+            nc.vector.tensor_copy(
+                out=plain[m][:, kp, :].bitcast(F32).rearrange("p (x u) -> p x u", u=2),
+                in_=turned[m, kp][:].rearrange("p u s r -> p (s r) u"),
+            )
+
+        def scale_plain(m, count):
+            nc.gpsimd.tensor_tensor(
+                out=rel_laid[m // 2][:, 0:count, m % 2, :].rearrange("p g (x t) -> p g x t", t=4),
+                in0=plain[m][:].rearrange("p g (x t) -> p g x t", t=4),
+                in1=scale[:, 0:count, :].unsqueeze(2).to_broadcast([P, count, 2 * P, 4]),
+                op=ALU.mult,
+            )
+
         def quantise_group(g):
             nc.vector.quantize_mx(
                 out=rel_codes[g][:].bitcast(FP8X4),
@@ -473,7 +496,13 @@ def tile_compositionalkoopmanoperators_pa_kernel(
                     at(step - lead - 1 - AHEAD, LOAD, load_pair, m)
                     at(step - lead - 1, WIDEN, widen, m)
                 at(step - lead, FREE if 0 < step - lead < TURN_FIRST else TURN, turn, m, kp)
-            at(step, SCALE, scale_out, m, kp)
+            count = HELPED.get(step // ROUND, 0) if m % 2 == 0 else 0
+            if kp < count:
+                at(step, SCALE, copy_out, m, kp, count)
+                if kp == count - 1:
+                    at(step, JOBS, scale_plain, m, count)
+            else:
+                at(step, SCALE, scale_out, m, kp)
             if (m % 2, kp) == (1, 1):
                 end = step // ROUND * ROUND + ROUND - 1
                 at(end, QUANTISE, quantise_group, m // 2)
@@ -483,8 +512,10 @@ def tile_compositionalkoopmanoperators_pa_kernel(
         pieces += [(key, kp, c) for key in ("o", "a") for kp in range(PASSES) for c in range(SETS)]
         done = {piece: -1 for piece in first_i + first_r + first_s}
         rnd = 0
+        start = 0
+        supplied = group_ready[GROUPS - 1]
         while pieces:
-            start = ROUND * rnd
+            length = ROUND if start < supplied else LATE_ROUND
             on_gpsimd, on_scalar, on_vector = SHARES[rnd] if rnd < len(SHARES) else (JOB, 0, 0)
             job, pieces = tuple(pieces[:on_gpsimd]), pieces[on_gpsimd:]
             at(start - JOB_AHEAD, LOAD, load_job, job)
@@ -501,28 +532,27 @@ def tile_compositionalkoopmanoperators_pa_kernel(
                 batches.append(batch)
             for batch in batches + [job[:4], job[4:]]:
                 if batch and pieces:
-                    at(start + ROUND - 1, QUANTISE, quantise_batch, batch)
+                    at(start + length - 1, QUANTISE, quantise_batch, batch)
                 for piece in batch:
-                    done[piece] = start + ROUND - 1
+                    done[piece] = start + length - 1
             rnd = rnd + 1
+            start = start + length
         last_job = job
         set_ready = {}
         for c in range(SETS):
-            step = max(done[key, kp, c] for key in ("i", "s", "r") for kp in range(PASSES)) + 1
+            step = max(done[key, kp, c] for key in ("i", "s", "r") for kp in range(PASSES)) + 1 + (c >= TERMS_LATE)
             at(step, TERMS if c else FREE, term_products, c)
             at(step, TERM_COPIES if c else WIDEN, term_copies, c)
             set_ready[c] = step + (c > 0)
         at(ROUND * (GROUPS - 1), LOAD, load_out_bias)
 
         units = [(g, q) for h in range(2) for g in range(GROUPS) for q in range(4 * h, 4 * h + 4)]
-        supplied = group_ready[GROUPS - 1]
         placed = []
         step = 0
         while units:
             ready = [(g, q) for g, q in units if max(group_ready[g], set_ready[q // 2]) <= step - FRESH]
             ready += [(g, q) for g, q in units if step - FRESH < max(group_ready[g], set_ready[q // 2]) <= step]
-            spread = (len(ready) + EAGER) // (ROUND - step % ROUND + SPARE)
-            now = ready[: min(PER_BEAT, spread) if step < supplied else BURST]
+            now = ready[: FIRST_BEATS[step] if step < len(FIRST_BEATS) else PER_BEAT if step < supplied else BURST]
             units = [unit for unit in units if unit not in now]
             placed += [(step, unit) for unit in now]
             step = step + 1
@@ -535,11 +565,14 @@ def tile_compositionalkoopmanoperators_pa_kernel(
             if not folded:
                 at(step, ADD, add_receivers, g, q)
             late = supplied + LATE <= step and n < len(placed) - 2
-            paired = late and n % 4 < PAIRED
-            shared = SENDERS // 2 if n >= len(placed) - 2 else 1 if late and n % 4 < SHARED else 0
-            at(step + 1, SCALE if shared else RELU, relu_senders, g, q, folded, shared)
+            beat = step % ROUND
+            paired = PAIR_FROM <= step < supplied and (beat == 2 or (beat == 1 and n % 2 < PAIRED - 2)) and PAIRED > 0
             if paired:
-                at(sum_step, PAIR, pair_senders, g, q)
+                sum_step = step - beat + ROUND - 1
+            shared = SENDERS // 2 if n >= len(placed) - 2 else 1 if late and n % 4 < SHARED else 0
+            at(step + 1, RELU, relu_senders, g, q, folded, shared)
+            if paired:
+                at(sum_step, SCALE, pair_senders, g, q)
             at(sum_step, SUM, sum_senders, g, q, 2 if paired else SENDERS)
             last_sum[q // 4] = max(last_sum[q // 4], sum_step)
 

@@ -17,7 +17,7 @@ CHUNKS = NF // P
 
 ROUND = 5
 JOB = 4
-PER_BEAT = 2
+STEADY = (2, 2, 2, 2, 2)
 BURST = 3
 AHEAD = 2
 SUM_LAG = 2
@@ -25,22 +25,30 @@ TURN_LEAD = 1
 EARLY = 2
 EDGE = 1
 TURN_FIRST = 5
+TURN_FROM = 1
+FIRST_COPIES = 0
 JOB_AHEAD = 4
 FIRST_BEATS = (1, 1, 0, 0, 0, 1, 1, 1, 1, 2)
-PAIRED = 2
-PAIR_FROM = 10
+PAIRED = 0
+PAIR_FROM = 20
+PAIR_BACK = 4
 SHARED = 0
 LATE = 2
 FRESH = 1
-FOLDED = (0, 1, 6, 7)
+FOLDED = (0, 1, 7)
 SHARES = ((4, 2, 0), (4, 2, 0), (4, 2, 0), (4, 0, 0), (2, 0, 0), (2, 0, 0))
 EXITS = (6, 6)
 HELPED = {1: 1, 2: 1, 3: 1, 4: 2, 5: 2}
 LATE_ROUND = 3
+APART = (11, 13, 15)
+COPY_FROM = 10
+ON_SCALAR = ()
 TERMS_LATE = 2
+FIRST_TERMS = 0
+SLOW = 1
 LAY_AT = 0
 RUN = 8
-OUT_PARTS = 4
+OUT_WIDTHS = (256, 256, 256, 256)
 BANKS = 6
 
 F32 = mybir.dt.float32
@@ -167,17 +175,38 @@ def tile_compositionalkoopmanoperators_pa_kernel(
         laid = {}
         w_codes = {}
 
-        def interleave(batch, x, engine):
+        def laid_tile(count, shared):
+            if shared:
+                return rotating([P, count, 4 * PIECE], BF16, "job_laid", 1)
+            return rotating([P, count, 4 * PIECE], BF16, "laid", 2)
+
+        def interleave(batch, x, engine, shared=False):
             if x == 0:
-                laid[batch] = rotating([P, len(batch), 4 * PIECE], BF16, "laid", 2)[:]
+                laid[batch] = laid_tile(len(batch), shared)[:]
             copy = nc.scalar.copy if engine == "scalar" else nc.vector.tensor_copy
             copy(
                 out=laid[batch][:, x].rearrange("p (c i t) -> p c t i", i=RUN, t=4),
                 in_=w_raw[batch[x]][:].rearrange("p t (c i) -> p c t i", i=RUN),
             )
 
-        def run_job(job):
-            whole = rotating([P, len(job), 4 * PIECE], BF16, "job_laid", 1)
+        woven = {}
+
+        def weave(piece):
+            woven[piece] = bank_tile([P, 4 * PIECE], BF16)
+            for m in range(2):
+                nc.tensor.matmul(
+                    out=woven[piece][:, K_PASS * m : K_PASS * (m + 1)],
+                    lhsT=ident_bf[:],
+                    rhs=w_raw[piece][:, :, P * m : P * (m + 1)].rearrange("p t n -> p n t"),
+                    start=True,
+                    stop=True,
+                )
+
+        def empty_woven(batch, x):
+            nc.scalar.copy(out=laid[batch][:, x], in_=woven[batch[x]][:])
+
+        def run_job(job, shared=True):
+            whole = laid_tile(len(job), shared)
             laid[job[:4]] = whole[:, 0 : len(job[:4])]
             if len(job) > 4:
                 laid[job[4:]] = whole[:, 4 : len(job)]
@@ -251,13 +280,51 @@ def tile_compositionalkoopmanoperators_pa_kernel(
             wide[m] = rotating([P, 2 * NF], BF16, "wide", 3)
             nc.scalar.copy(out=wide[m][:], in_=rel_raw[m][:].bitcast(FP8))
 
+        halves = {}
+
+        def load_half(kp):
+            halves[kp] = kept([P, 2, K_PASS], U8, "rel_half%d" % kp)
+            nc.sync.dma_start(
+                out=halves[kp][:],
+                in_=rel_rows[:, 0 : 2 * NF].rearrange("p (s g k) -> p g s k", s=2, g=PASSES)[:, kp],
+            )
+
+        def widen_half(kp):
+            wide[0, kp] = kept([P, 2 * K_PASS], BF16, "wide_half%d" % kp)
+            nc.scalar.copy(out=wide[0, kp][:], in_=halves[kp][:].rearrange("p s k -> p (s k)").bitcast(FP8))
+
+        def turn_half(kp):
+            turned[0, kp] = bank_tile([P, 2, 2, P], F32)
+            words = wide[0, kp][:].bitcast(F32)
+            for u in range(2):
+                for s in range(2):
+                    nc.tensor.transpose(turned[0, kp][:, u, s, :], words[:, 256 * s + u : 256 * (s + 1) : 2], ident[:])
+
+        ones = kept([P, 1], F32, "ones")
+        nc.vector.memset(ones[:], 1.0)
+
+        def widen_apart(m):
+            wide[m] = rotating([P, 2 * NF], BF16, "wide", 3)
+            nc.vector.tensor_scalar(
+                out=wide[m][:].rearrange("q (u x e) -> q x u e", u=2, e=2),
+                in0=rel_raw[m][:].bitcast(FP8).rearrange("q (x u e) -> q x u e", u=2, e=2),
+                scalar1=ones[:],
+                scalar2=None,
+                op0=ALU.mult,
+            )
+
         def turn(m, kp):
             turned[m, kp] = bank_tile([P, 2, 2, P], F32)
             words = wide[m][:].bitcast(F32)
             for u in range(2):
                 for s in range(2):
-                    first = K_PASS * s + 256 * kp
-                    nc.tensor.transpose(turned[m, kp][:, u, s, :], words[:, first + u : first + 256 : 2], ident[:])
+                    if m in APART:
+                        first = K_PASS * u + P * (2 * s + kp)
+                        rows = words[:, first : first + P]
+                    else:
+                        first = K_PASS * s + 256 * kp
+                        rows = words[:, first + u : first + 256 : 2]
+                    nc.tensor.transpose(turned[m, kp][:, u, s, :], rows, ident[:])
 
         def scale_out(m, kp):
             g = m // 2
@@ -274,12 +341,13 @@ def tile_compositionalkoopmanoperators_pa_kernel(
 
         plain = {}
 
-        def copy_out(m, kp, count):
+        def copy_out(m, kp, count, on_scalar):
             if (m % 2, kp) == (0, 0):
                 rel_laid[m // 2] = rotating([P, PASSES, 2, 2 * P * 4], BF16, "rel_laid", 2)
             if kp == 0:
                 plain[m] = rotating([P, count, 2 * P * 4], BF16, "plain", 1)
-            nc.vector.tensor_copy(
+            copy = nc.scalar.copy if on_scalar else nc.vector.tensor_copy
+            copy(
                 out=plain[m][:, kp, :].bitcast(F32).rearrange("p (x u) -> p x u", u=2),
                 in_=turned[m, kp][:].rearrange("p u s r -> p (s r) u"),
             )
@@ -290,6 +358,21 @@ def tile_compositionalkoopmanoperators_pa_kernel(
                 in0=plain[m][:].rearrange("p g (x t) -> p g x t", t=4),
                 in1=scale[:, 0:count, :].unsqueeze(2).to_broadcast([P, count, 2 * P, 4]),
                 op=ALU.mult,
+            )
+
+        def scale_on_scalar(m, kp):
+            if (m % 2, kp) == (0, 0):
+                rel_laid[m // 2] = rotating([P, PASSES, 2, 2 * P * 4], BF16, "rel_laid", 2)
+            planes = rotating([P, 4, 2 * P], BF16, "planes", 1)
+            values = turned[m, kp][:].rearrange("p u s r -> p (u s r)").bitcast(BF16)
+            values = values.rearrange("p (u x e) -> p u e x", u=2, e=2)
+            for t in range(4):
+                nc.scalar.activation(
+                    planes[:, t, :], values[:, t // 2, t % 2, :], ACT.Copy, scale=scale[:, kp, t : t + 1]
+                )
+            nc.scalar.copy(
+                out=rel_laid[m // 2][:, kp, m % 2, :].rearrange("p (c i t) -> p c t i", i=RUN, t=4),
+                in_=planes[:].rearrange("p t (c i) -> p c t i", i=RUN),
             )
 
         def quantise_group(g):
@@ -425,10 +508,11 @@ def tile_compositionalkoopmanoperators_pa_kernel(
                 )
 
         def finish(n):
-            width = NF // OUT_PARTS
-            cols = slice(width * n, width * (n + 1))
-            h, first = divmod(width * n, K_PASS)
-            result = rotating([P, width], F32, "result", OUT_PARTS)
+            width = OUT_WIDTHS[n]
+            left = sum(OUT_WIDTHS[:n])
+            cols = slice(left, left + width)
+            h, first = divmod(left, K_PASS)
+            result = kept([P, width], F32, "result%d" % n)
             nc.vector.tensor_tensor(
                 out=result[:], in0=final[h][:, first : first + width], in1=out_bias[:, cols], op=ALU.add
             )
@@ -445,8 +529,8 @@ def tile_compositionalkoopmanoperators_pa_kernel(
             load_piece(piece)
         load_pair(1)
         load_particles()
-        load_bias()
         load_job(first_s)
+        load_bias()
         for piece in first_i:
             load_piece(piece)
         load_pair(2)
@@ -462,49 +546,61 @@ def tile_compositionalkoopmanoperators_pa_kernel(
         turn_particles()
         turn(1, 1)
         turn_bias()
-        run_job(first_s)
+        run_job(first_s, False)
         scale_out(0, 1)
         scale_out(1, 0)
         empty_particles()
-        interleave(first_i, 0, "scalar")
+        interleave(first_i, 0, "scalar", True)
         scale_out(1, 1)
-        interleave(first_i, 1, "scalar")
+        interleave(first_i, 1, "scalar", True)
         empty_bias()
         widen(2)
         turn(2, 0)
         turn(2, 1)
         quantise_particles()
+        quantise_group(0)
+        quantise_batch(first_s)
+        quantise_batch(first_i)
 
         plan = {}
 
         def at(step, rank, fn, *args):
             plan.setdefault((step, rank), []).append((fn, args))
 
-        at(-1, QUANTISE, quantise_group, 0)
-        at(-1, QUANTISE, quantise_batch, first_i)
-        at(-1, QUANTISE, quantise_batch, first_s)
+        lengths = [ROUND] * len(EXITS) + [len(STEADY)] * GROUPS
+        starts = [sum(lengths[:rnd]) for rnd in range(len(lengths))]
+
+        def round_of(step):
+            return max(rnd for rnd, start in enumerate(starts) if start <= step)
+
         group_ready = {0: 0}
         banks = [(m, kp) for m in range(2, N // 2) for kp in range(PASSES)]
         steps = []
         for rnd in range(GROUPS):
             count = EXITS[rnd] if rnd < len(EXITS) else 4
-            steps += [ROUND * rnd + max(0, n - max(0, count - ROUND)) for n in range(count)]
+            steps += [starts[rnd] + max(0, n - max(0, count - ROUND)) for n in range(count)]
         for (m, kp), step in zip(banks, steps):
             lead = TURN_LEAD + (EARLY if step < ROUND else EDGE if step == ROUND else 0)
             if m > 2:
-                if kp == 0:
+                if kp == 0 and m in APART:
+                    before = starts[round_of(step)] - 1
+                    at(before - AHEAD, LOAD, load_pair, m)
+                    at(before, PAIR, widen_apart, m)
+                elif kp == 0:
                     at(step - lead - 1 - AHEAD, LOAD, load_pair, m)
                     at(step - lead - 1, WIDEN, widen, m)
-                at(step - lead, FREE if 0 < step - lead < TURN_FIRST else TURN, turn, m, kp)
-            count = HELPED.get(step // ROUND, 0) if m % 2 == 0 else 0
+                at(step - lead, FREE if TURN_FROM <= step - lead < TURN_FIRST else TURN, turn, m, kp)
+            count = HELPED.get(round_of(step), 0) if m % 2 == 0 else 0
             if kp < count:
-                at(step, SCALE, copy_out, m, kp, count)
+                at(step, SCALE, copy_out, m, kp, count, step >= COPY_FROM)
                 if kp == count - 1:
                     at(step, JOBS, scale_plain, m, count)
+            elif step in ON_SCALAR and (kp == 0 or step % ROUND > 0):
+                at(step, LAY, scale_on_scalar, m, kp)
             else:
                 at(step, SCALE, scale_out, m, kp)
             if (m % 2, kp) == (1, 1):
-                end = step // ROUND * ROUND + ROUND - 1
+                end = starts[round_of(step) + 1] - 1
                 at(end, QUANTISE, quantise_group, m // 2)
                 group_ready[m // 2] = end + 1
 
@@ -515,7 +611,7 @@ def tile_compositionalkoopmanoperators_pa_kernel(
         start = 0
         supplied = group_ready[GROUPS - 1]
         while pieces:
-            length = ROUND if start < supplied else LATE_ROUND
+            length = lengths[rnd] if start < supplied else LATE_ROUND
             on_gpsimd, on_scalar, on_vector = SHARES[rnd] if rnd < len(SHARES) else (JOB, 0, 0)
             job, pieces = tuple(pieces[:on_gpsimd]), pieces[on_gpsimd:]
             at(start - JOB_AHEAD, LOAD, load_job, job)
@@ -541,10 +637,10 @@ def tile_compositionalkoopmanoperators_pa_kernel(
         set_ready = {}
         for c in range(SETS):
             step = max(done[key, kp, c] for key in ("i", "s", "r") for kp in range(PASSES)) + 1 + (c >= TERMS_LATE)
-            at(step, TERMS if c else FREE, term_products, c)
-            at(step, TERM_COPIES if c else WIDEN, term_copies, c)
+            at(step if c else -FIRST_TERMS, TERMS, term_products, c)
+            at(step if c else -FIRST_COPIES, TERM_COPIES, term_copies, c)
             set_ready[c] = step + (c > 0)
-        at(ROUND * (GROUPS - 1), LOAD, load_out_bias)
+        at(supplied, LOAD, load_out_bias)
 
         units = [(g, q) for h in range(2) for g in range(GROUPS) for q in range(4 * h, 4 * h + 4)]
         placed = []
@@ -552,25 +648,26 @@ def tile_compositionalkoopmanoperators_pa_kernel(
         while units:
             ready = [(g, q) for g, q in units if max(group_ready[g], set_ready[q // 2]) <= step - FRESH]
             ready += [(g, q) for g, q in units if step - FRESH < max(group_ready[g], set_ready[q // 2]) <= step]
-            now = ready[: FIRST_BEATS[step] if step < len(FIRST_BEATS) else PER_BEAT if step < supplied else BURST]
+            beat = step - starts[round_of(step)]
+            now = ready[: FIRST_BEATS[step] if step < len(FIRST_BEATS) else STEADY[beat] if step < supplied else BURST]
             units = [unit for unit in units if unit not in now]
-            placed += [(step, unit) for unit in now]
+            placed += [(step, m, unit) for m, unit in enumerate(now)]
             step = step + 1
         last_step = step - 1
         last_sum = [0, 0]
-        for n, (step, (g, q)) in enumerate(placed):
+        for n, (step, m, (g, q)) in enumerate(placed):
             folded = n in FOLDED
-            sum_step = step + (SUM_LAG if step < supplied else 2)
+            slow = SLOW if step < ROUND else 0
+            sum_step = step + slow + (SUM_LAG if step < supplied else 2)
             at(step, MULTIPLY, product, g, q, folded)
             if not folded:
                 at(step, ADD, add_receivers, g, q)
             late = supplied + LATE <= step and n < len(placed) - 2
-            beat = step % ROUND
-            paired = PAIR_FROM <= step < supplied and (beat == 2 or (beat == 1 and n % 2 < PAIRED - 2)) and PAIRED > 0
+            paired = PAIR_FROM <= step < supplied and starts[round_of(step) + 1] - step == PAIR_BACK and m < PAIRED
             if paired:
-                sum_step = step - beat + ROUND - 1
+                sum_step = step + PAIR_BACK - 1
             shared = SENDERS // 2 if n >= len(placed) - 2 else 1 if late and n % 4 < SHARED else 0
-            at(step + 1, RELU, relu_senders, g, q, folded, shared)
+            at(step + slow + 1, RELU, relu_senders, g, q, folded, shared)
             if paired:
                 at(sum_step, SCALE, pair_senders, g, q)
             at(sum_step, SUM, sum_senders, g, q, 2 if paired else SENDERS)
@@ -590,7 +687,7 @@ def tile_compositionalkoopmanoperators_pa_kernel(
         at(end + 3, WIDEN, agg_empty, 1)
         at(end + 4, QUANTISE, agg_quantise, 1)
         at(end + 5, MULTIPLY, final_pass, "a", 1)
-        for n in range(OUT_PARTS):
+        for n in range(len(OUT_WIDTHS)):
             at(last_sum[1] + 6, ADD, finish, n)
 
         for place in sorted(plan):

@@ -17,16 +17,16 @@ CHUNKS = NF // P
 
 ROUND = 5
 JOB = 4
-STEADY = (2, 2, 2, 2, 2)
+STEADY = (3, 2, 3, 2)
 BURST = 3
 AHEAD = 2
 SUM_LAG = 2
 TURN_LEAD = 1
-EARLY = 2
-EDGE = 1
-TURN_FIRST = 5
-TURN_FROM = 1
-FIRST_COPIES = 0
+EARLY = 3
+EDGE = 2
+TURN_FIRST = 2
+TURN_FROM = 0
+FIRST_COPIES = 1
 JOB_AHEAD = 4
 FIRST_BEATS = (1, 1, 0, 0, 0, 1, 1, 1, 1, 2)
 PAIRED = 0
@@ -38,15 +38,18 @@ FRESH = 1
 FOLDED = (0, 1, 7)
 SHARES = ((4, 2, 0), (4, 2, 0), (4, 2, 0), (4, 0, 0), (2, 0, 0), (2, 0, 0))
 EXITS = (6, 6)
-HELPED = {1: 1, 2: 1, 3: 1, 4: 2, 5: 2}
+HELPED = {6: 1, 8: 1, 10: 1, 12: 2, 14: 2}
 LATE_ROUND = 3
 APART = (11, 13, 15)
-COPY_FROM = 10
+COPY_FROM = 2
+COPY_TO = 9
 ON_SCALAR = ()
 TERMS_LATE = 2
 FIRST_TERMS = 0
 SLOW = 1
 LAY_AT = 0
+LAY_GAP = 2
+LAY_GAP2 = 0
 RUN = 8
 OUT_WIDTHS = (256, 256, 256, 256)
 BANKS = 6
@@ -178,7 +181,7 @@ def tile_compositionalkoopmanoperators_pa_kernel(
         def laid_tile(count, shared):
             if shared:
                 return rotating([P, count, 4 * PIECE], BF16, "job_laid", 1)
-            return rotating([P, count, 4 * PIECE], BF16, "laid", 2)
+            return rotating([P, count, 4 * PIECE], BF16, "laid", 3)
 
         def interleave(batch, x, engine, shared=False):
             if x == 0:
@@ -580,7 +583,7 @@ def tile_compositionalkoopmanoperators_pa_kernel(
             count = EXITS[rnd] if rnd < len(EXITS) else 4
             steps += [starts[rnd] + max(0, n - max(0, count - ROUND)) for n in range(count)]
         for (m, kp), step in zip(banks, steps):
-            lead = TURN_LEAD + (EARLY if step < ROUND else EDGE if step == ROUND else 0)
+            lead = EARLY + kp if step < ROUND else EDGE if step == ROUND else TURN_LEAD
             if m > 2:
                 if kp == 0 and m in APART:
                     before = starts[round_of(step)] - 1
@@ -590,15 +593,15 @@ def tile_compositionalkoopmanoperators_pa_kernel(
                     at(step - lead - 1 - AHEAD, LOAD, load_pair, m)
                     at(step - lead - 1, WIDEN, widen, m)
                 at(step - lead, FREE if TURN_FROM <= step - lead < TURN_FIRST else TURN, turn, m, kp)
-            count = HELPED.get(round_of(step), 0) if m % 2 == 0 else 0
+            count = HELPED.get(m, 0)
             if kp < count:
-                at(step, SCALE, copy_out, m, kp, count, step >= COPY_FROM)
+                at(step, SCALE, copy_out, m, kp, count, COPY_FROM <= round_of(step) < COPY_TO)
                 if kp == count - 1:
                     at(step, JOBS, scale_plain, m, count)
             elif step in ON_SCALAR and (kp == 0 or step % ROUND > 0):
                 at(step, LAY, scale_on_scalar, m, kp)
             else:
-                at(step, SCALE, scale_out, m, kp)
+                at(step - (m == 2), SCALE, scale_out, m, kp)
             if (m % 2, kp) == (1, 1):
                 end = starts[round_of(step) + 1] - 1
                 at(end, QUANTISE, quantise_group, m // 2)
@@ -622,8 +625,8 @@ def tile_compositionalkoopmanoperators_pa_kernel(
                 size = len(engines[n : n + 2])
                 batch, pieces = tuple(pieces[:size]), pieces[size:]
                 for x, piece in enumerate(batch):
-                    step = start + (LAY_AT if engines[n + x] == "scalar" else ROUND - 1)
-                    at(start - AHEAD + 1, LOAD, load_piece, piece)
+                    step = start + (LAY_AT + x * (LAY_GAP if rnd == 1 else LAY_GAP2 if rnd == 2 else 0) if engines[n + x] == "scalar" else ROUND - 1)
+                    at(start - AHEAD + 1 - (3 if n == 0 and len(engines) > 2 else 0), LOAD, load_piece, piece)
                     at(step, LAY, interleave, batch, x, engines[n + x])
                 batches.append(batch)
             for batch in batches + [job[:4], job[4:]]:
@@ -637,8 +640,8 @@ def tile_compositionalkoopmanoperators_pa_kernel(
         set_ready = {}
         for c in range(SETS):
             step = max(done[key, kp, c] for key in ("i", "s", "r") for kp in range(PASSES)) + 1 + (c >= TERMS_LATE)
-            at(step if c else -FIRST_TERMS, TERMS, term_products, c)
-            at(step if c else -FIRST_COPIES, TERM_COPIES, term_copies, c)
+            at(step if c else -1, TERMS if c else SUM, term_products, c)
+            at(step, TERM_COPIES if c > 0 or FIRST_COPIES else FREE, term_copies, c)
             set_ready[c] = step + (c > 0)
         at(supplied, LOAD, load_out_bias)
 
@@ -665,11 +668,11 @@ def tile_compositionalkoopmanoperators_pa_kernel(
             late = supplied + LATE <= step and n < len(placed) - 2
             paired = PAIR_FROM <= step < supplied and starts[round_of(step) + 1] - step == PAIR_BACK and m < PAIRED
             if paired:
-                sum_step = step + PAIR_BACK - 1
+                sum_step = step + PAIR_BACK
             shared = SENDERS // 2 if n >= len(placed) - 2 else 1 if late and n % 4 < SHARED else 0
             at(step + slow + 1, RELU, relu_senders, g, q, folded, shared)
             if paired:
-                at(sum_step, SCALE, pair_senders, g, q)
+                at(sum_step - 1, PAIR, pair_senders, g, q)
             at(sum_step, SUM, sum_senders, g, q, 2 if paired else SENDERS)
             last_sum[q // 4] = max(last_sum[q // 4], sum_step)
 

@@ -15,43 +15,15 @@ PIECE = 256
 SETS = NF // PIECE
 CHUNKS = NF // P
 
-ROUND = 5
-JOB = 4
-STEADY = (3, 2, 3, 2)
-BURST = 3
+ROUND = 2 * PASSES
 AHEAD = 2
-SUM_LAG = 2
-TURN_LEAD = 1
-EARLY = 3
-EDGE = 2
-TURN_FIRST = 2
-TURN_FROM = 0
-FIRST_COPIES = 1
-JOB_AHEAD = 4
-FIRST_BEATS = (1, 1, 0, 0, 0, 1, 1, 1, 1, 2)
-PAIRED = 0
-PAIR_FROM = 20
-PAIR_BACK = 4
-SHARED = 0
-LATE = 2
-FRESH = 1
-FOLDED = (0, 1, 7)
-SHARES = ((4, 2, 0), (4, 2, 0), (4, 2, 0), (4, 0, 0), (2, 0, 0), (2, 0, 0))
-EXITS = (6, 6)
-HELPED = {6: 1, 8: 1, 10: 1, 12: 2, 14: 2}
-LATE_ROUND = 3
-APART = (11, 13, 15)
-COPY_FROM = 2
-COPY_TO = 9
-ON_SCALAR = ()
-TERMS_LATE = 2
-FIRST_TERMS = 0
-SLOW = 1
-LAY_AT = 0
-LAY_GAP = 2
-LAY_GAP2 = 0
+BURST = 3
+ON_SCALAR = 2
+BOTH_BANKS = 2
+APART = 3
+LAST_JOB = 3
 RUN = 8
-OUT_WIDTHS = (256, 256, 256, 256)
+OUT_PARTS = 4
 BANKS = 6
 
 F32 = mybir.dt.float32
@@ -65,7 +37,7 @@ ACT = mybir.ActivationFunctionType
 
 FLOPS = 2 * GRAPHS * N * N * NF * NF + 4 * 2 * GRAPHS * N * NF * NF
 
-LOAD, FREE, WIDEN, SCALE, MULTIPLY, TERMS, ADD, PAIR, LAY, RELU, TERM_COPIES, QUANTISE, JOBS, TURN, SUM, LAST = range(16)
+LOAD, WIDEN, SCALE, MULTIPLY, TERMS, ADD, LAY, RELU, COPY_TERMS, CLOSE, GPSIMD, TURN, SUM = range(13)
 
 
 def tile_compositionalkoopmanoperators_pa_kernel(
@@ -108,9 +80,10 @@ def tile_compositionalkoopmanoperators_pa_kernel(
             rows = slice(row + K_PASS * kp, row + K_PASS * (kp + 1))
             return w[rows, PIECE * c : PIECE * (c + 1)].rearrange("(p t) n -> p t n", t=4)
 
-        def load_piece(piece):
-            w_raw[piece] = rotating([P, 4, PIECE], BF16, "w_raw", 5)
-            nc.sync.dma_start(out=w_raw[piece][:], in_=piece_rows(*piece))
+        def load_pieces(pieces):
+            for piece in pieces:
+                w_raw[piece] = rotating([P, 4, PIECE], BF16, "w_raw", 4)
+                nc.sync.dma_start(out=w_raw[piece][:], in_=piece_rows(*piece))
 
         def load_job(job):
             w_raw[job] = rotating([P, len(job), 4, PIECE], BF16, "job_raw", 2)
@@ -122,12 +95,6 @@ def tile_compositionalkoopmanoperators_pa_kernel(
         bias_rows = kept([P, P // 2], F32, "bias_rows")
         out_bias = kept([P, NF], BF16, "out_bias")
 
-        def load_scales():
-            nc.sync.dma_start(out=scale[:], in_=rel_scale.rearrange("a b c (g p t) -> p (a b c g) t", p=P, t=4))
-
-        def load_particles():
-            nc.sync.dma_start(out=obj_sb[:], in_=obj_rows)
-
         def load_out_bias():
             nc.sync.dma_start(out=out_bias[:], in_=pp_b.partition_broadcast(P))
 
@@ -135,86 +102,32 @@ def tile_compositionalkoopmanoperators_pa_kernel(
         ident_bf = kept([P, P], BF16, "ident_bf")
         nc.scalar.activation(ident_bf[:], ident[:], ACT.Relu)
 
-        def load_bias():
-            nc.sync.dma_start(out=bias_rows[:].bitcast(BF16)[0:CHUNKS, :], in_=rp_b.rearrange("(q p) -> q p", p=P))
-
         def turn_rows(rows, bank, passes):
             words = rows.bitcast(F32)
             for kp in range(passes):
                 for u in range(2):
                     nc.tensor.transpose(bank[:, 2 * kp + u, :], words[:, 256 * kp + u : 256 * (kp + 1) : 2], ident[:])
 
-        obj_laid = kept([P, PASSES * P * 4], BF16, "obj_laid")
-        obj_codes = kept([P, PASSES * P], U32, "obj_codes")
-        obj_scales = kept([P, PASSES * P], U8, "obj_scales")
-        obj_bank = {}
-
-        def turn_particles():
-            obj_bank[0] = bank_tile([P, 4, P], F32)
-            turn_rows(obj_sb[:], obj_bank[0], PASSES)
-
-        def empty_particles():
-            nc.scalar.copy(
-                out=obj_laid[:].bitcast(F32).rearrange("p (g r u) -> p g r u", g=PASSES, u=2),
-                in_=obj_bank[0][:].rearrange("p (g u) r -> p g r u", g=PASSES),
-            )
-
-        def quantise_particles():
-            nc.vector.quantize_mx(out=obj_codes[:].bitcast(FP8X4), scales=obj_scales[:], in_=obj_laid[:])
-
-        def particles(kp):
-            return obj_codes[:, P * kp : P * (kp + 1)].bitcast(FP8X4), obj_scales[:, P * kp : P * (kp + 1)]
-
-        bias_cols = kept([P, CHUNKS], F32, "bias_cols")
-        bias_bank = {}
-
-        def turn_bias():
-            bias_bank[0] = bank_tile([P, P], BF16)
-            nc.tensor.transpose(bias_bank[0][:], bias_rows[:].bitcast(BF16), ident_bf[:])
-
-        def empty_bias():
-            nc.scalar.copy(out=bias_cols[:], in_=bias_bank[0][:, 0:CHUNKS])
-
         laid = {}
         w_codes = {}
 
-        def laid_tile(count, shared):
-            if shared:
-                return rotating([P, count, 4 * PIECE], BF16, "job_laid", 1)
-            return rotating([P, count, 4 * PIECE], BF16, "laid", 3)
+        def laid_tile(pieces, last):
+            if last:
+                return rotating([P, len(pieces), 4 * PIECE], BF16, "job_laid", 1)
+            return rotating([P, len(pieces), 4 * PIECE], BF16, "laid", 3)
 
-        def interleave(batch, x, engine, shared=False):
+        def lay(pieces, x, copy, last=False):
             if x == 0:
-                laid[batch] = laid_tile(len(batch), shared)[:]
-            copy = nc.scalar.copy if engine == "scalar" else nc.vector.tensor_copy
+                laid[pieces] = laid_tile(pieces, last)
             copy(
-                out=laid[batch][:, x].rearrange("p (c i t) -> p c t i", i=RUN, t=4),
-                in_=w_raw[batch[x]][:].rearrange("p t (c i) -> p c t i", i=RUN),
+                out=laid[pieces][:, x].rearrange("p (c i t) -> p c t i", i=RUN, t=4),
+                in_=w_raw[pieces[x]][:].rearrange("p t (c i) -> p c t i", i=RUN),
             )
 
-        woven = {}
-
-        def weave(piece):
-            woven[piece] = bank_tile([P, 4 * PIECE], BF16)
-            for m in range(2):
-                nc.tensor.matmul(
-                    out=woven[piece][:, K_PASS * m : K_PASS * (m + 1)],
-                    lhsT=ident_bf[:],
-                    rhs=w_raw[piece][:, :, P * m : P * (m + 1)].rearrange("p t n -> p n t"),
-                    start=True,
-                    stop=True,
-                )
-
-        def empty_woven(batch, x):
-            nc.scalar.copy(out=laid[batch][:, x], in_=woven[batch[x]][:])
-
-        def run_job(job, shared=True):
-            whole = laid_tile(len(job), shared)
-            laid[job[:4]] = whole[:, 0 : len(job[:4])]
-            if len(job) > 4:
-                laid[job[4:]] = whole[:, 4 : len(job)]
+        def run_job(job, last=True):
+            laid[job] = laid_tile(job, last)
             nc.gpsimd.tensor_scalar(
-                out=whole[:].rearrange("p x (n t) -> p x n t", t=4),
+                out=laid[job][:].rearrange("p x (n t) -> p x n t", t=4),
                 in0=w_raw[job][:].rearrange("p x t n -> p x n t"),
                 scalar1=1.0,
                 scalar2=0.0,
@@ -222,16 +135,14 @@ def tile_compositionalkoopmanoperators_pa_kernel(
                 op1=ALU.add,
             )
 
-        def quantise_batch(batch):
-            name = "%s%d%d" % batch[0]
-            codes = kept([P, len(batch) * PIECE], U32, "codes_" + name)
-            scales = kept([P, len(batch) * PIECE], U8, "scales_" + name)
+        def quantise_pieces(pieces):
+            name = "%s%d%d" % pieces[0]
+            codes = kept([P, len(pieces) * PIECE], U32, "codes_" + name)
+            scales = kept([P, len(pieces) * PIECE], U8, "scales_" + name)
             nc.vector.quantize_mx(
-                out=codes[:].bitcast(FP8X4),
-                scales=scales[:],
-                in_=laid[batch].rearrange("p x n -> p (x n)"),
+                out=codes[:].bitcast(FP8X4), scales=scales[:], in_=laid[pieces][:].rearrange("p x n -> p (x n)")
             )
-            for x, piece in enumerate(batch):
+            for x, piece in enumerate(pieces):
                 w_codes[piece] = (codes, scales, PIECE * x)
 
         def piece_weights(piece, first, width):
@@ -242,9 +153,16 @@ def tile_compositionalkoopmanoperators_pa_kernel(
         def chunk_weights(key, kp, q):
             return piece_weights((key, kp, q // 2), P * (q % 2), P)
 
+        obj_laid = kept([P, PASSES * P * 4], BF16, "obj_laid")
+        obj_codes = kept([P, PASSES * P], U32, "obj_codes")
+        obj_scales = kept([P, PASSES * P], U8, "obj_scales")
+        bias_cols = kept([P, CHUNKS], F32, "bias_cols")
         term_bank = {}
         recv = {}
         send = {}
+
+        def particles(kp):
+            return obj_codes[:, P * kp : P * (kp + 1)].bitcast(FP8X4), obj_scales[:, P * kp : P * (kp + 1)]
 
         def term_products(c):
             term_bank[c] = bank_tile([P, 4, P], F32)
@@ -263,7 +181,7 @@ def tile_compositionalkoopmanoperators_pa_kernel(
                             stop=(kp == PASSES - 1),
                         )
 
-        def term_copies(c):
+        def copy_terms(c):
             recv[c] = kept([P, 2, P], F32, "recv%d" % c)
             send[c] = kept([P, 2, P], F32, "send%d" % c)
             for m in range(2):
@@ -275,36 +193,17 @@ def tile_compositionalkoopmanoperators_pa_kernel(
 
         wide = {}
         turned = {}
+        plain = {}
         rel_laid = {}
         rel_codes = [kept([P, PASSES * SENDERS * P], U32, "rel_codes%d" % g) for g in range(GROUPS)]
         rel_scales = [kept([P, PASSES * SENDERS * P], U8, "rel_scales%d" % g) for g in range(GROUPS)]
+        apart = [2 * g + 1 for g in range(GROUPS - APART, GROUPS)]
+        ones = kept([P, 1], F32, "ones")
+        nc.vector.memset(ones[:], 1.0)
 
         def widen(m):
             wide[m] = rotating([P, 2 * NF], BF16, "wide", 3)
             nc.scalar.copy(out=wide[m][:], in_=rel_raw[m][:].bitcast(FP8))
-
-        halves = {}
-
-        def load_half(kp):
-            halves[kp] = kept([P, 2, K_PASS], U8, "rel_half%d" % kp)
-            nc.sync.dma_start(
-                out=halves[kp][:],
-                in_=rel_rows[:, 0 : 2 * NF].rearrange("p (s g k) -> p g s k", s=2, g=PASSES)[:, kp],
-            )
-
-        def widen_half(kp):
-            wide[0, kp] = kept([P, 2 * K_PASS], BF16, "wide_half%d" % kp)
-            nc.scalar.copy(out=wide[0, kp][:], in_=halves[kp][:].rearrange("p s k -> p (s k)").bitcast(FP8))
-
-        def turn_half(kp):
-            turned[0, kp] = bank_tile([P, 2, 2, P], F32)
-            words = wide[0, kp][:].bitcast(F32)
-            for u in range(2):
-                for s in range(2):
-                    nc.tensor.transpose(turned[0, kp][:, u, s, :], words[:, 256 * s + u : 256 * (s + 1) : 2], ident[:])
-
-        ones = kept([P, 1], F32, "ones")
-        nc.vector.memset(ones[:], 1.0)
 
         def widen_apart(m):
             wide[m] = rotating([P, 2 * NF], BF16, "wide", 3)
@@ -321,7 +220,7 @@ def tile_compositionalkoopmanoperators_pa_kernel(
             words = wide[m][:].bitcast(F32)
             for u in range(2):
                 for s in range(2):
-                    if m in APART:
+                    if m in apart:
                         first = K_PASS * u + P * (2 * s + kp)
                         rows = words[:, first : first + P]
                     else:
@@ -329,27 +228,25 @@ def tile_compositionalkoopmanoperators_pa_kernel(
                         rows = words[:, first + u : first + 256 : 2]
                     nc.tensor.transpose(turned[m, kp][:, u, s, :], rows, ident[:])
 
-        def scale_out(m, kp):
-            g = m // 2
+        def open_group(m, kp):
             if (m % 2, kp) == (0, 0):
-                rel_laid[g] = rotating([P, PASSES, 2, 2 * P * 4], BF16, "rel_laid", 2)
+                rel_laid[m // 2] = rotating([P, PASSES, 2, 2 * P * 4], BF16, "rel_laid", 2)
+
+        def scale_out(m, kp):
+            open_group(m, kp)
             values = turned[m, kp][:].rearrange("p u s r -> p (u s r)").bitcast(BF16)
             factors = scale[:, kp, :].rearrange("p (u e) -> p u e", u=2)
             nc.vector.tensor_tensor(
-                out=rel_laid[g][:, kp, m % 2, :].rearrange("p (x u e) -> p x u e", u=2, e=2),
+                out=rel_laid[m // 2][:, kp, m % 2, :].rearrange("p (x u e) -> p x u e", u=2, e=2),
                 in0=values.rearrange("p (u x e) -> p x u e", u=2, e=2),
                 in1=factors.unsqueeze(1).to_broadcast([P, 2 * P, 2, 2]),
                 op=ALU.mult,
             )
 
-        plain = {}
-
-        def copy_out(m, kp, count, on_scalar):
-            if (m % 2, kp) == (0, 0):
-                rel_laid[m // 2] = rotating([P, PASSES, 2, 2 * P * 4], BF16, "rel_laid", 2)
+        def copy_out(m, kp, count, copy):
+            open_group(m, kp)
             if kp == 0:
                 plain[m] = rotating([P, count, 2 * P * 4], BF16, "plain", 1)
-            copy = nc.scalar.copy if on_scalar else nc.vector.tensor_copy
             copy(
                 out=plain[m][:, kp, :].bitcast(F32).rearrange("p (x u) -> p x u", u=2),
                 in_=turned[m, kp][:].rearrange("p u s r -> p (s r) u"),
@@ -363,21 +260,6 @@ def tile_compositionalkoopmanoperators_pa_kernel(
                 op=ALU.mult,
             )
 
-        def scale_on_scalar(m, kp):
-            if (m % 2, kp) == (0, 0):
-                rel_laid[m // 2] = rotating([P, PASSES, 2, 2 * P * 4], BF16, "rel_laid", 2)
-            planes = rotating([P, 4, 2 * P], BF16, "planes", 1)
-            values = turned[m, kp][:].rearrange("p u s r -> p (u s r)").bitcast(BF16)
-            values = values.rearrange("p (u x e) -> p u e x", u=2, e=2)
-            for t in range(4):
-                nc.scalar.activation(
-                    planes[:, t, :], values[:, t // 2, t % 2, :], ACT.Copy, scale=scale[:, kp, t : t + 1]
-                )
-            nc.scalar.copy(
-                out=rel_laid[m // 2][:, kp, m % 2, :].rearrange("p (c i t) -> p c t i", i=RUN, t=4),
-                in_=planes[:].rearrange("p t (c i) -> p c t i", i=RUN),
-            )
-
         def quantise_group(g):
             nc.vector.quantize_mx(
                 out=rel_codes[g][:].bitcast(FP8X4),
@@ -389,6 +271,9 @@ def tile_compositionalkoopmanoperators_pa_kernel(
         summed = [0, 0]
         acc = {}
         eff = {}
+
+        def eff_tile():
+            return rotating([P, SENDERS, P], F32, "eff", 4 * BURST)
 
         def product(g, q, folded):
             acc[g, q] = bank_tile([P, SENDERS, P], F32)
@@ -419,7 +304,7 @@ def tile_compositionalkoopmanoperators_pa_kernel(
                     )
 
         def add_receivers(g, q):
-            eff[g, q] = rotating([P, SENDERS, P], F32, "eff", 12)
+            eff[g, q] = eff_tile()
             nc.vector.tensor_tensor(
                 out=eff[g, q][:],
                 in0=acc[g, q][:],
@@ -429,7 +314,7 @@ def tile_compositionalkoopmanoperators_pa_kernel(
 
         def relu_senders(g, q, folded, on_vector):
             if folded:
-                eff[g, q] = rotating([P, SENDERS, P], F32, "eff", 12)
+                eff[g, q] = eff_tile()
             src = acc[g, q] if folded else eff[g, q]
             for s in range(SENDERS):
                 for b in range(GRAPHS):
@@ -448,23 +333,18 @@ def tile_compositionalkoopmanoperators_pa_kernel(
                     else:
                         nc.scalar.activation(eff[g, q][:, s, cols], src[:, s, cols], ACT.Relu, bias=bias)
 
-        def pair_senders(g, q):
-            nc.vector.tensor_tensor(
-                out=eff[g, q][:, 0:2, :], in0=eff[g, q][:, 0:2, :], in1=eff[g, q][:, 2:4, :], op=ALU.add
-            )
-
-        def sum_senders(g, q, terms):
+        def sum_senders(g, q):
             h = q // 4
-            for s in range(terms):
+            for s in range(SENDERS):
                 nc.tensor.matmul(
                     out=agg[h][:, q % 4, :],
                     lhsT=eff[g, q][:, s, :],
                     rhs=ident[:],
                     is_transpose=True,
                     start=(summed[h] == 0),
-                    stop=(summed[h] == 4 * N - SENDERS // terms),
+                    stop=(summed[h] == 4 * N - 1),
                 )
-                summed[h] = summed[h] + SENDERS // terms
+                summed[h] = summed[h] + 1
 
         agg_rows = {}
         agg_bank = {}
@@ -473,22 +353,22 @@ def tile_compositionalkoopmanoperators_pa_kernel(
         agg_scales = {}
         final = {}
 
-        def agg_round(h):
+        def round_agg(h):
             agg_rows[h] = kept([P, K_PASS], BF16, "agg_rows%d" % h)
             nc.vector.tensor_copy(out=agg_rows[h][:], in_=agg[h][:].rearrange("p q f -> p (q f)"))
 
-        def agg_turn(h):
+        def turn_agg(h):
             agg_bank[h] = bank_tile([P, 2, P], F32)
             turn_rows(agg_rows[h][:], agg_bank[h], 1)
 
-        def agg_empty(h):
+        def lay_agg(h):
             agg_laid[h] = kept([P, 4 * P], BF16, "agg_laid%d" % h)
             nc.scalar.copy(
                 out=agg_laid[h][:].bitcast(F32).rearrange("p (r u) -> p r u", u=2),
                 in_=agg_bank[h][:].rearrange("p u r -> p r u"),
             )
 
-        def agg_quantise(h):
+        def quantise_agg(h):
             agg_codes[h] = kept([P, P], U32, "agg_codes%d" % h)
             agg_scales[h] = kept([P, P], U8, "agg_scales%d" % h)
             nc.vector.quantize_mx(out=agg_codes[h][:].bitcast(FP8X4), scales=agg_scales[h][:], in_=agg_laid[h][:])
@@ -511,10 +391,9 @@ def tile_compositionalkoopmanoperators_pa_kernel(
                 )
 
         def finish(n):
-            width = OUT_WIDTHS[n]
-            left = sum(OUT_WIDTHS[:n])
-            cols = slice(left, left + width)
-            h, first = divmod(left, K_PASS)
+            width = NF // OUT_PARTS
+            cols = slice(width * n, width * (n + 1))
+            h, first = divmod(width * n, K_PASS)
             result = kept([P, width], F32, "result%d" % n)
             nc.vector.tensor_tensor(
                 out=result[:], in0=final[h][:, first : first + width], in1=out_bias[:, cols], op=ALU.add
@@ -522,177 +401,182 @@ def tile_compositionalkoopmanoperators_pa_kernel(
             nc.scalar.activation(result[:], result[:], ACT.Relu)
             nc.sync.dma_start(out=out_rows[:, cols], in_=result[:])
 
-        def both_passes(key, c):
-            return tuple((key, kp, c) for kp in range(PASSES))
-
-        first_i, first_r, first_s = both_passes("i", 0), both_passes("r", 0), both_passes("s", 0)
+        first_r, first_s, first_i = (tuple((key, kp, 0) for kp in range(PASSES)) for key in ("r", "s", "i"))
         load_pair(0)
-        load_scales()
-        for piece in first_r:
-            load_piece(piece)
+        nc.sync.dma_start(out=scale[:], in_=rel_scale.rearrange("a b c (g p t) -> p (a b c g) t", p=P, t=4))
+        load_pieces(first_r)
         load_pair(1)
-        load_particles()
+        nc.sync.dma_start(out=obj_sb[:], in_=obj_rows)
         load_job(first_s)
-        load_bias()
-        for piece in first_i:
-            load_piece(piece)
+        nc.sync.dma_start(out=bias_rows[:].bitcast(BF16)[0:CHUNKS, :], in_=rp_b.rearrange("(q p) -> q p", p=P))
+        load_pieces(first_i)
         load_pair(2)
+
         widen(0)
-        interleave(first_r, 0, "vector")
-        interleave(first_r, 1, "vector")
-        turn(0, 0)
-        turn(0, 1)
+        for x in range(PASSES):
+            lay(first_r, x, nc.vector.tensor_copy)
+        for kp in range(PASSES):
+            turn(0, kp)
         widen(1)
         scale_out(0, 0)
-        quantise_batch(first_r)
+        quantise_pieces(first_r)
         turn(1, 0)
-        turn_particles()
+        obj_bank = bank_tile([P, 4, P], F32)
+        turn_rows(obj_sb[:], obj_bank, PASSES)
         turn(1, 1)
-        turn_bias()
-        run_job(first_s, False)
+        bias_bank = bank_tile([P, P], BF16)
+        nc.tensor.transpose(bias_bank[:], bias_rows[:].bitcast(BF16), ident_bf[:])
+        run_job(first_s, last=False)
         scale_out(0, 1)
-        scale_out(1, 0)
-        empty_particles()
-        interleave(first_i, 0, "scalar", True)
-        scale_out(1, 1)
-        interleave(first_i, 1, "scalar", True)
-        empty_bias()
+        for kp in range(PASSES):
+            scale_out(1, kp)
+        nc.scalar.copy(
+            out=obj_laid[:].bitcast(F32).rearrange("p (g r u) -> p g r u", g=PASSES, u=2),
+            in_=obj_bank[:].rearrange("p (g u) r -> p g r u", g=PASSES),
+        )
+        for x in range(PASSES):
+            lay(first_i, x, nc.scalar.copy, last=True)
+        nc.scalar.copy(out=bias_cols[:], in_=bias_bank[:, 0:CHUNKS])
         widen(2)
-        turn(2, 0)
-        turn(2, 1)
-        quantise_particles()
+        for kp in range(PASSES):
+            turn(2, kp)
+        nc.vector.quantize_mx(out=obj_codes[:].bitcast(FP8X4), scales=obj_scales[:], in_=obj_laid[:])
         quantise_group(0)
-        quantise_batch(first_s)
-        quantise_batch(first_i)
-
-        plan = {}
-
-        def at(step, rank, fn, *args):
-            plan.setdefault((step, rank), []).append((fn, args))
-
-        lengths = [ROUND] * len(EXITS) + [len(STEADY)] * GROUPS
-        starts = [sum(lengths[:rnd]) for rnd in range(len(lengths))]
-
-        def round_of(step):
-            return max(rnd for rnd, start in enumerate(starts) if start <= step)
-
-        group_ready = {0: 0}
-        banks = [(m, kp) for m in range(2, N // 2) for kp in range(PASSES)]
-        steps = []
-        for rnd in range(GROUPS):
-            count = EXITS[rnd] if rnd < len(EXITS) else 4
-            steps += [starts[rnd] + max(0, n - max(0, count - ROUND)) for n in range(count)]
-        for (m, kp), step in zip(banks, steps):
-            lead = EARLY + kp if step < ROUND else EDGE if step == ROUND else TURN_LEAD
-            if m > 2:
-                if kp == 0 and m in APART:
-                    before = starts[round_of(step)] - 1
-                    at(before - AHEAD, LOAD, load_pair, m)
-                    at(before, PAIR, widen_apart, m)
-                elif kp == 0:
-                    at(step - lead - 1 - AHEAD, LOAD, load_pair, m)
-                    at(step - lead - 1, WIDEN, widen, m)
-                at(step - lead, FREE if TURN_FROM <= step - lead < TURN_FIRST else TURN, turn, m, kp)
-            count = HELPED.get(m, 0)
-            if kp < count:
-                at(step, SCALE, copy_out, m, kp, count, COPY_FROM <= round_of(step) < COPY_TO)
-                if kp == count - 1:
-                    at(step, JOBS, scale_plain, m, count)
-            elif step in ON_SCALAR and (kp == 0 or step % ROUND > 0):
-                at(step, LAY, scale_on_scalar, m, kp)
-            else:
-                at(step - (m == 2), SCALE, scale_out, m, kp)
-            if (m % 2, kp) == (1, 1):
-                end = starts[round_of(step) + 1] - 1
-                at(end, QUANTISE, quantise_group, m // 2)
-                group_ready[m // 2] = end + 1
+        quantise_pieces(first_s)
+        quantise_pieces(first_i)
 
         pieces = [(key, kp, c) for c in range(1, SETS) for key in ("i", "s", "r") for kp in range(PASSES)]
         pieces += [(key, kp, c) for key in ("o", "a") for kp in range(PASSES) for c in range(SETS)]
-        done = {piece: -1 for piece in first_i + first_r + first_s}
-        rnd = 0
-        start = 0
+        per_set = 3 * PASSES
+        job, others = tuple(pieces[: per_set - ON_SCALAR]), tuple(pieces[per_set - ON_SCALAR : per_set])
+        pieces = pieces[per_set:]
+        load_pair(3)
+        load_job(job)
+        load_pair(4)
+        load_pieces(others)
+        run_job(job)
+        for m in (3, 4):
+            widen(m)
+            for kp in range(PASSES):
+                scale_out(m - 1, kp)
+            for kp in range(PASSES):
+                turn(m, kp)
+            if m == 3:
+                term_products(0)
+        load_pair(5)
+        product(0, 0, True)
+        for x in range(ON_SCALAR):
+            lay(others, x, nc.scalar.copy)
+        copy_terms(0)
+        product(0, 1, True)
+        widen(5)
+        for kp in range(PASSES):
+            relu_senders(0, kp, True, 0)
+            scale_out(4, kp)
+        for kp in range(PASSES):
+            turn(5, kp)
+        sum_senders(0, 0)
+        quantise_group(1)
+        quantise_pieces(others)
+        quantise_pieces(job)
+        sum_senders(0, 1)
+
+        plan = {}
+
+        def at(beat, rank, fn, *args):
+            plan.setdefault((beat, rank), []).append((fn, args))
+
+        for kp in range(PASSES):
+            at(0, SCALE, scale_out, 5, kp)
+        at(ROUND, CLOSE, quantise_group, 2)
+        group_ready = {0: -1, 1: 0, 2: ROUND + 1}
+        on_gpsimd = {}
+        for g in range(3, GROUPS):
+            end = ROUND * (g - 2)
+            on_gpsimd[g] = PASSES if g >= GROUPS - BOTH_BANKS else 1
+            copy = nc.scalar.copy if g > 3 else nc.vector.tensor_copy
+            for n in range(ROUND):
+                m, kp = 2 * g + n // PASSES, n % PASSES
+                beat = end - ROUND + 1 + n
+                if kp == 0 and m in apart:
+                    at(end - ROUND - AHEAD, LOAD, load_pair, m)
+                    at(end - ROUND, LAY, widen_apart, m)
+                elif kp == 0:
+                    at(beat - 2 - AHEAD, LOAD, load_pair, m)
+                    at(beat - 2, WIDEN, widen, m)
+                at(beat - 1, TURN, turn, m, kp)
+                if n < on_gpsimd[g]:
+                    at(beat, SCALE, copy_out, m, kp, on_gpsimd[g], copy)
+                else:
+                    at(beat, SCALE, scale_out, m, kp)
+            at(end - ROUND + on_gpsimd[g], GPSIMD, scale_plain, 2 * g, on_gpsimd[g])
+            at(end, CLOSE, quantise_group, g)
+            group_ready[g] = end + 1
         supplied = group_ready[GROUPS - 1]
-        while pieces:
-            length = lengths[rnd] if start < supplied else LATE_ROUND
-            on_gpsimd, on_scalar, on_vector = SHARES[rnd] if rnd < len(SHARES) else (JOB, 0, 0)
-            job, pieces = tuple(pieces[:on_gpsimd]), pieces[on_gpsimd:]
-            at(start - JOB_AHEAD, LOAD, load_job, job)
-            at(start - 1, JOBS, run_job, job)
-            engines = ["scalar"] * on_scalar + ["vector"] * on_vector
-            batches = []
-            for n in range(0, len(engines), 2):
-                size = len(engines[n : n + 2])
-                batch, pieces = tuple(pieces[:size]), pieces[size:]
-                for x, piece in enumerate(batch):
-                    step = start + (LAY_AT + x * (LAY_GAP if rnd == 1 else LAY_GAP2 if rnd == 2 else 0) if engines[n + x] == "scalar" else ROUND - 1)
-                    at(start - AHEAD + 1 - (3 if n == 0 and len(engines) > 2 else 0), LOAD, load_piece, piece)
-                    at(step, LAY, interleave, batch, x, engines[n + x])
-                batches.append(batch)
-            for batch in batches + [job[:4], job[4:]]:
-                if batch and pieces:
-                    at(start + length - 1, QUANTISE, quantise_batch, batch)
-                for piece in batch:
-                    done[piece] = start + length - 1
-            rnd = rnd + 1
-            start = start + length
-        last_job = job
-        set_ready = {}
-        for c in range(SETS):
-            step = max(done[key, kp, c] for key in ("i", "s", "r") for kp in range(PASSES)) + 1 + (c >= TERMS_LATE)
-            at(step if c else -1, TERMS if c else SUM, term_products, c)
-            at(step, TERM_COPIES if c > 0 or FIRST_COPIES else FREE, term_copies, c)
-            set_ready[c] = step + (c > 0)
+
+        for g in range(3, GROUPS):
+            start, end = group_ready[g - 1] if g > 3 else 0, group_ready[g] - 1
+            size = per_set - ON_SCALAR * on_gpsimd[g]
+            job, pieces = tuple(pieces[:size]), pieces[size:]
+            at(start - ROUND, LOAD, load_job, job)
+            at(start - 1, GPSIMD, run_job, job)
+            if g - 1 < SETS:
+                others, pieces = tuple(pieces[:ON_SCALAR]), pieces[ON_SCALAR:]
+                at(start - 1, LOAD, load_pieces, others)
+                for x in range(ON_SCALAR):
+                    at(start + 2 * x, LAY, lay, others, x, nc.scalar.copy)
+                at(end, CLOSE, quantise_pieces, others)
+            at(end, CLOSE, quantise_pieces, job)
+        first_a, second_a = tuple(pieces[:SETS]), tuple(pieces[SETS:])
+        at(supplied - ROUND, LOAD, load_job, first_a)
+        at(supplied - 1, GPSIMD, run_job, first_a)
+        at(supplied + LAST_JOB - ROUND, LOAD, load_job, second_a)
+        at(supplied + LAST_JOB - 1, CLOSE, quantise_pieces, first_a)
+        at(supplied + LAST_JOB - 1, GPSIMD, run_job, second_a)
         at(supplied, LOAD, load_out_bias)
 
-        units = [(g, q) for h in range(2) for g in range(GROUPS) for q in range(4 * h, 4 * h + 4)]
-        placed = []
-        step = 0
-        while units:
-            ready = [(g, q) for g, q in units if max(group_ready[g], set_ready[q // 2]) <= step - FRESH]
-            ready += [(g, q) for g, q in units if step - FRESH < max(group_ready[g], set_ready[q // 2]) <= step]
-            beat = step - starts[round_of(step)]
-            now = ready[: FIRST_BEATS[step] if step < len(FIRST_BEATS) else STEADY[beat] if step < supplied else BURST]
-            units = [unit for unit in units if unit not in now]
-            placed += [(step, m, unit) for m, unit in enumerate(now)]
-            step = step + 1
-        last_step = step - 1
-        last_sum = [0, 0]
-        for n, (step, m, (g, q)) in enumerate(placed):
-            folded = n in FOLDED
-            slow = SLOW if step < ROUND else 0
-            sum_step = step + slow + (SUM_LAG if step < supplied else 2)
-            at(step, MULTIPLY, product, g, q, folded)
-            if not folded:
-                at(step, ADD, add_receivers, g, q)
-            late = supplied + LATE <= step and n < len(placed) - 2
-            paired = PAIR_FROM <= step < supplied and starts[round_of(step) + 1] - step == PAIR_BACK and m < PAIRED
-            if paired:
-                sum_step = step + PAIR_BACK
-            shared = SENDERS // 2 if n >= len(placed) - 2 else 1 if late and n % 4 < SHARED else 0
-            at(step + slow + 1, RELU, relu_senders, g, q, folded, shared)
-            if paired:
-                at(sum_step - 1, PAIR, pair_senders, g, q)
-            at(sum_step, SUM, sum_senders, g, q, 2 if paired else SENDERS)
-            last_sum[q // 4] = max(last_sum[q // 4], sum_step)
+        set_ready = {0: -1}
+        for c in range(1, SETS):
+            beat = 0 if c == 1 else group_ready[c + 1] + 1
+            at(beat, TERMS, term_products, c)
+            at(beat, COPY_TERMS, copy_terms, c)
+            set_ready[c] = beat + 1
 
-        end = last_sum[1]
-        at(last_sum[0] + 1, SCALE, agg_round, 0)
-        at(end, QUANTISE, quantise_batch, last_job)
-        at(end + 1, SCALE, agg_round, 1)
-        at(end + 1, FREE, agg_turn, 0)
-        at(last_step + 1, MULTIPLY, final_pass, "o", 0)
-        at(end + 1, MULTIPLY, final_pass, "o", 1)
-        at(end + 1, RELU, agg_empty, 0)
-        at(end + 1, QUANTISE, agg_quantise, 0)
-        at(end + 2, FREE, agg_turn, 1)
-        at(end + 2, MULTIPLY, final_pass, "a", 0)
-        at(end + 3, WIDEN, agg_empty, 1)
-        at(end + 4, QUANTISE, agg_quantise, 1)
-        at(end + 5, MULTIPLY, final_pass, "a", 1)
-        for n in range(len(OUT_WIDTHS)):
-            at(last_sum[1] + 6, ADD, finish, n)
+        units = [(g, q) for h in range(2) for g in range(GROUPS) for q in range(4 * h, 4 * h + 4)][2:]
+        beat = 0
+        last_sum = [0, 0]
+        while units:
+            ready = [(g, q) for g, q in units if max(group_ready[g], set_ready[q // 2]) < beat]
+            ready += [(g, q) for g, q in units if max(group_ready[g], set_ready[q // 2]) == beat]
+            count = 1 if beat < ROUND else BURST - (beat % 2 == 0 and beat < supplied)
+            for g, q in ready[:count]:
+                units = [unit for unit in units if unit != (g, q)]
+                folded = (beat, g, q) == (ROUND, 1, 3)
+                at(beat, MULTIPLY, product, g, q, folded)
+                if not folded:
+                    at(beat, ADD, add_receivers, g, q)
+                at(beat + 1, RELU, relu_senders, g, q, folded, SENDERS // 2 if len(units) < 2 else 0)
+                at(beat + 2, SUM, sum_senders, g, q)
+                last_sum[q // 4] = beat + 2
+            beat = beat + 1
+
+        at(last_sum[0] + 1, SCALE, round_agg, 0)
+        at(beat, MULTIPLY, final_pass, "o", 0)
+        at(last_sum[1], CLOSE, quantise_pieces, second_a)
 
         for place in sorted(plan):
             for fn, args in plan[place]:
                 fn(*args)
+
+        turn_agg(0)
+        round_agg(1)
+        final_pass("o", 1)
+        lay_agg(0)
+        quantise_agg(0)
+        turn_agg(1)
+        final_pass("a", 0)
+        lay_agg(1)
+        quantise_agg(1)
+        final_pass("a", 1)
+        for n in range(OUT_PARTS):
+            finish(n)

@@ -399,7 +399,8 @@ def tile_compositionalkoopmanoperators_pa_kernel(
                 out=result[:], in0=final[h][:, first : first + width], in1=out_bias[:, cols], op=ALU.add
             )
             nc.scalar.activation(result[:], result[:], ACT.Relu)
-            nc.sync.dma_start(out=out_rows[:, cols], in_=result[:])
+            queue = nc.scalar if n == OUT_PARTS - 1 else nc.sync
+            queue.dma_start(out=out_rows[:, cols], in_=result[:])
 
         first_r, first_s, first_i = (tuple((key, kp, 0) for kp in range(PASSES)) for key in ("r", "s", "i"))
         load_pair(0)
@@ -551,7 +552,7 @@ def tile_compositionalkoopmanoperators_pa_kernel(
             count = 1 if beat < ROUND else BURST - (beat % 2 == 0 and beat < supplied)
             for g, q in ready[:count]:
                 units = [unit for unit in units if unit != (g, q)]
-                folded = (beat, g, q) == (ROUND, 1, 3)
+                folded = beat % ROUND == 0 and 0 < beat <= (SETS - 2) * ROUND and (g, q) == ready[count - 1]
                 at(beat, MULTIPLY, product, g, q, folded)
                 if not folded:
                     at(beat, ADD, add_receivers, g, q)

@@ -156,7 +156,6 @@ def tile_compositionalkoopmanoperators_pa_kernel(
         obj_laid = kept([P, PASSES * P * 4], BF16, "obj_laid")
         obj_codes = kept([P, PASSES * P], U32, "obj_codes")
         obj_scales = kept([P, PASSES * P], U8, "obj_scales")
-        bias_cols = kept([P, CHUNKS], F32, "bias_cols")
         term_bank = {}
         recv = {}
         send = {}
@@ -196,6 +195,7 @@ def tile_compositionalkoopmanoperators_pa_kernel(
         plain = {}
         rel_laid = {}
         rel_codes = [kept([P, PASSES * SENDERS * P], U32, "rel_codes%d" % g) for g in range(GROUPS)]
+        bias_cols = kept([P, CHUNKS], F32, "bias_cols")
         rel_scales = [kept([P, PASSES * SENDERS * P], U8, "rel_scales%d" % g) for g in range(GROUPS)]
         apart = [2 * g + 1 for g in range(GROUPS - APART, GROUPS)]
         ones = kept([P, 1], F32, "ones")

@@ -11,20 +11,37 @@ GRAPHS = 4
 N = 32
 SENDERS = 4
 GROUPS = N // SENDERS
+PAIRS = 2 * GROUPS
 PIECE = 256
 SETS = NF // PIECE
 CHUNKS = NF // P
-
-ROUND = 2 * PASSES
-AHEAD = 2
-BURST = 3
-ON_SCALAR = 2
-BOTH_BANKS = 2
-APART = 3
-LAST_JOB = 3
 RUN = 8
 OUT_PARTS = 4
 BANKS = 6
+
+BEATS = {}
+STEADY = [(4, 2), (4, 2), (4, 0)]
+WEAVE0 = False
+GFIRST = False
+LAST = [4, 4, 4, 4]
+GS = [0, 0, 0, 0, 0, 1, 1, 1]
+JOB = [2, 4, 4, 4, 4, 4, 4, 4]
+REST = {2: "S", 3: "G"}
+ZFROM = {0: 5}
+CFROM = {}
+DRANGE = {}
+NFOLD = {}
+SUM_LAG = 1
+SUM_SPLIT = 0
+RELU_SPLIT = 0
+EFF = 12
+SHARE_LAST = 2
+PA_GAP = 2
+TERMS_RANK = 6
+TERMS_COPY = 15
+LOAD_AHEAD = 2
+WIDEN_RANK = 7
+FLOORS = 2
 
 F32 = mybir.dt.float32
 BF16 = mybir.dt.bfloat16
@@ -34,10 +51,11 @@ FP8 = mybir.dt.float8_e4m3fn
 FP8X4 = mybir.dt.float8_e4m3fn_x4
 ALU = mybir.AluOpType
 ACT = mybir.ActivationFunctionType
+AX = mybir.AxisListType
 
 FLOPS = 2 * GRAPHS * N * N * NF * NF + 4 * 2 * GRAPHS * N * NF * NF
 
-LOAD, WIDEN, SCALE, MULTIPLY, TERMS, ADD, LAY, RELU, COPY_TERMS, CLOSE, GPSIMD, TURN, SUM = range(13)
+LOAD, TURN0, COPY_OUT, SCALE, TERMS, MULTIPLY, COPY_TERMS, WIDEN, BACKS, LAY, CLOSE, GPSIMD, LATE, ADD, CLAMP, RELU, WEAVES, TURN, SUM = range(19)
 
 
 def tile_compositionalkoopmanoperators_pa_kernel(
@@ -102,12 +120,6 @@ def tile_compositionalkoopmanoperators_pa_kernel(
         ident_bf = kept([P, P], BF16, "ident_bf")
         nc.scalar.activation(ident_bf[:], ident[:], ACT.Relu)
 
-        def turn_rows(rows, bank, passes):
-            words = rows.bitcast(F32)
-            for kp in range(passes):
-                for u in range(2):
-                    nc.tensor.transpose(bank[:, 2 * kp + u, :], words[:, 256 * kp + u : 256 * (kp + 1) : 2], ident[:])
-
         laid = {}
         w_codes = {}
 
@@ -122,6 +134,36 @@ def tile_compositionalkoopmanoperators_pa_kernel(
             copy(
                 out=laid[pieces][:, x].rearrange("p (c i t) -> p c t i", i=RUN, t=4),
                 in_=w_raw[pieces[x]][:].rearrange("p t (c i) -> p c t i", i=RUN),
+            )
+
+        woven = {}
+
+        def weave(piece):
+            woven[piece] = bank_tile([P, 4 * PIECE], BF16)
+            for n in range(2):
+                nc.tensor.matmul(
+                    out=woven[piece][:, K_PASS * n : K_PASS * (n + 1)],
+                    lhsT=ident_bf[:],
+                    rhs=w_raw[piece][:, :, P * n : P * (n + 1)].rearrange("p t n -> p n t"),
+                    start=True,
+                    stop=True,
+                )
+
+        def lay_woven(pieces, x, last=False):
+            if x == 0:
+                laid[pieces] = laid_tile(pieces, last)
+            nc.scalar.copy(out=laid[pieces][:, x], in_=woven[pieces[x]][:])
+
+        def lay_gpsimd(pieces, x):
+            if x == 0:
+                laid[pieces] = laid_tile(pieces, False)
+            nc.gpsimd.tensor_scalar(
+                out=laid[pieces][:, x].rearrange("p (n t) -> p n t", t=4),
+                in0=w_raw[pieces[x]][:].rearrange("p t n -> p n t"),
+                scalar1=1.0,
+                scalar2=0.0,
+                op0=ALU.mult,
+                op1=ALU.add,
             )
 
         def run_job(job, last=True):
@@ -139,9 +181,16 @@ def tile_compositionalkoopmanoperators_pa_kernel(
             name = "%s%d%d" % pieces[0]
             codes = kept([P, len(pieces) * PIECE], U32, "codes_" + name)
             scales = kept([P, len(pieces) * PIECE], U8, "scales_" + name)
-            nc.vector.quantize_mx(
-                out=codes[:].bitcast(FP8X4), scales=scales[:], in_=laid[pieces][:].rearrange("p x n -> p (x n)")
-            )
+            first = 0
+            for width in (4, 2, 1):
+                if len(pieces) & width:
+                    cols = slice(PIECE * first, PIECE * (first + width))
+                    nc.vector.quantize_mx(
+                        out=codes[:, cols].bitcast(FP8X4),
+                        scales=scales[:, cols],
+                        in_=laid[pieces][:, first : first + width].rearrange("p x n -> p (x n)"),
+                    )
+                    first = first + width
             for x, piece in enumerate(pieces):
                 w_codes[piece] = (codes, scales, PIECE * x)
 
@@ -159,6 +208,7 @@ def tile_compositionalkoopmanoperators_pa_kernel(
         term_bank = {}
         recv = {}
         send = {}
+        minus = {}
 
         def particles(kp):
             return obj_codes[:, P * kp : P * (kp + 1)].bitcast(FP8X4), obj_scales[:, P * kp : P * (kp + 1)]
@@ -189,6 +239,14 @@ def tile_compositionalkoopmanoperators_pa_kernel(
                     send[c][:, m, :], term_bank[c][:, 2 + m, :], ACT.Identity, bias=bias_cols[:, q : q + 1]
                 )
             nc.scalar.copy(out=recv[c][:], in_=term_bank[c][:, 0:2, :])
+            for m in range(2):
+                q = 2 * c + m
+                if q in ZFROM:
+                    minus[q] = kept([P, P], F32, "minus%d" % q)
+                    nc.scalar.activation(minus[q][:], term_bank[c][:, m, :], ACT.Copy, scale=-1.0)
+                if q in CFROM or q in DRANGE:
+                    minus[q] = kept([P, P], F32, "minus%d" % q)
+                    nc.scalar.activation(minus[q][:], send[c][:, m, :], ACT.Copy, scale=-1.0)
 
         wide = {}
         turned = {}
@@ -197,22 +255,12 @@ def tile_compositionalkoopmanoperators_pa_kernel(
         rel_codes = [kept([P, PASSES * SENDERS * P], U32, "rel_codes%d" % g) for g in range(GROUPS)]
         bias_cols = kept([P, CHUNKS], F32, "bias_cols")
         rel_scales = [kept([P, PASSES * SENDERS * P], U8, "rel_scales%d" % g) for g in range(GROUPS)]
-        apart = [2 * g + 1 for g in range(GROUPS - APART, GROUPS)]
-        ones = kept([P, 1], F32, "ones")
-        nc.vector.memset(ones[:], 1.0)
 
         def widen(m):
             wide[m] = rotating([P, 2 * NF], BF16, "wide", 3)
-            nc.scalar.copy(out=wide[m][:], in_=rel_raw[m][:].bitcast(FP8))
-
-        def widen_apart(m):
-            wide[m] = rotating([P, 2 * NF], BF16, "wide", 3)
-            nc.vector.tensor_scalar(
-                out=wide[m][:].rearrange("q (u x e) -> q x u e", u=2, e=2),
-                in0=rel_raw[m][:].bitcast(FP8).rearrange("q (x u e) -> q x u e", u=2, e=2),
-                scalar1=ones[:],
-                scalar2=None,
-                op0=ALU.mult,
+            nc.scalar.copy(
+                out=wide[m][:].rearrange("q (u x e) -> q u x e", u=2, e=2),
+                in_=rel_raw[m][:].bitcast(FP8).rearrange("q (x u e) -> q u x e", u=2, e=2),
             )
 
         def turn(m, kp):
@@ -220,20 +268,15 @@ def tile_compositionalkoopmanoperators_pa_kernel(
             words = wide[m][:].bitcast(F32)
             for u in range(2):
                 for s in range(2):
-                    if m in apart:
-                        first = K_PASS * u + P * (2 * s + kp)
-                        rows = words[:, first : first + P]
-                    else:
-                        first = K_PASS * s + 256 * kp
-                        rows = words[:, first + u : first + 256 : 2]
-                    nc.tensor.transpose(turned[m, kp][:, u, s, :], rows, ident[:])
+                    first = K_PASS * u + P * (2 * s + kp)
+                    nc.tensor.transpose(turned[m, kp][:, u, s, :], words[:, first : first + P], ident[:])
 
-        def open_group(m, kp):
-            if (m % 2, kp) == (0, 0):
+        def open_group(m):
+            if m // 2 not in rel_laid:
                 rel_laid[m // 2] = rotating([P, PASSES, 2, 2 * P * 4], BF16, "rel_laid", 2)
 
         def scale_out(m, kp):
-            open_group(m, kp)
+            open_group(m)
             values = turned[m, kp][:].rearrange("p u s r -> p (u s r)").bitcast(BF16)
             factors = scale[:, kp, :].rearrange("p (u e) -> p u e", u=2)
             nc.vector.tensor_tensor(
@@ -243,11 +286,11 @@ def tile_compositionalkoopmanoperators_pa_kernel(
                 op=ALU.mult,
             )
 
-        def copy_out(m, kp, count, copy):
-            open_group(m, kp)
+        def copy_out(m, kp, count):
+            open_group(m)
             if kp == 0:
                 plain[m] = rotating([P, count, 2 * P * 4], BF16, "plain", 1)
-            copy(
+            nc.scalar.copy(
                 out=plain[m][:, kp, :].bitcast(F32).rearrange("p (x u) -> p x u", u=2),
                 in_=turned[m, kp][:].rearrange("p u s r -> p (s r) u"),
             )
@@ -268,12 +311,67 @@ def tile_compositionalkoopmanoperators_pa_kernel(
             )
 
         agg = [psum.tile([P, 4, P], F32, name="agg%d" % h, tag="agg%d" % h) for h in range(2)]
+        clamped = {}
+        for q in range(CHUNKS):
+            if q in ZFROM:
+                clamped[q] = (ZFROM[q], GROUPS)
+            if q in CFROM:
+                clamped[q] = (CFROM[q], GROUPS)
+            if q in DRANGE:
+                clamped[q] = DRANGE[q]
+        to_sum = [4 * N + len([q for q in clamped if q // 4 == h]) for h in range(2)]
         summed = [0, 0]
         acc = {}
         eff = {}
+        floor = {}
+        back = {}
 
         def eff_tile():
-            return rotating([P, SENDERS, P], F32, "eff", 4 * BURST)
+            return rotating([P, SENDERS, P], F32, "eff", EFF)
+
+        def sender_terms(tile_, g):
+            return (
+                tile_.rearrange("p (b j) -> p j b", b=GRAPHS)[:, SENDERS * g : SENDERS * (g + 1), :]
+                .unsqueeze(3)
+                .to_broadcast([P, SENDERS, GRAPHS, N])
+            )
+
+        def build_floor(g, q):
+            floor[g, q] = rotating([P, SENDERS, P], F32, "floor", FLOORS)
+            nc.gpsimd.tensor_tensor(
+                out=floor[g, q][:].rearrange("p s (b i) -> p s b i", b=GRAPHS),
+                in0=minus[q][:].rearrange("p (b i) -> p b i", b=GRAPHS).unsqueeze(1).to_broadcast([P, SENDERS, GRAPHS, N]),
+                in1=sender_terms(send[q // 2][:, q % 2, :], g),
+                op=ALU.subtract,
+            )
+
+        def build_back(q):
+            lo, hi = clamped[q]
+            sums = kept([P, GRAPHS], F32, "sums%d" % q)
+            back[q] = kept([P, P], F32, "back%d" % q)
+            nc.vector.tensor_reduce(
+                out=sums[:],
+                in_=send[q // 2][:, q % 2, :].rearrange("p (b j) -> p b j", b=GRAPHS)[:, :, SENDERS * lo : SENDERS * hi],
+                axis=AX.X,
+                op=ALU.add,
+            )
+            return sums
+
+        def finish_back(q, sums):
+            lo, hi = clamped[q]
+            nc.vector.scalar_tensor_tensor(
+                out=back[q][:].rearrange("p (b i) -> p b i", b=GRAPHS),
+                in0=recv[q // 2][:, q % 2, :].rearrange("p (b i) -> p b i", b=GRAPHS),
+                scalar=float(SENDERS * (hi - lo)) if q in ZFROM else 0.0,
+                in1=sums[:].unsqueeze(2).to_broadcast([P, GRAPHS, N]),
+                op0=ALU.mult,
+                op1=ALU.add,
+            )
+
+        def backs(qs):
+            sums = [build_back(q) for q in qs]
+            for q, sm in zip(qs, sums):
+                finish_back(q, sm)
 
         def product(g, q, folded):
             acc[g, q] = bank_tile([P, SENDERS, P], F32)
@@ -312,6 +410,21 @@ def tile_compositionalkoopmanoperators_pa_kernel(
                 op=ALU.add,
             )
 
+        def clamp_floor(g, q):
+            eff[g, q] = eff_tile()
+            nc.vector.tensor_tensor(out=eff[g, q][:], in0=acc[g, q][:], in1=floor[g, q][:], op=ALU.max)
+
+        def clamp_senders(g, q, folded):
+            if folded:
+                eff[g, q] = eff_tile()
+            src = acc[g, q] if folded else eff[g, q]
+            nc.vector.tensor_tensor(
+                out=eff[g, q][:].rearrange("p s (b i) -> p s b i", b=GRAPHS),
+                in0=src[:].rearrange("p s (b i) -> p s b i", b=GRAPHS),
+                in1=sender_terms(minus[q][:], g),
+                op=ALU.max,
+            )
+
         def relu_senders(g, q, folded, on_vector):
             if folded:
                 eff[g, q] = eff_tile()
@@ -333,18 +446,23 @@ def tile_compositionalkoopmanoperators_pa_kernel(
                     else:
                         nc.scalar.activation(eff[g, q][:, s, cols], src[:, s, cols], ACT.Relu, bias=bias)
 
-        def sum_senders(g, q):
+        def add_rows(q, rows):
             h = q // 4
+            nc.tensor.matmul(
+                out=agg[h][:, q % 4, :],
+                lhsT=rows,
+                rhs=ident[:],
+                is_transpose=True,
+                start=(summed[h] == 0),
+                stop=(summed[h] == to_sum[h] - 1),
+            )
+            summed[h] = summed[h] + 1
+
+        def sum_senders(g, q):
             for s in range(SENDERS):
-                nc.tensor.matmul(
-                    out=agg[h][:, q % 4, :],
-                    lhsT=eff[g, q][:, s, :],
-                    rhs=ident[:],
-                    is_transpose=True,
-                    start=(summed[h] == 0),
-                    stop=(summed[h] == 4 * N - 1),
-                )
-                summed[h] = summed[h] + 1
+                add_rows(q, eff[g, q][:, s, :])
+            if q in clamped and g == clamped[q][1] - 1:
+                add_rows(q, back[q][:])
 
         agg_rows = {}
         agg_bank = {}
@@ -355,11 +473,16 @@ def tile_compositionalkoopmanoperators_pa_kernel(
 
         def round_agg(h):
             agg_rows[h] = kept([P, K_PASS], BF16, "agg_rows%d" % h)
-            nc.vector.tensor_copy(out=agg_rows[h][:], in_=agg[h][:].rearrange("p q f -> p (q f)"))
+            nc.vector.tensor_copy(
+                out=agg_rows[h][:].rearrange("p (u x e) -> p u x e", u=2, e=2),
+                in_=agg[h][:].rearrange("p q f -> p (q f)").rearrange("p (x u e) -> p u x e", u=2, e=2),
+            )
 
         def turn_agg(h):
             agg_bank[h] = bank_tile([P, 2, P], F32)
-            turn_rows(agg_rows[h][:], agg_bank[h], 1)
+            words = agg_rows[h][:].bitcast(F32)
+            for u in range(2):
+                nc.tensor.transpose(agg_bank[h][:, u, :], words[:, P * u : P * (u + 1)], ident[:])
 
         def lay_agg(h):
             agg_laid[h] = kept([P, 4 * P], BF16, "agg_laid%d" % h)
@@ -421,10 +544,13 @@ def tile_compositionalkoopmanoperators_pa_kernel(
         widen(1)
         scale_out(0, 0)
         quantise_pieces(first_r)
-        turn(1, 0)
         obj_bank = bank_tile([P, 4, P], F32)
-        turn_rows(obj_sb[:], obj_bank, PASSES)
-        turn(1, 1)
+        obj_words = obj_sb[:].bitcast(F32)
+        for kp in range(PASSES):
+            for u in range(2):
+                nc.tensor.transpose(obj_bank[:, 2 * kp + u, :], obj_words[:, 256 * kp + u : 256 * (kp + 1) : 2], ident[:])
+        for kp in range(PASSES):
+            turn(1, kp)
         bias_bank = bank_tile([P, P], BF16)
         nc.tensor.transpose(bias_bank[:], bias_rows[:].bitcast(BF16), ident_bf[:])
         run_job(first_s, last=False)
@@ -436,9 +562,15 @@ def tile_compositionalkoopmanoperators_pa_kernel(
             in_=obj_bank[:].rearrange("p (g u) r -> p g r u", g=PASSES),
         )
         for x in range(PASSES):
-            lay(first_i, x, nc.scalar.copy, last=True)
+            if WEAVE0:
+                weave(first_i[x])
+                lay_woven(first_i, x, last=True)
+            else:
+                lay(first_i, x, nc.scalar.copy, last=True)
         nc.scalar.copy(out=bias_cols[:], in_=bias_bank[:, 0:CHUNKS])
-        widen(2)
+        load_pair(3)
+        for m in (2, 3):
+            widen(m)
         for kp in range(PASSES):
             turn(2, kp)
         nc.vector.quantize_mx(out=obj_codes[:].bitcast(FP8X4), scales=obj_scales[:], in_=obj_laid[:])
@@ -449,121 +581,183 @@ def tile_compositionalkoopmanoperators_pa_kernel(
         pieces = [(key, kp, c) for c in range(1, SETS) for key in ("i", "s", "r") for kp in range(PASSES)]
         pieces += [(key, kp, c) for key in ("o", "a") for kp in range(PASSES) for c in range(SETS)]
         per_set = 3 * PASSES
-        job, others = tuple(pieces[: per_set - ON_SCALAR]), tuple(pieces[per_set - ON_SCALAR : per_set])
+        job, two = tuple(pieces[:4]), tuple(pieces[4:6])
         pieces = pieces[per_set:]
-        load_pair(3)
         load_job(job)
         load_pair(4)
-        load_pieces(others)
-        run_job(job)
-        for m in (3, 4):
-            widen(m)
-            for kp in range(PASSES):
-                scale_out(m - 1, kp)
-            for kp in range(PASSES):
-                turn(m, kp)
-            if m == 3:
-                term_products(0)
+        load_pieces(two)
         load_pair(5)
-        product(0, 0, True)
-        for x in range(ON_SCALAR):
-            lay(others, x, nc.scalar.copy)
-        copy_terms(0)
-        product(0, 1, True)
-        widen(5)
+        run_job(job)
+        term_products(0)
         for kp in range(PASSES):
-            relu_senders(0, kp, True, 0)
-            scale_out(4, kp)
+            turn(3, kp)
+        for m in (2, 3):
+            for kp in range(PASSES):
+                scale_out(m, kp)
+        widen(4)
+        copy_terms(0)
+        widen(5)
+        product(0, 0, True)
+        for kp in range(PASSES):
+            turn(4, kp)
+        product(0, 1, True)
         for kp in range(PASSES):
             turn(5, kp)
+        for x in range(2):
+            lay(two, x, nc.scalar.copy)
+            relu_senders(0, x, True, 0)
+        for kp in range(PASSES):
+            scale_out(4, kp)
         sum_senders(0, 0)
         quantise_group(1)
-        quantise_pieces(others)
+        quantise_pieces(two)
         quantise_pieces(job)
+
+        job, two = tuple(pieces[:4]), tuple(pieces[4:6])
+        pieces = pieces[per_set:]
+        load_pair(6)
+        load_job(job)
+        load_pair(7)
+        load_pieces(two)
+        load_pair(8)
+        run_job(job)
+        widen(6)
+        product(1, 0, True)
+        product(1, 1, True)
+        relu_senders(1, 0, True, 0)
+        for kp in range(PASSES):
+            scale_out(5, kp)
+        for kp in range(PASSES):
+            turn(6, kp)
+        widen(7)
+        relu_senders(1, 1, True, 0)
+        term_products(1)
+        copy_terms(1)
+        product(0, 2, True)
+        for kp in range(PASSES):
+            scale_out(6, kp)
+        for kp in range(PASSES):
+            turn(7, kp)
         sum_senders(0, 1)
+        sum_senders(1, 0)
+        lay(two, 0, nc.scalar.copy)
+        relu_senders(0, 2, True, 0)
+        product(0, 3, True)
+        product(1, 2, True)
+        lay(two, 1, nc.scalar.copy)
+        widen(8)
+        for kp in range(PASSES):
+            scale_out(7, kp)
+        relu_senders(0, 3, True, 0)
+        product(1, 3, True)
+        quantise_group(2)
+        quantise_group(3)
+        quantise_pieces(two)
+        quantise_pieces(job)
+        relu_senders(1, 2, True, 0)
+        relu_senders(1, 3, True, 0)
+        for kp in range(PASSES):
+            turn(8, kp)
+        sum_senders(1, 1)
+        sum_senders(0, 2)
 
         plan = {}
 
         def at(beat, rank, fn, *args):
             plan.setdefault((beat, rank), []).append((fn, args))
 
-        for kp in range(PASSES):
-            at(0, SCALE, scale_out, 5, kp)
-        at(ROUND, CLOSE, quantise_group, 2)
-        group_ready = {0: -1, 1: 0, 2: ROUND + 1}
-        on_gpsimd = {}
-        for g in range(3, GROUPS):
-            end = ROUND * (g - 2)
-            on_gpsimd[g] = PASSES if g >= GROUPS - BOTH_BANKS else 1
-            copy = nc.scalar.copy if g > 3 else nc.vector.tensor_copy
-            for n in range(ROUND):
-                m, kp = 2 * g + n // PASSES, n % PASSES
-                beat = end - ROUND + 1 + n
-                if kp == 0 and m in apart:
-                    at(end - ROUND - AHEAD, LOAD, load_pair, m)
-                    at(end - ROUND, LAY, widen_apart, m)
-                elif kp == 0:
-                    at(beat - 2 - AHEAD, LOAD, load_pair, m)
-                    at(beat - 2, WIDEN, widen, m)
-                at(beat - 1, TURN, turn, m, kp)
-                if n < on_gpsimd[g]:
-                    at(beat, SCALE, copy_out, m, kp, on_gpsimd[g], copy)
-                else:
-                    at(beat, SCALE, scale_out, m, kp)
-            at(end - ROUND + on_gpsimd[g], GPSIMD, scale_plain, 2 * g, on_gpsimd[g])
-            at(end, CLOSE, quantise_group, g)
-            group_ready[g] = end + 1
-        supplied = group_ready[GROUPS - 1]
+        at(0, SUM, sum_senders, 0, 3)
+        at(0, SUM, sum_senders, 1, 2)
+        at(1, SUM, sum_senders, 1, 3)
+        count = []
+        opens = {}
+        closes = {0: -2, 1: -2, 2: -2, 3: -1}
+        banks = [(m, kp) for m in range(8, PAIRS) for kp in range(PASSES)]
+        for r in range(4, GROUPS):
+            opens[r] = len(count)
+            for units_, here in BEATS.get(r, STEADY):
+                beat = len(count)
+                count.append(units_)
+                for m, kp in banks[:here]:
+                    if m > 8:
+                        at(beat - 1, TURN, turn, m, kp)
+                    if m > 8 and kp == 0:
+                        at(beat - 2 - LOAD_AHEAD, LOAD, load_pair, m)
+                        at(max(beat - 2, 0), WIDEN_RANK if beat > 1 else COPY_OUT, widen, m)
+                    if m % 2 == 0 and kp < GS[m // 2]:
+                        at(beat, COPY_OUT, copy_out, m, kp, GS[m // 2])
+                        if kp == GS[m // 2] - 1:
+                            at(beat, GPSIMD, scale_plain, m, GS[m // 2])
+                    else:
+                        at(beat, SCALE, scale_out, m, kp)
+                banks = banks[here:]
+            closes[r] = len(count) - 1
+            at(closes[r], CLOSE, quantise_group, r)
+        supplied = len(count)
+        count.extend(LAST)
 
-        for g in range(3, GROUPS):
-            start, end = group_ready[g - 1] if g > 3 else 0, group_ready[g] - 1
-            size = per_set - ON_SCALAR * on_gpsimd[g]
-            job, pieces = tuple(pieces[:size]), pieces[size:]
-            at(start - ROUND, LOAD, load_job, job)
-            at(start - 1, GPSIMD, run_job, job)
-            if g - 1 < SETS:
-                others, pieces = tuple(pieces[:ON_SCALAR]), pieces[ON_SCALAR:]
-                at(start - 1, LOAD, load_pieces, others)
-                for x in range(ON_SCALAR):
-                    at(start + 2 * x, LAY, lay, others, x, nc.scalar.copy)
-                at(end, CLOSE, quantise_pieces, others)
-            at(end, CLOSE, quantise_pieces, job)
-        first_a, second_a = tuple(pieces[:SETS]), tuple(pieces[SETS:])
-        at(supplied - ROUND, LOAD, load_job, first_a)
-        at(supplied - 1, GPSIMD, run_job, first_a)
-        at(supplied + LAST_JOB - ROUND, LOAD, load_job, second_a)
-        at(supplied + LAST_JOB - 1, CLOSE, quantise_pieces, first_a)
-        at(supplied + LAST_JOB - 1, GPSIMD, run_job, second_a)
+        for r in range(4, GROUPS):
+            job, pieces = tuple(pieces[: JOB[r]]), pieces[JOB[r] :]
+            at(opens[r] - 3, LOAD, load_job, job)
+            at(opens[r] - 1, GPSIMD, run_job, job)
+            if r == 4:
+                others, pieces = tuple(pieces[: per_set - JOB[r]]), pieces[per_set - JOB[r] :]
+                at(opens[r] - 2, LOAD, load_pieces, others)
+                for x in range(len(others)):
+                    at(opens[r] - 1, GPSIMD, lay_gpsimd, others, x)
+                at(closes[r], CLOSE, quantise_pieces, others)
+            at(closes[r], CLOSE, quantise_pieces, job)
+        beat = supplied - 1
+        while pieces:
+            job, pieces = tuple(pieces[:SETS]), pieces[SETS:]
+            at(beat - 2, LOAD, load_job, job)
+            at(beat, GPSIMD, run_job, job)
+            beat = beat + PA_GAP
+            at(beat, CLAMP, quantise_pieces, job)
         at(supplied, LOAD, load_out_bias)
+        set_ready = {0: -2, 1: -2}
+        for c in range(2, SETS):
+            set_ready[c] = closes[c + 1] + 2
+            at(closes[c + 1] + 1, TERMS_RANK, term_products, c)
+            at(closes[c + 1] + 1, TERMS_COPY, copy_terms, c)
+        if clamped:
+            at(closes[SETS + 1], BACKS, backs, sorted(clamped))
 
-        set_ready = {0: -1}
-        for c in range(1, SETS):
-            beat = 0 if c == 1 else group_ready[c + 1] + 1
-            at(beat, TERMS, term_products, c)
-            at(beat, COPY_TERMS, copy_terms, c)
-            set_ready[c] = beat + 1
-
-        units = [(g, q) for h in range(2) for g in range(GROUPS) for q in range(4 * h, 4 * h + 4)][2:]
+        units = [(g, q) for h in range(2) for g in range(GROUPS) for q in range(4 * h, 4 * h + 4) if g > 1 or q > 3]
         beat = 0
         last_sum = [0, 0]
         while units:
-            ready = [(g, q) for g, q in units if max(group_ready[g], set_ready[q // 2]) < beat]
-            ready += [(g, q) for g, q in units if max(group_ready[g], set_ready[q // 2]) == beat]
-            count = 1 if beat < ROUND else BURST - (beat % 2 == 0 and beat < supplied)
-            for g, q in ready[:count]:
+            ready = [(g, q) for g, q in units if max(closes[g] + 1, set_ready[q // 2]) < beat]
+            ready += [(g, q) for g, q in units if max(closes[g] + 1, set_ready[q // 2]) == beat]
+            burst = ready[: count[beat]]
+            for n, (g, q) in enumerate(burst):
                 units = [unit for unit in units if unit != (g, q)]
-                folded = beat % ROUND == 0 and 0 < beat <= (SETS - 2) * ROUND and (g, q) == ready[count - 1]
-                at(beat, MULTIPLY, product, g, q, folded)
-                if not folded:
+                inside = q in clamped and clamped[q][0] <= g < clamped[q][1]
+                lag = SUM_LAG + (n >= SUM_SPLIT)
+                if inside and q in ZFROM:
+                    at(closes[g - 1] + 1, GPSIMD, build_floor, g, q)
+                    at(beat, MULTIPLY, product, g, q, False)
+                    at(beat, ADD, clamp_floor, g, q)
+                elif inside and q in DRANGE:
+                    at(beat, MULTIPLY, product, g, q, True)
+                    at(beat, ADD, clamp_senders, g, q, True)
+                elif inside:
+                    at(beat, MULTIPLY, product, g, q, False)
                     at(beat, ADD, add_receivers, g, q)
-                at(beat + 1, RELU, relu_senders, g, q, folded, SENDERS // 2 if len(units) < 2 else 0)
-                at(beat + 2, SUM, sum_senders, g, q)
-                last_sum[q // 4] = beat + 2
+                    at(beat, CLAMP, clamp_senders, g, q, False)
+                else:
+                    folded = n < NFOLD.get(beat, 0)
+                    at(beat, MULTIPLY, product, g, q, folded)
+                    if not folded:
+                        at(beat, ADD, add_receivers, g, q)
+                    late = n >= RELU_SPLIT and not folded
+                    at(beat + late, LATE if late else RELU, relu_senders, g, q, folded, SENDERS // 2 if len(units) < SHARE_LAST else 0)
+                at(beat + lag, SUM, sum_senders, g, q)
+                last_sum[q // 4] = max(last_sum[q // 4], beat + lag)
             beat = beat + 1
 
         at(last_sum[0] + 1, SCALE, round_agg, 0)
         at(beat, MULTIPLY, final_pass, "o", 0)
-        at(last_sum[1], CLOSE, quantise_pieces, second_a)
 
         for place in sorted(plan):
             for fn, args in plan[place]:

@@ -19,29 +19,44 @@ RUN = 8
 OUT_PARTS = 4
 BANKS = 6
 
-BEATS = {}
-STEADY = [(4, 2), (4, 2), (4, 0)]
+BEATS = {4: [(3, 0), (3, 1), (3, 1), (2, 1), (2, 1)]}
+STEADY = [(3, 1)] * 4
 WEAVE0 = False
 GFIRST = False
-LAST = [4, 4, 4, 4]
+LAST = [4, 2, 2]
 GS = [0, 0, 0, 0, 0, 1, 1, 1]
-JOB = [2, 4, 4, 4, 4, 4, 4, 4]
+JOB = [0, 0, 0, 0, 4, 4, 4, 4]
 REST = {2: "S", 3: "G"}
-ZFROM = {0: 5}
-CFROM = {}
+ZFROM = {}
+CFROM = {0: (4, 6), 6: (7, 8), 7: (7, 8)}
 DRANGE = {}
 NFOLD = {}
 SUM_LAG = 1
 SUM_SPLIT = 0
 RELU_SPLIT = 0
 EFF = 12
-SHARE_LAST = 2
-PA_GAP = 2
+SHARE_LAST = 0
+PA_GAP = 3
 TERMS_RANK = 6
 TERMS_COPY = 15
 LOAD_AHEAD = 2
 WIDEN_RANK = 7
 FLOORS = 2
+PARTS = 2
+FOLD2 = False
+FOLD3 = False
+EXTRA = [0, 0, 0, 0, 2, 0, 0, 0]
+CTO = 6
+Q_TAIL = True
+Q_RANK = 16
+R0_RANK = 3
+BEFORE = 3
+SUMS = 3
+WIDEN_AHEAD = 3
+TERMS_LATE = 1
+VLAY = [0] * 8
+O_AT = [0, 2]
+APART = range(16)
 
 F32 = mybir.dt.float32
 BF16 = mybir.dt.bfloat16
@@ -55,7 +70,7 @@ AX = mybir.AxisListType
 
 FLOPS = 2 * GRAPHS * N * N * NF * NF + 4 * 2 * GRAPHS * N * NF * NF
 
-LOAD, TURN0, COPY_OUT, SCALE, TERMS, MULTIPLY, COPY_TERMS, WIDEN, BACKS, LAY, CLOSE, GPSIMD, LATE, ADD, CLAMP, RELU, WEAVES, TURN, SUM = range(19)
+LOAD, TURN0, COPY_OUT, SCALE, TERMS, MULTIPLY, COPY_TERMS, WIDEN, LAY, LATE, ADD, BACKS, CLOSE, GPSIMD, CLAMP, RELU, WEAVES, TURN, COPY2, LATER, SUM = range(21)
 
 
 def tile_compositionalkoopmanoperators_pa_kernel(
@@ -166,16 +181,18 @@ def tile_compositionalkoopmanoperators_pa_kernel(
                 op1=ALU.add,
             )
 
-        def run_job(job, last=True):
+        def run_job(job, last=True, parts=1):
             laid[job] = laid_tile(job, last)
-            nc.gpsimd.tensor_scalar(
-                out=laid[job][:].rearrange("p x (n t) -> p x n t", t=4),
-                in0=w_raw[job][:].rearrange("p x t n -> p x n t"),
-                scalar1=1.0,
-                scalar2=0.0,
-                op0=ALU.mult,
-                op1=ALU.add,
-            )
+            size = len(job) // parts
+            for first in range(0, len(job), size):
+                nc.gpsimd.tensor_scalar(
+                    out=laid[job][:, first : first + size].rearrange("p x (n t) -> p x n t", t=4),
+                    in0=w_raw[job][:, first : first + size].rearrange("p x t n -> p x n t"),
+                    scalar1=1.0,
+                    scalar2=0.0,
+                    op0=ALU.mult,
+                    op1=ALU.add,
+                )
 
         def quantise_pieces(pieces):
             name = "%s%d%d" % pieces[0]
@@ -258,18 +275,26 @@ def tile_compositionalkoopmanoperators_pa_kernel(
 
         def widen(m):
             wide[m] = rotating([P, 2 * NF], BF16, "wide", 3)
-            nc.scalar.copy(
-                out=wide[m][:].rearrange("q (u x e) -> q u x e", u=2, e=2),
-                in_=rel_raw[m][:].bitcast(FP8).rearrange("q (x u e) -> q u x e", u=2, e=2),
-            )
+            if m in APART:
+                nc.scalar.copy(
+                    out=wide[m][:].rearrange("q (u x e) -> q u x e", u=2, e=2),
+                    in_=rel_raw[m][:].bitcast(FP8).rearrange("q (x u e) -> q u x e", u=2, e=2),
+                )
+            else:
+                nc.scalar.copy(out=wide[m][:], in_=rel_raw[m][:].bitcast(FP8))
 
         def turn(m, kp):
             turned[m, kp] = bank_tile([P, 2, 2, P], F32)
             words = wide[m][:].bitcast(F32)
             for u in range(2):
                 for s in range(2):
-                    first = K_PASS * u + P * (2 * s + kp)
-                    nc.tensor.transpose(turned[m, kp][:, u, s, :], words[:, first : first + P], ident[:])
+                    if m in APART:
+                        first = K_PASS * u + P * (2 * s + kp)
+                        rows = words[:, first : first + P]
+                    else:
+                        first = K_PASS * s + 256 * kp
+                        rows = words[:, first + u : first + 256 : 2]
+                    nc.tensor.transpose(turned[m, kp][:, u, s, :], rows, ident[:])
 
         def open_group(m):
             if m // 2 not in rel_laid:
@@ -316,7 +341,7 @@ def tile_compositionalkoopmanoperators_pa_kernel(
             if q in ZFROM:
                 clamped[q] = (ZFROM[q], GROUPS)
             if q in CFROM:
-                clamped[q] = (CFROM[q], GROUPS)
+                clamped[q] = CFROM[q]
             if q in DRANGE:
                 clamped[q] = DRANGE[q]
         to_sum = [4 * N + len([q for q in clamped if q // 4 == h]) for h in range(2)]
@@ -401,8 +426,8 @@ def tile_compositionalkoopmanoperators_pa_kernel(
                         stop=(kp == PASSES - 1 and s == SENDERS - 1),
                     )
 
-        def add_receivers(g, q):
-            eff[g, q] = eff_tile()
+        def add_receivers(g, q, held=False):
+            eff[g, q] = rotating([P, SENDERS, P], F32, "held", 2) if held else eff_tile()
             nc.vector.tensor_tensor(
                 out=eff[g, q][:],
                 in0=acc[g, q][:],
@@ -561,36 +586,42 @@ def tile_compositionalkoopmanoperators_pa_kernel(
             out=obj_laid[:].bitcast(F32).rearrange("p (g r u) -> p g r u", g=PASSES, u=2),
             in_=obj_bank[:].rearrange("p (g u) r -> p g r u", g=PASSES),
         )
-        for x in range(PASSES):
-            if WEAVE0:
-                weave(first_i[x])
-                lay_woven(first_i, x, last=True)
-            else:
-                lay(first_i, x, nc.scalar.copy, last=True)
         nc.scalar.copy(out=bias_cols[:], in_=bias_bank[:, 0:CHUNKS])
+        pieces = [(key, kp, c) for c in range(1, SETS) for key in ("i", "s", "r") for kp in range(PASSES)]
+        pieces += [(key, kp, c) for key in ("o", "a") for kp in range(PASSES) for c in range(SETS)]
+        per_set = 3 * PASSES
+        job, two = tuple(pieces[:4]), tuple(pieces[4:6])
+        next_job, next_two = tuple(pieces[6:10]), tuple(pieces[10:12])
+        pieces = pieces[2 * per_set :]
         load_pair(3)
-        for m in (2, 3):
-            widen(m)
+        load_pieces(two)
+        load_job(job)
+        load_pair(4)
+        load_pair(5)
+        load_pieces(next_two)
+        load_pair(6)
+        load_job(next_job)
+        for x in range(PASSES):
+            weave(first_i[x])
+        lay_woven(first_i, 0, last=True)
+        widen(2)
+        lay_woven(first_i, 1)
+        widen(3)
+        weave(two[0])
         for kp in range(PASSES):
             turn(2, kp)
+        weave(two[1])
+        for kp in range(PASSES):
+            turn(3, kp)
+        for x in range(2):
+            lay_woven(two, x)
         nc.vector.quantize_mx(out=obj_codes[:].bitcast(FP8X4), scales=obj_scales[:], in_=obj_laid[:])
         quantise_group(0)
         quantise_pieces(first_s)
         quantise_pieces(first_i)
 
-        pieces = [(key, kp, c) for c in range(1, SETS) for key in ("i", "s", "r") for kp in range(PASSES)]
-        pieces += [(key, kp, c) for key in ("o", "a") for kp in range(PASSES) for c in range(SETS)]
-        per_set = 3 * PASSES
-        job, two = tuple(pieces[:4]), tuple(pieces[4:6])
-        pieces = pieces[per_set:]
-        load_job(job)
-        load_pair(4)
-        load_pieces(two)
-        load_pair(5)
-        run_job(job)
+        run_job(job, parts=PARTS)
         term_products(0)
-        for kp in range(PASSES):
-            turn(3, kp)
         for m in (2, 3):
             for kp in range(PASSES):
                 scale_out(m, kp)
@@ -604,24 +635,23 @@ def tile_compositionalkoopmanoperators_pa_kernel(
         for kp in range(PASSES):
             turn(5, kp)
         for x in range(2):
-            lay(two, x, nc.scalar.copy)
             relu_senders(0, x, True, 0)
         for kp in range(PASSES):
             scale_out(4, kp)
+        for x in range(2):
+            weave(next_two[x])
+        widen(6)
+        for x in range(2):
+            lay_woven(next_two, x)
         sum_senders(0, 0)
         quantise_group(1)
         quantise_pieces(two)
         quantise_pieces(job)
 
-        job, two = tuple(pieces[:4]), tuple(pieces[4:6])
-        pieces = pieces[per_set:]
-        load_pair(6)
-        load_job(job)
+        job, two = next_job, next_two
         load_pair(7)
-        load_pieces(two)
         load_pair(8)
         run_job(job)
-        widen(6)
         product(1, 0, True)
         product(1, 1, True)
         relu_senders(1, 0, True, 0)
@@ -633,22 +663,25 @@ def tile_compositionalkoopmanoperators_pa_kernel(
         relu_senders(1, 1, True, 0)
         term_products(1)
         copy_terms(1)
-        product(0, 2, True)
+        product(0, 2, FOLD2)
+        product(0, 3, FOLD3)
         for kp in range(PASSES):
             scale_out(6, kp)
         for kp in range(PASSES):
             turn(7, kp)
         sum_senders(0, 1)
-        sum_senders(1, 0)
-        lay(two, 0, nc.scalar.copy)
-        relu_senders(0, 2, True, 0)
-        product(0, 3, True)
-        product(1, 2, True)
-        lay(two, 1, nc.scalar.copy)
+        if not FOLD2:
+            add_receivers(0, 2)
+        if not FOLD3:
+            add_receivers(0, 3)
         widen(8)
+        relu_senders(0, 2, FOLD2, 0)
+        product(1, 2, True)
+        sum_senders(1, 0)
+        sum_senders(1, 1)
         for kp in range(PASSES):
             scale_out(7, kp)
-        relu_senders(0, 3, True, 0)
+        relu_senders(0, 3, FOLD3, 0)
         product(1, 3, True)
         quantise_group(2)
         quantise_group(3)
@@ -656,20 +689,16 @@ def tile_compositionalkoopmanoperators_pa_kernel(
         quantise_pieces(job)
         relu_senders(1, 2, True, 0)
         relu_senders(1, 3, True, 0)
-        for kp in range(PASSES):
-            turn(8, kp)
-        sum_senders(1, 1)
         sum_senders(0, 2)
+        sum_senders(0, 3)
 
         plan = {}
 
         def at(beat, rank, fn, *args):
             plan.setdefault((beat, rank), []).append((fn, args))
 
-        at(0, SUM, sum_senders, 0, 3)
-        at(0, SUM, sum_senders, 1, 2)
-        at(1, SUM, sum_senders, 1, 3)
         count = []
+        copies = []
         opens = {}
         closes = {0: -2, 1: -2, 2: -2, 3: -1}
         banks = [(m, kp) for m in range(8, PAIRS) for kp in range(PASSES)]
@@ -679,20 +708,20 @@ def tile_compositionalkoopmanoperators_pa_kernel(
                 beat = len(count)
                 count.append(units_)
                 for m, kp in banks[:here]:
-                    if m > 8:
-                        at(beat - 1, TURN, turn, m, kp)
+                    at(beat - 1, TURN, turn, m, kp)
                     if m > 8 and kp == 0:
-                        at(beat - 2 - LOAD_AHEAD, LOAD, load_pair, m)
-                        at(max(beat - 2, 0), WIDEN_RANK if beat > 1 else COPY_OUT, widen, m)
+                        at(beat - WIDEN_AHEAD - LOAD_AHEAD, LOAD, load_pair, m)
+                        at(beat - WIDEN_AHEAD, WIDEN_RANK, widen, m)
                     if m % 2 == 0 and kp < GS[m // 2]:
-                        at(beat, COPY_OUT, copy_out, m, kp, GS[m // 2])
+                        at(beat - (BEFORE < 3), COPY2 if BEFORE < 3 else COPY_OUT, copy_out, m, kp, GS[m // 2])
+                        copies.append(beat - 1)
                         if kp == GS[m // 2] - 1:
                             at(beat, GPSIMD, scale_plain, m, GS[m // 2])
                     else:
                         at(beat, SCALE, scale_out, m, kp)
                 banks = banks[here:]
             closes[r] = len(count) - 1
-            at(closes[r], CLOSE, quantise_group, r)
+            at(closes[r], LAY if r == GROUPS - 1 else CLOSE, quantise_group, r)
         supplied = len(count)
         count.extend(LAST)
 
@@ -700,32 +729,43 @@ def tile_compositionalkoopmanoperators_pa_kernel(
             job, pieces = tuple(pieces[: JOB[r]]), pieces[JOB[r] :]
             at(opens[r] - 3, LOAD, load_job, job)
             at(opens[r] - 1, GPSIMD, run_job, job)
-            if r == 4:
-                others, pieces = tuple(pieces[: per_set - JOB[r]]), pieces[per_set - JOB[r] :]
+            if EXTRA[r]:
+                others, pieces = tuple(pieces[: EXTRA[r]]), pieces[EXTRA[r] :]
                 at(opens[r] - 2, LOAD, load_pieces, others)
                 for x in range(len(others)):
                     at(opens[r] - 1, GPSIMD, lay_gpsimd, others, x)
                 at(closes[r], CLOSE, quantise_pieces, others)
+            if VLAY[r]:
+                mine, pieces = tuple(pieces[: VLAY[r]]), pieces[VLAY[r] :]
+                at(opens[r], LOAD, load_pieces, mine)
+                for x in range(len(mine)):
+                    at(closes[r], BACKS, lay, mine, x, nc.vector.tensor_copy)
+                at(closes[r], CLOSE, quantise_pieces, mine)
             at(closes[r], CLOSE, quantise_pieces, job)
         beat = supplied - 1
+        last_job = None
         while pieces:
             job, pieces = tuple(pieces[:SETS]), pieces[SETS:]
             at(beat - 2, LOAD, load_job, job)
-            at(beat, GPSIMD, run_job, job)
+            at(beat, GPSIMD if beat < supplied else RELU, run_job, job)
             beat = beat + PA_GAP
-            at(beat, CLAMP, quantise_pieces, job)
+            if pieces or not Q_TAIL:
+                at(beat, CLAMP, quantise_pieces, job)
+            else:
+                last_job = job
         at(supplied, LOAD, load_out_bias)
         set_ready = {0: -2, 1: -2}
         for c in range(2, SETS):
-            set_ready[c] = closes[c + 1] + 2
-            at(closes[c + 1] + 1, TERMS_RANK, term_products, c)
-            at(closes[c + 1] + 1, TERMS_COPY, copy_terms, c)
+            set_ready[c] = closes[c + 1] + 2 + TERMS_LATE
+            at(closes[c + 1] + 1 + TERMS_LATE, TERMS_RANK, term_products, c)
+            at(closes[c + 1] + 1 + TERMS_LATE, TERMS_COPY, copy_terms, c)
         if clamped:
             at(closes[SETS + 1], BACKS, backs, sorted(clamped))
 
         units = [(g, q) for h in range(2) for g in range(GROUPS) for q in range(4 * h, 4 * h + 4) if g > 1 or q > 3]
         beat = 0
         last_sum = [0, 0]
+        waiting = [(0, 1, 2), (0, 1, 3)]
         while units:
             ready = [(g, q) for g, q in units if max(closes[g] + 1, set_ready[q // 2]) < beat]
             ready += [(g, q) for g, q in units if max(closes[g] + 1, set_ready[q // 2]) == beat]
@@ -741,23 +781,41 @@ def tile_compositionalkoopmanoperators_pa_kernel(
                 elif inside and q in DRANGE:
                     at(beat, MULTIPLY, product, g, q, True)
                     at(beat, ADD, clamp_senders, g, q, True)
-                elif inside:
+                elif inside and beat >= supplied:
                     at(beat, MULTIPLY, product, g, q, False)
                     at(beat, ADD, add_receivers, g, q)
-                    at(beat, CLAMP, clamp_senders, g, q, False)
+                    at(beat, RELU, clamp_senders, g, q, False)
+                    lag = 1 + (beat == supplied + 1)
+                elif inside:
+                    at(beat, MULTIPLY, product, g, q, False)
+                    at(beat, ADD, add_receivers, g, q, True)
+                    lag = min([closes[r] for r in closes if closes[r] >= beat] + [supplied - 1 + PA_GAP]) - beat
+                    at(beat + lag, BACKS if beat < supplied else RELU, clamp_senders, g, q, False)
+                    lag = lag + 1
                 else:
                     folded = n < NFOLD.get(beat, 0)
                     at(beat, MULTIPLY, product, g, q, folded)
                     if not folded:
                         at(beat, ADD, add_receivers, g, q)
                     late = n >= RELU_SPLIT and not folded
-                    at(beat + late, LATE if late else RELU, relu_senders, g, q, folded, SENDERS // 2 if len(units) < SHARE_LAST else 0)
-                at(beat + lag, SUM, sum_senders, g, q)
-                last_sum[q // 4] = max(last_sum[q // 4], beat + lag)
+                    at(beat + late, (LATER if beat + 1 in copies and n >= BEFORE else LATE) if late else RELU, relu_senders, g, q, folded, SENDERS // 2 if len(units) < SHARE_LAST else 0)
+                waiting.append((beat + lag, g, q))
             beat = beat + 1
+        when = 0
+        while waiting:
+            due = [entry for entry in sorted(waiting) if entry[0] <= when][: SUMS + (when >= supplied - 1)]
+            for entry in due:
+                waiting.remove(entry)
+                at(when, SUM, sum_senders, entry[1], entry[2])
+                last_sum[entry[2] // 4] = when
+            when = when + 1
 
-        at(last_sum[0] + 1, SCALE, round_agg, 0)
-        at(beat, MULTIPLY, final_pass, "o", 0)
+        at(last_sum[0] + 1, R0_RANK, round_agg, 0)
+        if last_job:
+            at(beat - 1, Q_RANK, quantise_pieces, last_job)
+        for kp in range(PASSES):
+            if O_AT[kp] < 2:
+                at(beat + O_AT[kp], MULTIPLY, final_pass, "o", kp)
 
         for place in sorted(plan):
             for fn, args in plan[place]:
@@ -765,7 +823,9 @@ def tile_compositionalkoopmanoperators_pa_kernel(
 
         turn_agg(0)
         round_agg(1)
-        final_pass("o", 1)
+        for kp in range(PASSES):
+            if O_AT[kp] == 2:
+                final_pass("o", kp)
         lay_agg(0)
         quantise_agg(0)
         turn_agg(1)

@@ -23,20 +23,20 @@ BEATS = {4: [(3, 0), (3, 1), (3, 1), (2, 1), (2, 1)]}
 STEADY = [(3, 1)] * 4
 WEAVE0 = False
 GFIRST = False
-LAST = [4, 2, 2]
-GS = [0, 0, 0, 0, 0, 1, 1, 1]
+LAST = [4, 2, 2, 2]
+GS = [0, 0, 0, 0, 1, 1, 1, 1]
 JOB = [0, 0, 0, 0, 4, 4, 4, 4]
 REST = {2: "S", 3: "G"}
 ZFROM = {}
-CFROM = {0: (4, 6), 6: (7, 8), 7: (7, 8)}
-DRANGE = {}
+CFROM = {6: (7, 8), 7: (7, 8)}
+DRANGE = {0: (3, 7)}
 NFOLD = {}
 SUM_LAG = 1
 SUM_SPLIT = 0
 RELU_SPLIT = 0
 EFF = 12
 SHARE_LAST = 0
-PA_GAP = 3
+PA_GAP = 2
 TERMS_RANK = 6
 TERMS_COPY = 15
 LOAD_AHEAD = 2
@@ -45,13 +45,19 @@ FLOORS = 2
 PARTS = 2
 FOLD2 = False
 FOLD3 = False
-EXTRA = [0, 0, 0, 0, 2, 0, 0, 0]
+EXTRA = [(), (), (), (), (2,), (1,), (1,), ()]
 CTO = 6
 Q_TAIL = True
 Q_RANK = 16
 R0_RANK = 3
 BEFORE = 3
 SUMS = 3
+G7 = 0
+QPOS = 3
+FOLD4 = True
+FOLD5 = True
+G3FIRST = False
+TAILQ = (6, 7)
 WIDEN_AHEAD = 3
 TERMS_LATE = 1
 VLAY = [0] * 8
@@ -653,42 +659,52 @@ def tile_compositionalkoopmanoperators_pa_kernel(
         load_pair(8)
         run_job(job)
         product(1, 0, True)
-        product(1, 1, True)
-        relu_senders(1, 0, True, 0)
+        term_products(1)
         for kp in range(PASSES):
             scale_out(5, kp)
-        for kp in range(PASSES):
-            turn(6, kp)
-        widen(7)
-        relu_senders(1, 1, True, 0)
-        term_products(1)
+        turn(6, 0)
+        sum_senders(0, 1)
+        turn(6, 1)
+        relu_senders(1, 0, True, 0)
         copy_terms(1)
+        widen(7)
+        product(1, 1, True)
         product(0, 2, FOLD2)
         product(0, 3, FOLD3)
+        relu_senders(1, 1, True, 0)
         for kp in range(PASSES):
             scale_out(6, kp)
         for kp in range(PASSES):
             turn(7, kp)
-        sum_senders(0, 1)
+        sum_senders(1, 0)
         if not FOLD2:
             add_receivers(0, 2)
         if not FOLD3:
             add_receivers(0, 3)
-        widen(8)
+        if G7:
+            copy_out(7, 0, 1)
+            scale_plain(7, 1)
         relu_senders(0, 2, FOLD2, 0)
-        product(1, 2, True)
-        sum_senders(1, 0)
+        widen(8)
+        product(1, 2, FOLD4)
+        product(1, 3, FOLD5)
         sum_senders(1, 1)
-        for kp in range(PASSES):
+        for kp in range(G7, PASSES):
             scale_out(7, kp)
         relu_senders(0, 3, FOLD3, 0)
-        product(1, 3, True)
+        if not FOLD4:
+            add_receivers(1, 2)
+        if not FOLD5:
+            add_receivers(1, 3)
         quantise_group(2)
-        quantise_group(3)
+        if G3FIRST:
+            quantise_group(3)
         quantise_pieces(two)
+        if not G3FIRST:
+            quantise_group(3)
         quantise_pieces(job)
-        relu_senders(1, 2, True, 0)
-        relu_senders(1, 3, True, 0)
+        relu_senders(1, 2, FOLD4, 0)
+        relu_senders(1, 3, FOLD5, 0)
         sum_senders(0, 2)
         sum_senders(0, 3)
 
@@ -729,8 +745,8 @@ def tile_compositionalkoopmanoperators_pa_kernel(
             job, pieces = tuple(pieces[: JOB[r]]), pieces[JOB[r] :]
             at(opens[r] - 3, LOAD, load_job, job)
             at(opens[r] - 1, GPSIMD, run_job, job)
-            if EXTRA[r]:
-                others, pieces = tuple(pieces[: EXTRA[r]]), pieces[EXTRA[r] :]
+            for size in EXTRA[r]:
+                others, pieces = tuple(pieces[:size]), pieces[size:]
                 at(opens[r] - 2, LOAD, load_pieces, others)
                 for x in range(len(others)):
                     at(opens[r] - 1, GPSIMD, lay_gpsimd, others, x)
@@ -784,8 +800,7 @@ def tile_compositionalkoopmanoperators_pa_kernel(
                 elif inside and beat >= supplied:
                     at(beat, MULTIPLY, product, g, q, False)
                     at(beat, ADD, add_receivers, g, q)
-                    at(beat, RELU, clamp_senders, g, q, False)
-                    lag = 1 + (beat == supplied + 1)
+                    lag = 99
                 elif inside:
                     at(beat, MULTIPLY, product, g, q, False)
                     at(beat, ADD, add_receivers, g, q, True)
@@ -802,34 +817,40 @@ def tile_compositionalkoopmanoperators_pa_kernel(
                 waiting.append((beat + lag, g, q))
             beat = beat + 1
         when = 0
-        while waiting:
+        while when < beat:
             due = [entry for entry in sorted(waiting) if entry[0] <= when][: SUMS + (when >= supplied - 1)]
             for entry in due:
                 waiting.remove(entry)
                 at(when, SUM, sum_senders, entry[1], entry[2])
-                last_sum[entry[2] // 4] = when
             when = when + 1
-
-        at(last_sum[0] + 1, R0_RANK, round_agg, 0)
-        if last_job:
-            at(beat - 1, Q_RANK, quantise_pieces, last_job)
-        for kp in range(PASSES):
-            if O_AT[kp] < 2:
-                at(beat + O_AT[kp], MULTIPLY, final_pass, "o", kp)
 
         for place in sorted(plan):
             for fn, args in plan[place]:
                 fn(*args)
 
-        turn_agg(0)
+        last = GROUPS - 1
+        if QPOS == 0 and last_job:
+            quantise_pieces(last_job)
+        for q in TAILQ:
+            clamp_senders(last, q, False)
+        round_agg(0)
+        if QPOS == 1 and last_job:
+            quantise_pieces(last_job)
+        final_pass("o", 0)
+        for entry in sorted(waiting):
+            if entry[2] == TAILQ[0]:
+                turn_agg(0)
+                lay_agg(0)
+                quantise_agg(0)
+            sum_senders(entry[1], entry[2])
+        if QPOS == 2 and last_job:
+            quantise_pieces(last_job)
         round_agg(1)
-        for kp in range(PASSES):
-            if O_AT[kp] == 2:
-                final_pass("o", kp)
-        lay_agg(0)
-        quantise_agg(0)
-        turn_agg(1)
+        if QPOS == 3 and last_job:
+            quantise_pieces(last_job)
+        final_pass("o", 1)
         final_pass("a", 0)
+        turn_agg(1)
         lay_agg(1)
         quantise_agg(1)
         final_pass("a", 1)

@@ -19,17 +19,17 @@ RUN = 8
 OUT_PARTS = 4
 BANKS = 6
 
-BEATS = {4: [(3, 0), (3, 1), (3, 1), (2, 1), (2, 1)]}
+BEATS = {4: [(3, 0), (3, 1), (3, 1), (2, 1), (2, 1)], 7: [(3, 2), (3, 1), (3, 1), (2, 0)]}
 STEADY = [(3, 1)] * 4
 WEAVE0 = False
 GFIRST = False
 LAST = [4, 2, 2, 2]
 GS = [0, 0, 0, 0, 1, 1, 1, 1]
-JOB = [0, 0, 0, 0, 4, 4, 4, 4]
+JOB = [0, 0, 0, 0, 4, 4, 4, 3]
 REST = {2: "S", 3: "G"}
 ZFROM = {}
-CFROM = {6: (7, 8), 7: (7, 8)}
-DRANGE = {0: (3, 7)}
+CFROM = {5: (7, 8), 6: (7, 8), 7: (7, 8)}
+DRANGE = {}
 NFOLD = {}
 SUM_LAG = 1
 SUM_SPLIT = 0
@@ -45,7 +45,7 @@ FLOORS = 2
 PARTS = 2
 FOLD2 = False
 FOLD3 = False
-EXTRA = [(), (), (), (), (2,), (1,), (1,), ()]
+EXTRA = [(), (), (), (), (1,), (1,), (1,), ()]
 CTO = 6
 Q_TAIL = True
 Q_RANK = 16
@@ -53,11 +53,15 @@ R0_RANK = 3
 BEFORE = 3
 SUMS = 3
 G7 = 0
+WIDE = 5
+SLAY = [0, 0, 0, 0, 1, 0, 0, 0]
+SOFF = 0
+BACKS_AT = 7
 QPOS = 3
 FOLD4 = True
 FOLD5 = True
 G3FIRST = False
-TAILQ = (6, 7)
+TAILQ = (5, 6, 7)
 WIDEN_AHEAD = 3
 TERMS_LATE = 1
 VLAY = [0] * 8
@@ -130,12 +134,13 @@ def tile_compositionalkoopmanoperators_pa_kernel(
                 nc.sync.dma_start(out=w_raw[job][:, x], in_=piece_rows(*piece))
 
         scale = kept([P, PASSES, 4], F32, "scale")
-        obj_sb = kept([P, NF], BF16, "obj_sb")
+        obj_sb = rotating([P, NF], BF16, "rows", 1)
         bias_rows = kept([P, P // 2], F32, "bias_rows")
-        out_bias = kept([P, NF], BF16, "out_bias")
+        out_bias = {}
 
         def load_out_bias():
-            nc.sync.dma_start(out=out_bias[:], in_=pp_b.partition_broadcast(P))
+            out_bias[0] = rotating([P, NF], BF16, "rows", 1)
+            nc.sync.dma_start(out=out_bias[0][:], in_=pp_b.partition_broadcast(P))
 
         nc.vector.memset(bias_rows[:], 0.0)
         ident_bf = kept([P, P], BF16, "ident_bf")
@@ -280,7 +285,7 @@ def tile_compositionalkoopmanoperators_pa_kernel(
         rel_scales = [kept([P, PASSES * SENDERS * P], U8, "rel_scales%d" % g) for g in range(GROUPS)]
 
         def widen(m):
-            wide[m] = rotating([P, 2 * NF], BF16, "wide", 3)
+            wide[m] = rotating([P, 2 * NF], BF16, "wide", WIDE)
             if m in APART:
                 nc.scalar.copy(
                     out=wide[m][:].rearrange("q (u x e) -> q u x e", u=2, e=2),
@@ -548,13 +553,13 @@ def tile_compositionalkoopmanoperators_pa_kernel(
             width = NF // OUT_PARTS
             cols = slice(width * n, width * (n + 1))
             h, first = divmod(width * n, K_PASS)
-            result = kept([P, width], F32, "result%d" % n)
+            result = eff_tile()[:].rearrange("p s r -> p (s r)")[:, 0:width]
             nc.vector.tensor_tensor(
-                out=result[:], in0=final[h][:, first : first + width], in1=out_bias[:, cols], op=ALU.add
+                out=result, in0=final[h][:, first : first + width], in1=out_bias[0][:, cols], op=ALU.add
             )
-            nc.scalar.activation(result[:], result[:], ACT.Relu)
+            nc.scalar.activation(result, result, ACT.Relu)
             queue = nc.scalar if n == OUT_PARTS - 1 else nc.sync
-            queue.dma_start(out=out_rows[:, cols], in_=result[:])
+            queue.dma_start(out=out_rows[:, cols], in_=result)
 
         first_r, first_s, first_i = (tuple((key, kp, 0) for kp in range(PASSES)) for key in ("r", "s", "i"))
         load_pair(0)
@@ -605,7 +610,8 @@ def tile_compositionalkoopmanoperators_pa_kernel(
         load_pair(4)
         load_pair(5)
         load_pieces(next_two)
-        load_pair(6)
+        for m in range(6, 10):
+            load_pair(m)
         load_job(next_job)
         for x in range(PASSES):
             weave(first_i[x])
@@ -655,9 +661,10 @@ def tile_compositionalkoopmanoperators_pa_kernel(
         quantise_pieces(job)
 
         job, two = next_job, next_two
-        load_pair(7)
-        load_pair(8)
+        load_pair(10)
+        load_pair(11)
         run_job(job)
+        widen(7)
         product(1, 0, True)
         term_products(1)
         for kp in range(PASSES):
@@ -667,7 +674,8 @@ def tile_compositionalkoopmanoperators_pa_kernel(
         turn(6, 1)
         relu_senders(1, 0, True, 0)
         copy_terms(1)
-        widen(7)
+        widen(8)
+        widen(9)
         product(1, 1, True)
         product(0, 2, FOLD2)
         product(0, 3, FOLD3)
@@ -685,7 +693,7 @@ def tile_compositionalkoopmanoperators_pa_kernel(
             copy_out(7, 0, 1)
             scale_plain(7, 1)
         relu_senders(0, 2, FOLD2, 0)
-        widen(8)
+        widen(10)
         product(1, 2, FOLD4)
         product(1, 3, FOLD5)
         sum_senders(1, 1)
@@ -705,6 +713,7 @@ def tile_compositionalkoopmanoperators_pa_kernel(
         quantise_pieces(job)
         relu_senders(1, 2, FOLD4, 0)
         relu_senders(1, 3, FOLD5, 0)
+        widen(11)
         sum_senders(0, 2)
         sum_senders(0, 3)
 
@@ -725,7 +734,7 @@ def tile_compositionalkoopmanoperators_pa_kernel(
                 count.append(units_)
                 for m, kp in banks[:here]:
                     at(beat - 1, TURN, turn, m, kp)
-                    if m > 8 and kp == 0:
+                    if m > 11 and kp == 0:
                         at(beat - WIDEN_AHEAD - LOAD_AHEAD, LOAD, load_pair, m)
                         at(beat - WIDEN_AHEAD, WIDEN_RANK, widen, m)
                     if m % 2 == 0 and kp < GS[m // 2]:
@@ -751,6 +760,12 @@ def tile_compositionalkoopmanoperators_pa_kernel(
                 for x in range(len(others)):
                     at(opens[r] - 1, GPSIMD, lay_gpsimd, others, x)
                 at(closes[r], CLOSE, quantise_pieces, others)
+            if SLAY[r]:
+                his, pieces = tuple(pieces[: SLAY[r]]), pieces[SLAY[r] :]
+                at(opens[r] - 2, LOAD, load_pieces, his)
+                for x in range(len(his)):
+                    at(opens[r] + 2 * x + SOFF, WIDEN, lay, his, x, nc.scalar.copy)
+                at(closes[r], CLOSE, quantise_pieces, his)
             if VLAY[r]:
                 mine, pieces = tuple(pieces[: VLAY[r]]), pieces[VLAY[r] :]
                 at(opens[r], LOAD, load_pieces, mine)
@@ -776,7 +791,7 @@ def tile_compositionalkoopmanoperators_pa_kernel(
             at(closes[c + 1] + 1 + TERMS_LATE, TERMS_RANK, term_products, c)
             at(closes[c + 1] + 1 + TERMS_LATE, TERMS_COPY, copy_terms, c)
         if clamped:
-            at(closes[SETS + 1], BACKS, backs, sorted(clamped))
+            at(closes[BACKS_AT], BACKS, backs, sorted(clamped))
 
         units = [(g, q) for h in range(2) for g in range(GROUPS) for q in range(4 * h, 4 * h + 4) if g > 1 or q > 3]
         beat = 0
@@ -829,30 +844,22 @@ def tile_compositionalkoopmanoperators_pa_kernel(
                 fn(*args)
 
         last = GROUPS - 1
-        if QPOS == 0 and last_job:
-            quantise_pieces(last_job)
         for q in TAILQ:
             clamp_senders(last, q, False)
         round_agg(0)
-        if QPOS == 1 and last_job:
-            quantise_pieces(last_job)
         final_pass("o", 0)
         for entry in sorted(waiting):
-            if entry[2] == TAILQ[0]:
-                turn_agg(0)
-                lay_agg(0)
-                quantise_agg(0)
             sum_senders(entry[1], entry[2])
-        if QPOS == 2 and last_job:
-            quantise_pieces(last_job)
         round_agg(1)
-        if QPOS == 3 and last_job:
-            quantise_pieces(last_job)
+        turn_agg(0)
+        lay_agg(0)
+        quantise_agg(0)
+        quantise_pieces(last_job)
         final_pass("o", 1)
-        final_pass("a", 0)
         turn_agg(1)
         lay_agg(1)
         quantise_agg(1)
+        final_pass("a", 0)
         final_pass("a", 1)
         for n in range(OUT_PARTS):
             finish(n)

@@ -29,7 +29,7 @@ JOB = [0, 0, 0, 0, 4, 4, 4, 3]
 REST = {2: "S", 3: "G"}
 ZFROM = {}
 CFROM = {5: (7, 8), 6: (7, 8), 7: (7, 8)}
-DRANGE = {}
+DRANGE = {0: (5, 6)}
 NFOLD = {}
 SUM_LAG = 1
 SUM_SPLIT = 0
@@ -54,7 +54,9 @@ BEFORE = 3
 SUMS = 3
 G7 = 0
 WIDE = 5
-SLAY = [0, 0, 0, 0, 1, 0, 0, 0]
+WIDEFOLD = True
+R2X = 1
+SLAY = [0] * 8
 SOFF = 0
 BACKS_AT = 7
 QPOS = 3
@@ -71,6 +73,7 @@ APART = range(16)
 F32 = mybir.dt.float32
 BF16 = mybir.dt.bfloat16
 U32 = mybir.dt.uint32
+I32 = mybir.dt.int32
 U8 = mybir.dt.uint8
 FP8 = mybir.dt.float8_e4m3fn
 FP8X4 = mybir.dt.float8_e4m3fn_x4
@@ -231,15 +234,29 @@ def tile_compositionalkoopmanoperators_pa_kernel(
             return piece_weights((key, kp, q // 2), P * (q % 2), P)
 
         obj_laid = kept([P, PASSES * P * 4], BF16, "obj_laid")
-        obj_codes = kept([P, PASSES * P], U32, "obj_codes")
-        obj_scales = kept([P, PASSES * P], U8, "obj_scales")
+        obj_codes = kept([P, PASSES, 2, P], U32, "obj_codes")
+        obj_scales = kept([P, PASSES, 2, P], U8, "obj_scales")
+        nc.vector.memset(obj_scales[:], 0)
+
+        def quantise_particles():
+            for kp in range(PASSES):
+                nc.vector.quantize_mx(
+                    out=obj_codes[:, kp, 0, :].bitcast(FP8X4),
+                    scales=obj_scales[:, kp, 0, :],
+                    in_=obj_laid[:, 4 * P * kp : 4 * P * (kp + 1)],
+                )
+
+        def repeat_particles():
+            nc.vector.tensor_copy(out=obj_codes[:, :, 1, :], in_=obj_codes[:, :, 0, :])
+            nc.vector.tensor_copy(out=obj_scales[:, :, 1, :].bitcast(U32), in_=obj_scales[:, :, 0, :].bitcast(U32))
+
         term_bank = {}
         recv = {}
         send = {}
         minus = {}
 
         def particles(kp):
-            return obj_codes[:, P * kp : P * (kp + 1)].bitcast(FP8X4), obj_scales[:, P * kp : P * (kp + 1)]
+            return obj_codes[:, kp, 0, :].bitcast(FP8X4), obj_scales[:, kp, 0, :]
 
         def term_products(c):
             term_bank[c] = bank_tile([P, 4, P], F32)
@@ -423,7 +440,19 @@ def tile_compositionalkoopmanoperators_pa_kernel(
                     start=(kp == 0),
                     stop=(kp == PASSES - 1 and not folded),
                 )
-            for kp in range(PASSES if folded else 0):
+            for kp in range(PASSES if folded and WIDEFOLD else 0):
+                wc, ws = chunk_weights("i", kp, q)
+                for s in range(0, SENDERS, 2):
+                    nc.tensor.matmul_mx(
+                        out=acc[g, q][:, s : s + 2, :].rearrange("p s r -> p (s r)"),
+                        lhsT=wc,
+                        lhsT_scale=ws,
+                        rhs=obj_codes[:, kp].rearrange("p s r -> p (s r)").bitcast(FP8X4),
+                        rhs_scale=obj_scales[:, kp].rearrange("p s r -> p (s r)"),
+                        start=False,
+                        stop=(kp == PASSES - 1 and s == SENDERS - 2),
+                    )
+            for kp in range(PASSES if folded and not WIDEFOLD else 0):
                 wc, ws = chunk_weights("i", kp, q)
                 oc, osc = particles(kp)
                 for s in range(SENDERS):
@@ -497,7 +526,7 @@ def tile_compositionalkoopmanoperators_pa_kernel(
         def sum_senders(g, q):
             for s in range(SENDERS):
                 add_rows(q, eff[g, q][:, s, :])
-            if q in clamped and g == clamped[q][1] - 1:
+            if q in clamped and g == GROUPS - 1:
                 add_rows(q, back[q][:])
 
         agg_rows = {}
@@ -627,8 +656,10 @@ def tile_compositionalkoopmanoperators_pa_kernel(
             turn(3, kp)
         for x in range(2):
             lay_woven(two, x)
-        nc.vector.quantize_mx(out=obj_codes[:].bitcast(FP8X4), scales=obj_scales[:], in_=obj_laid[:])
+        quantise_particles()
         quantise_group(0)
+        if WIDEFOLD:
+            repeat_particles()
         quantise_pieces(first_s)
         quantise_pieces(first_i)
 
@@ -664,6 +695,10 @@ def tile_compositionalkoopmanoperators_pa_kernel(
         load_pair(10)
         load_pair(11)
         run_job(job)
+        early, pieces = tuple(pieces[:R2X]), pieces[R2X:]
+        load_pieces(early)
+        for x in range(R2X):
+            lay_gpsimd(early, x)
         widen(7)
         product(1, 0, True)
         term_products(1)
@@ -710,6 +745,8 @@ def tile_compositionalkoopmanoperators_pa_kernel(
         quantise_pieces(two)
         if not G3FIRST:
             quantise_group(3)
+        if R2X:
+            quantise_pieces(early)
         quantise_pieces(job)
         relu_senders(1, 2, FOLD4, 0)
         relu_senders(1, 3, FOLD5, 0)

from contextlib import ExitStack

import concourse.mybir as mybir
from concourse.masks import make_identity

P = 128
NF = 1024
K_PASS = 512
PASSES = NF // K_PASS
GRAPHS = 4
N = 32
SENDERS = 4
GROUPS = N // SENDERS
PAIRS = 2 * GROUPS
PIECE = 256
SETS = NF // PIECE
CHUNKS = NF // P
RUN = 8
OUT_PARTS = 4
BANKS = 6

BEATS = {4: [(3, 0), (3, 1), (3, 1), (2, 1), (2, 1)], 7: [(3, 2), (3, 1), (3, 1), (2, 0)]}
STEADY = [(3, 1)] * 4
WEAVE0 = False
GFIRST = False
LAST = [4, 2, 2, 2]
GS = [0, 0, 0, 0, 1, 1, 1, 1]
JOB = [0, 0, 0, 0, 4, 4, 4, 3]
REST = {2: "S", 3: "G"}
ZFROM = {}
CFROM = {5: (7, 8), 6: (7, 8), 7: (7, 8)}
DRANGE = {0: (5, 6)}
NFOLD = {}
SUM_LAG = 1
SUM_SPLIT = 0
RELU_SPLIT = 0
EFF = 12
SHARE_LAST = 0
PA_GAP = 2
TERMS_RANK = 6
TERMS_COPY = 15
LOAD_AHEAD = 2
WIDEN_RANK = 7
FLOORS = 2
PARTS = 2
FOLD2 = False
FOLD3 = False
EXTRA = [(), (), (), (), (1,), (1,), (1,), ()]
CTO = 6
Q_TAIL = True
Q_RANK = 16
R0_RANK = 3
BEFORE = 3
SUMS = 3
G7 = 0
WIDE = 5
WIDEFOLD = True
R2X = 1
SLAY = [0] * 8
SOFF = 0
BACKS_AT = 7
QPOS = 3
FOLD4 = True
FOLD5 = True
G3FIRST = False
TAILQ = (5, 6, 7)
WIDEN_AHEAD = 3
TERMS_LATE = 1
VLAY = [0] * 8
O_AT = [0, 2]
APART = range(16)

F32 = mybir.dt.float32
BF16 = mybir.dt.bfloat16
U32 = mybir.dt.uint32
I32 = mybir.dt.int32
U8 = mybir.dt.uint8
FP8 = mybir.dt.float8_e4m3fn
FP8X4 = mybir.dt.float8_e4m3fn_x4
ALU = mybir.AluOpType
ACT = mybir.ActivationFunctionType
AX = mybir.AxisListType

FLOPS = 2 * GRAPHS * N * N * NF * NF + 4 * 2 * GRAPHS * N * NF * NF

LOAD, TURN0, COPY_OUT, SCALE, TERMS, MULTIPLY, COPY_TERMS, WIDEN, LAY, LATE, ADD, BACKS, CLOSE, GPSIMD, CLAMP, RELU, WEAVES, TURN, COPY2, LATER, SUM = range(21)


def tile_compositionalkoopmanoperators_pa_kernel(
    tc, rel_bytes, rel_scale, obj, rp_w, rp_b, pp_w, pp_b, out
):
    nc = tc.nc
    rel_rows = rel_bytes.rearrange("b i j k -> (b i) (j k)")
    obj_rows = obj.rearrange("b n k -> (b n) k")
    out_rows = out.rearrange("b n k -> (b n) k")
    source = {"r": (rp_w, 0), "i": (rp_w, NF), "s": (rp_w, 2 * NF), "o": (pp_w, 0), "a": (pp_w, NF)}

    with ExitStack() as ctx:
        keep = ctx.enter_context(tc.tile_pool(name="keep", bufs=1))
        work = ctx.enter_context(tc.tile_pool(name="work", bufs=1))
        psum = ctx.enter_context(tc.psum_pool(name="psum", bufs=1))

        def kept(shape, dtype, name):
            return keep.tile(shape, dtype, name=name, tag=name, align_bytes=64)

        def rotating(shape, dtype, name, bufs):
            return work.tile(shape, dtype, name=name, tag=name, bufs=bufs, align_bytes=64)

        def bank_tile(shape, dtype):
            return psum.tile(shape, dtype, name="bank", tag="bank", bufs=BANKS)

        ident = kept([P, P], F32, "ident")
        make_identity(nc, ident[:])

        ctx.enter_context(tc.manual_schedule())

        rel_raw = {}
        w_raw = {}

        def load_pair(m):
            rel_raw[m] = rotating([P, 2 * NF], U8, "rel_raw", 4)
            nc.sync.dma_start(out=rel_raw[m][:], in_=rel_rows[:, 2 * NF * m : 2 * NF * (m + 1)])

        def piece_rows(key, kp, c):
            w, row = source[key]
            rows = slice(row + K_PASS * kp, row + K_PASS * (kp + 1))
            return w[rows, PIECE * c : PIECE * (c + 1)].rearrange("(p t) n -> p t n", t=4)

        def load_pieces(pieces):
            for piece in pieces:
                w_raw[piece] = rotating([P, 4, PIECE], BF16, "w_raw", 4)
                nc.sync.dma_start(out=w_raw[piece][:], in_=piece_rows(*piece))

        def load_job(job):
            w_raw[job] = rotating([P, len(job), 4, PIECE], BF16, "job_raw", 2)
            for x, piece in enumerate(job):
                nc.sync.dma_start(out=w_raw[job][:, x], in_=piece_rows(*piece))

        scale = kept([P, PASSES, 4], F32, "scale")
        obj_sb = rotating([P, NF], BF16, "rows", 1)
        bias_rows = kept([P, P // 2], F32, "bias_rows")
        out_bias = {}

        def load_out_bias():
            out_bias[0] = rotating([P, NF], BF16, "rows", 1)
            nc.sync.dma_start(out=out_bias[0][:], in_=pp_b.partition_broadcast(P))

        nc.vector.memset(bias_rows[:], 0.0)
        ident_bf = kept([P, P], BF16, "ident_bf")
        nc.scalar.activation(ident_bf[:], ident[:], ACT.Relu)

        laid = {}
        w_codes = {}

        def laid_tile(pieces, last):
            if last:
                return rotating([P, len(pieces), 4 * PIECE], BF16, "job_laid", 1)
            return rotating([P, len(pieces), 4 * PIECE], BF16, "laid", 3)

        def lay(pieces, x, copy, last=False):
            if x == 0:
                laid[pieces] = laid_tile(pieces, last)
            copy(
                out=laid[pieces][:, x].rearrange("p (c i t) -> p c t i", i=RUN, t=4),
                in_=w_raw[pieces[x]][:].rearrange("p t (c i) -> p c t i", i=RUN),
            )

        woven = {}

        def weave(piece):
            woven[piece] = bank_tile([P, 4 * PIECE], BF16)
            for n in range(2):
                nc.tensor.matmul(
                    out=woven[piece][:, K_PASS * n : K_PASS * (n + 1)],
                    lhsT=ident_bf[:],
                    rhs=w_raw[piece][:, :, P * n : P * (n + 1)].rearrange("p t n -> p n t"),
                    start=True,
                    stop=True,
                )

        def lay_woven(pieces, x, last=False):
            if x == 0:
                laid[pieces] = laid_tile(pieces, last)
            nc.scalar.copy(out=laid[pieces][:, x], in_=woven[pieces[x]][:])

        def lay_gpsimd(pieces, x):
            if x == 0:
                laid[pieces] = laid_tile(pieces, False)
            nc.gpsimd.tensor_scalar(
                out=laid[pieces][:, x].rearrange("p (n t) -> p n t", t=4),
                in0=w_raw[pieces[x]][:].rearrange("p t n -> p n t"),
                scalar1=1.0,
                scalar2=0.0,
                op0=ALU.mult,
                op1=ALU.add,
            )

        def run_job(job, last=True, parts=1):
            laid[job] = laid_tile(job, last)
            size = len(job) // parts
            for first in range(0, len(job), size):
                nc.gpsimd.tensor_scalar(
                    out=laid[job][:, first : first + size].rearrange("p x (n t) -> p x n t", t=4),
                    in0=w_raw[job][:, first : first + size].rearrange("p x t n -> p x n t"),
                    scalar1=1.0,
                    scalar2=0.0,
                    op0=ALU.mult,
                    op1=ALU.add,
                )

        def quantise_pieces(pieces):
            name = "%s%d%d" % pieces[0]
            codes = kept([P, len(pieces) * PIECE], U32, "codes_" + name)
            scales = kept([P, len(pieces) * PIECE], U8, "scales_" + name)
            first = 0
            for width in (4, 2, 1):
                if len(pieces) & width:
                    cols = slice(PIECE * first, PIECE * (first + width))
                    nc.vector.quantize_mx(
                        out=codes[:, cols].bitcast(FP8X4),
                        scales=scales[:, cols],
                        in_=laid[pieces][:, first : first + width].rearrange("p x n -> p (x n)"),
                    )
                    first = first + width
            for x, piece in enumerate(pieces):
                w_codes[piece] = (codes, scales, PIECE * x)

        def piece_weights(piece, first, width):
            codes, scales, base = w_codes[piece]
            cols = slice(base + first, base + first + width)
            return codes[:, cols].bitcast(FP8X4), scales[:, cols]

        def chunk_weights(key, kp, q):
            return piece_weights((key, kp, q // 2), P * (q % 2), P)

        obj_laid = kept([P, PASSES * P * 4], BF16, "obj_laid")
        obj_codes = kept([P, PASSES, 2, P], U32, "obj_codes")
        obj_scales = kept([P, PASSES, 2, P], U8, "obj_scales")
        nc.vector.memset(obj_scales[:], 0)

        def quantise_particles():
            for kp in range(PASSES):
                nc.vector.quantize_mx(
                    out=obj_codes[:, kp, 0, :].bitcast(FP8X4),
                    scales=obj_scales[:, kp, 0, :],
                    in_=obj_laid[:, 4 * P * kp : 4 * P * (kp + 1)],
                )

        def repeat_particles():
            nc.vector.tensor_copy(out=obj_codes[:, :, 1, :], in_=obj_codes[:, :, 0, :])
            nc.vector.tensor_copy(out=obj_scales[:, :, 1, :].bitcast(U32), in_=obj_scales[:, :, 0, :].bitcast(U32))

        term_bank = {}
        recv = {}
        send = {}
        minus = {}

        def particles(kp):
            return obj_codes[:, kp, 0, :].bitcast(FP8X4), obj_scales[:, kp, 0, :]

        def term_products(c):
            term_bank[c] = bank_tile([P, 4, P], F32)
            for n, key in enumerate(("i", "s")):
                for m in range(2):
                    for kp in range(PASSES):
                        wc, ws = chunk_weights(key, kp, 2 * c + m)
                        oc, osc = particles(kp)
                        nc.tensor.matmul_mx(
                            out=term_bank[c][:, 2 * n + m, :],
                            lhsT=wc,
                            lhsT_scale=ws,
                            rhs=oc,
                            rhs_scale=osc,
                            start=(kp == 0),
                            stop=(kp == PASSES - 1),
                        )

        def copy_terms(c):
            recv[c] = kept([P, 2, P], F32, "recv%d" % c)
            send[c] = kept([P, 2, P], F32, "send%d" % c)
            for m in range(2):
                q = 2 * c + m
                nc.scalar.activation(
                    send[c][:, m, :], term_bank[c][:, 2 + m, :], ACT.Identity, bias=bias_cols[:, q : q + 1]
                )
            nc.scalar.copy(out=recv[c][:], in_=term_bank[c][:, 0:2, :])
            for m in range(2):
                q = 2 * c + m
                if q in ZFROM:
                    minus[q] = kept([P, P], F32, "minus%d" % q)
                    nc.scalar.activation(minus[q][:], term_bank[c][:, m, :], ACT.Copy, scale=-1.0)
                if q in CFROM or q in DRANGE:
                    minus[q] = kept([P, P], F32, "minus%d" % q)
                    nc.scalar.activation(minus[q][:], send[c][:, m, :], ACT.Copy, scale=-1.0)

        wide = {}
        turned = {}
        plain = {}
        rel_laid = {}
        rel_codes = [kept([P, PASSES * SENDERS * P], U32, "rel_codes%d" % g) for g in range(GROUPS)]
        bias_cols = kept([P, CHUNKS], F32, "bias_cols")
        rel_scales = [kept([P, PASSES * SENDERS * P], U8, "rel_scales%d" % g) for g in range(GROUPS)]

        def widen(m):
            wide[m] = rotating([P, 2 * NF], BF16, "wide", WIDE)
            if m in APART:
                nc.scalar.copy(
                    out=wide[m][:].rearrange("q (u x e) -> q u x e", u=2, e=2),
                    in_=rel_raw[m][:].bitcast(FP8).rearrange("q (x u e) -> q u x e", u=2, e=2),
                )
            else:
                nc.scalar.copy(out=wide[m][:], in_=rel_raw[m][:].bitcast(FP8))

        def turn(m, kp):
            turned[m, kp] = bank_tile([P, 2, 2, P], F32)
            words = wide[m][:].bitcast(F32)
            for u in range(2):
                for s in range(2):
                    if m in APART:
                        first = K_PASS * u + P * (2 * s + kp)
                        rows = words[:, first : first + P]
                    else:
                        first = K_PASS * s + 256 * kp
                        rows = words[:, first + u : first + 256 : 2]
                    nc.tensor.transpose(turned[m, kp][:, u, s, :], rows, ident[:])

        def open_group(m):
            if m // 2 not in rel_laid:
                rel_laid[m // 2] = rotating([P, PASSES, 2, 2 * P * 4], BF16, "rel_laid", 2)

        def scale_out(m, kp):
            open_group(m)
            values = turned[m, kp][:].rearrange("p u s r -> p (u s r)").bitcast(BF16)
            factors = scale[:, kp, :].rearrange("p (u e) -> p u e", u=2)
            nc.vector.tensor_tensor(
                out=rel_laid[m // 2][:, kp, m % 2, :].rearrange("p (x u e) -> p x u e", u=2, e=2),
                in0=values.rearrange("p (u x e) -> p x u e", u=2, e=2),
                in1=factors.unsqueeze(1).to_broadcast([P, 2 * P, 2, 2]),
                op=ALU.mult,
            )

        def copy_out(m, kp, count):
            open_group(m)
            if kp == 0:
                plain[m] = rotating([P, count, 2 * P * 4], BF16, "plain", 1)
            nc.scalar.copy(
                out=plain[m][:, kp, :].bitcast(F32).rearrange("p (x u) -> p x u", u=2),
                in_=turned[m, kp][:].rearrange("p u s r -> p (s r) u"),
            )

        def scale_plain(m, count):
            nc.gpsimd.tensor_tensor(
                out=rel_laid[m // 2][:, 0:count, m % 2, :].rearrange("p g (x t) -> p g x t", t=4),
                in0=plain[m][:].rearrange("p g (x t) -> p g x t", t=4),
                in1=scale[:, 0:count, :].unsqueeze(2).to_broadcast([P, count, 2 * P, 4]),
                op=ALU.mult,
            )

        def quantise_group(g):
            nc.vector.quantize_mx(
                out=rel_codes[g][:].bitcast(FP8X4),
                scales=rel_scales[g][:],
                in_=rel_laid[g][:].rearrange("p g m x -> p (g m x)"),
            )

        agg = [psum.tile([P, 4, P], F32, name="agg%d" % h, tag="agg%d" % h) for h in range(2)]
        clamped = {}
        for q in range(CHUNKS):
            if q in ZFROM:
                clamped[q] = (ZFROM[q], GROUPS)
            if q in CFROM:
                clamped[q] = CFROM[q]
            if q in DRANGE:
                clamped[q] = DRANGE[q]
        to_sum = [4 * N + len([q for q in clamped if q // 4 == h]) for h in range(2)]
        summed = [0, 0]
        acc = {}
        eff = {}
        floor = {}
        back = {}

        def eff_tile():
            return rotating([P, SENDERS, P], F32, "eff", EFF)

        def sender_terms(tile_, g):
            return (
                tile_.rearrange("p (b j) -> p j b", b=GRAPHS)[:, SENDERS * g : SENDERS * (g + 1), :]
                .unsqueeze(3)
                .to_broadcast([P, SENDERS, GRAPHS, N])
            )

        def build_floor(g, q):
            floor[g, q] = rotating([P, SENDERS, P], F32, "floor", FLOORS)
            nc.gpsimd.tensor_tensor(
                out=floor[g, q][:].rearrange("p s (b i) -> p s b i", b=GRAPHS),
                in0=minus[q][:].rearrange("p (b i) -> p b i", b=GRAPHS).unsqueeze(1).to_broadcast([P, SENDERS, GRAPHS, N]),
                in1=sender_terms(send[q // 2][:, q % 2, :], g),
                op=ALU.subtract,
            )

        def build_back(q):
            lo, hi = clamped[q]
            sums = kept([P, GRAPHS], F32, "sums%d" % q)
            back[q] = kept([P, P], F32, "back%d" % q)
            nc.vector.tensor_reduce(
                out=sums[:],
                in_=send[q // 2][:, q % 2, :].rearrange("p (b j) -> p b j", b=GRAPHS)[:, :, SENDERS * lo : SENDERS * hi],
                axis=AX.X,
                op=ALU.add,
            )
            return sums

        def finish_back(q, sums):
            lo, hi = clamped[q]
            nc.vector.scalar_tensor_tensor(
                out=back[q][:].rearrange("p (b i) -> p b i", b=GRAPHS),
                in0=recv[q // 2][:, q % 2, :].rearrange("p (b i) -> p b i", b=GRAPHS),
                scalar=float(SENDERS * (hi - lo)) if q in ZFROM else 0.0,
                in1=sums[:].unsqueeze(2).to_broadcast([P, GRAPHS, N]),
                op0=ALU.mult,
                op1=ALU.add,
            )

        def backs(qs):
            sums = [build_back(q) for q in qs]
            for q, sm in zip(qs, sums):
                finish_back(q, sm)

        def product(g, q, folded):
            acc[g, q] = bank_tile([P, SENDERS, P], F32)
            for kp in range(PASSES):
                wc, ws = chunk_weights("r", kp, q)
                cols = slice(SENDERS * P * kp, SENDERS * P * (kp + 1))
                nc.tensor.matmul_mx(
                    out=acc[g, q][:].rearrange("p s r -> p (s r)"),
                    lhsT=wc,
                    lhsT_scale=ws,
                    rhs=rel_codes[g][:, cols].bitcast(FP8X4),
                    rhs_scale=rel_scales[g][:, cols],
                    start=(kp == 0),
                    stop=(kp == PASSES - 1 and not folded),
                )
            for kp in range(PASSES if folded and WIDEFOLD else 0):
                wc, ws = chunk_weights("i", kp, q)
                for s in range(0, SENDERS, 2):
                    nc.tensor.matmul_mx(
                        out=acc[g, q][:, s : s + 2, :].rearrange("p s r -> p (s r)"),
                        lhsT=wc,
                        lhsT_scale=ws,
                        rhs=obj_codes[:, kp].rearrange("p s r -> p (s r)").bitcast(FP8X4),
                        rhs_scale=obj_scales[:, kp].rearrange("p s r -> p (s r)"),
                        start=False,
                        stop=(kp == PASSES - 1 and s == SENDERS - 2),
                    )
            for kp in range(PASSES if folded and not WIDEFOLD else 0):
                wc, ws = chunk_weights("i", kp, q)
                oc, osc = particles(kp)
                for s in range(SENDERS):
                    nc.tensor.matmul_mx(
                        out=acc[g, q][:, s, :],
                        lhsT=wc,
                        lhsT_scale=ws,
                        rhs=oc,
                        rhs_scale=osc,
                        start=False,
                        stop=(kp == PASSES - 1 and s == SENDERS - 1),
                    )

        def add_receivers(g, q, held=False):
            eff[g, q] = rotating([P, SENDERS, P], F32, "held", 2) if held else eff_tile()
            nc.vector.tensor_tensor(
                out=eff[g, q][:],
                in0=acc[g, q][:],
                in1=recv[q // 2][:, q % 2, :].unsqueeze(1).to_broadcast([P, SENDERS, P]),
                op=ALU.add,
            )

        def clamp_floor(g, q):
            eff[g, q] = eff_tile()
            nc.vector.tensor_tensor(out=eff[g, q][:], in0=acc[g, q][:], in1=floor[g, q][:], op=ALU.max)

        def clamp_senders(g, q, folded):
            if folded:
                eff[g, q] = eff_tile()
            src = acc[g, q] if folded else eff[g, q]
            nc.vector.tensor_tensor(
                out=eff[g, q][:].rearrange("p s (b i) -> p s b i", b=GRAPHS),
                in0=src[:].rearrange("p s (b i) -> p s b i", b=GRAPHS),
                in1=sender_terms(minus[q][:], g),
                op=ALU.max,
            )

        def relu_senders(g, q, folded, on_vector):
            if folded:
                eff[g, q] = eff_tile()
            src = acc[g, q] if folded else eff[g, q]
            for s in range(SENDERS):
                for b in range(GRAPHS):
                    sender = N * b + SENDERS * g + s
                    bias = send[q // 2][:, q % 2, sender : sender + 1]
                    cols = slice(N * b, N * (b + 1))
                    if s < on_vector:
                        nc.vector.tensor_scalar(
                            out=eff[g, q][:, s, cols],
                            in0=src[:, s, cols],
                            scalar1=bias,
                            scalar2=0.0,
                            op0=ALU.add,
                            op1=ALU.max,
                        )
                    else:
                        nc.scalar.activation(eff[g, q][:, s, cols], src[:, s, cols], ACT.Relu, bias=bias)

        def add_rows(q, rows):
            h = q // 4
            nc.tensor.matmul(
                out=agg[h][:, q % 4, :],
                lhsT=rows,
                rhs=ident[:],
                is_transpose=True,
                start=(summed[h] == 0),
                stop=(summed[h] == to_sum[h] - 1),
            )
            summed[h] = summed[h] + 1

        def sum_senders(g, q):
            for s in range(SENDERS):
                add_rows(q, eff[g, q][:, s, :])
            if q in clamped and g == GROUPS - 1:
                add_rows(q, back[q][:])

        agg_rows = {}
        agg_bank = {}
        agg_laid = {}
        agg_codes = {}
        agg_scales = {}
        final = {}

        def round_agg(h):
            agg_rows[h] = kept([P, K_PASS], BF16, "agg_rows%d" % h)
            nc.vector.tensor_copy(
                out=agg_rows[h][:].rearrange("p (u x e) -> p u x e", u=2, e=2),
                in_=agg[h][:].rearrange("p q f -> p (q f)").rearrange("p (x u e) -> p u x e", u=2, e=2),
            )

        def turn_agg(h):
            agg_bank[h] = bank_tile([P, 2, P], F32)
            words = agg_rows[h][:].bitcast(F32)
            for u in range(2):
                nc.tensor.transpose(agg_bank[h][:, u, :], words[:, P * u : P * (u + 1)], ident[:])

        def lay_agg(h):
            agg_laid[h] = kept([P, 4 * P], BF16, "agg_laid%d" % h)
            nc.scalar.copy(
                out=agg_laid[h][:].bitcast(F32).rearrange("p (r u) -> p r u", u=2),
                in_=agg_bank[h][:].rearrange("p u r -> p r u"),
            )

        def quantise_agg(h):
            agg_codes[h] = kept([P, P], U32, "agg_codes%d" % h)
            agg_scales[h] = kept([P, P], U8, "agg_scales%d" % h)
            nc.vector.quantize_mx(out=agg_codes[h][:].bitcast(FP8X4), scales=agg_scales[h][:], in_=agg_laid[h][:])

        def final_pass(key, kp):
            lc, ls = particles(kp) if key == "o" else (agg_codes[kp][:].bitcast(FP8X4), agg_scales[kp][:])
            for c in range(SETS):
                h, m = divmod(c, 2)
                if (key, kp, m) == ("o", 0, 0):
                    final[h] = bank_tile([P, K_PASS], F32)
                wc, ws = piece_weights((key, kp, c), 0, PIECE)
                nc.tensor.matmul_mx(
                    out=final[h][:, PIECE * m : PIECE * (m + 1)],
                    lhsT=lc,
                    lhsT_scale=ls,
                    rhs=wc,
                    rhs_scale=ws,
                    start=((key, kp, m) == ("o", 0, 0)),
                    stop=((key, kp, m) == ("a", PASSES - 1, 1)),
                )

        def finish(n):
            width = NF // OUT_PARTS
            cols = slice(width * n, width * (n + 1))
            h, first = divmod(width * n, K_PASS)
            result = eff_tile()[:].rearrange("p s r -> p (s r)")[:, 0:width]
            nc.vector.tensor_tensor(
                out=result, in0=final[h][:, first : first + width], in1=out_bias[0][:, cols], op=ALU.add
            )
            nc.scalar.activation(result, result, ACT.Relu)
            queue = nc.scalar if n == OUT_PARTS - 1 else nc.sync
            queue.dma_start(out=out_rows[:, cols], in_=result)

        first_r, first_s, first_i = (tuple((key, kp, 0) for kp in range(PASSES)) for key in ("r", "s", "i"))
        load_pair(0)
        nc.sync.dma_start(out=scale[:], in_=rel_scale.rearrange("a b c (g p t) -> p (a b c g) t", p=P, t=4))
        load_pieces(first_r)
        load_pair(1)
        nc.sync.dma_start(out=obj_sb[:], in_=obj_rows)
        load_job(first_s)
        nc.sync.dma_start(out=bias_rows[:].bitcast(BF16)[0:CHUNKS, :], in_=rp_b.rearrange("(q p) -> q p", p=P))
        load_pieces(first_i)
        load_pair(2)

        widen(0)
        for x in range(PASSES):
            lay(first_r, x, nc.vector.tensor_copy)
        for kp in range(PASSES):
            turn(0, kp)
        widen(1)
        scale_out(0, 0)
        quantise_pieces(first_r)
        obj_bank = bank_tile([P, 4, P], F32)
        obj_words = obj_sb[:].bitcast(F32)
        for kp in range(PASSES):
            for u in range(2):
                nc.tensor.transpose(obj_bank[:, 2 * kp + u, :], obj_words[:, 256 * kp + u : 256 * (kp + 1) : 2], ident[:])
        for kp in range(PASSES):
            turn(1, kp)
        bias_bank = bank_tile([P, P], BF16)
        nc.tensor.transpose(bias_bank[:], bias_rows[:].bitcast(BF16), ident_bf[:])
        run_job(first_s, last=False)
        scale_out(0, 1)
        for kp in range(PASSES):
            scale_out(1, kp)
        nc.scalar.copy(
            out=obj_laid[:].bitcast(F32).rearrange("p (g r u) -> p g r u", g=PASSES, u=2),
            in_=obj_bank[:].rearrange("p (g u) r -> p g r u", g=PASSES),
        )
        nc.scalar.copy(out=bias_cols[:], in_=bias_bank[:, 0:CHUNKS])
        pieces = [(key, kp, c) for c in range(1, SETS) for key in ("i", "s", "r") for kp in range(PASSES)]
        pieces += [(key, kp, c) for key in ("o", "a") for kp in range(PASSES) for c in range(SETS)]
        per_set = 3 * PASSES
        job, two = tuple(pieces[:4]), tuple(pieces[4:6])
        next_job, next_two = tuple(pieces[6:10]), tuple(pieces[10:12])
        pieces = pieces[2 * per_set :]
        load_pair(3)
        load_pieces(two)
        load_job(job)
        load_pair(4)
        load_pair(5)
        load_pieces(next_two)
        for m in range(6, 10):
            load_pair(m)
        load_job(next_job)
        for x in range(PASSES):
            weave(first_i[x])
        lay_woven(first_i, 0, last=True)
        widen(2)
        lay_woven(first_i, 1)
        widen(3)
        weave(two[0])
        for kp in range(PASSES):
            turn(2, kp)
        weave(two[1])
        for kp in range(PASSES):
            turn(3, kp)
        for x in range(2):
            lay_woven(two, x)
        quantise_particles()
        quantise_group(0)
        if WIDEFOLD:
            repeat_particles()
        quantise_pieces(first_s)
        quantise_pieces(first_i)

        run_job(job, parts=PARTS)
        term_products(0)
        for m in (2, 3):
            for kp in range(PASSES):
                scale_out(m, kp)
        widen(4)
        copy_terms(0)
        widen(5)
        product(0, 0, True)
        for kp in range(PASSES):
            turn(4, kp)
        product(0, 1, True)
        for kp in range(PASSES):
            turn(5, kp)
        for x in range(2):
            relu_senders(0, x, True, 0)
        for kp in range(PASSES):
            scale_out(4, kp)
        for x in range(2):
            weave(next_two[x])
        widen(6)
        for x in range(2):
            lay_woven(next_two, x)
        sum_senders(0, 0)
        quantise_group(1)
        quantise_pieces(two)
        quantise_pieces(job)

        job, two = next_job, next_two
        load_pair(10)
        load_pair(11)
        run_job(job)
        early, pieces = tuple(pieces[:R2X]), pieces[R2X:]
        load_pieces(early)
        for x in range(R2X):
            lay_gpsimd(early, x)
        widen(7)
        product(1, 0, True)
        term_products(1)
        for kp in range(PASSES):
            scale_out(5, kp)
        turn(6, 0)
        sum_senders(0, 1)
        turn(6, 1)
        relu_senders(1, 0, True, 0)
        copy_terms(1)
        widen(8)
        widen(9)
        product(1, 1, True)
        product(0, 2, FOLD2)
        product(0, 3, FOLD3)
        relu_senders(1, 1, True, 0)
        for kp in range(PASSES):
            scale_out(6, kp)
        for kp in range(PASSES):
            turn(7, kp)
        sum_senders(1, 0)
        if not FOLD2:
            add_receivers(0, 2)
        if not FOLD3:
            add_receivers(0, 3)
        if G7:
            copy_out(7, 0, 1)
            scale_plain(7, 1)
        relu_senders(0, 2, FOLD2, 0)
        widen(10)
        product(1, 2, FOLD4)
        product(1, 3, FOLD5)
        sum_senders(1, 1)
        for kp in range(G7, PASSES):
            scale_out(7, kp)
        relu_senders(0, 3, FOLD3, 0)
        if not FOLD4:
            add_receivers(1, 2)
        if not FOLD5:
            add_receivers(1, 3)
        quantise_group(2)
        if G3FIRST:
            quantise_group(3)
        quantise_pieces(two)
        if not G3FIRST:
            quantise_group(3)
        if R2X:
            quantise_pieces(early)
        quantise_pieces(job)
        relu_senders(1, 2, FOLD4, 0)
        relu_senders(1, 3, FOLD5, 0)
        widen(11)
        sum_senders(0, 2)
        sum_senders(0, 3)

        plan = {}

        def at(beat, rank, fn, *args):
            plan.setdefault((beat, rank), []).append((fn, args))

        count = []
        copies = []
        opens = {}
        closes = {0: -2, 1: -2, 2: -2, 3: -1}
        banks = [(m, kp) for m in range(8, PAIRS) for kp in range(PASSES)]
        for r in range(4, GROUPS):
            opens[r] = len(count)
            for units_, here in BEATS.get(r, STEADY):
                beat = len(count)
                count.append(units_)
                for m, kp in banks[:here]:
                    at(beat - 1, TURN, turn, m, kp)
                    if m > 11 and kp == 0:
                        at(beat - WIDEN_AHEAD - LOAD_AHEAD, LOAD, load_pair, m)
                        at(beat - WIDEN_AHEAD, WIDEN_RANK, widen, m)
                    if m % 2 == 0 and kp < GS[m // 2]:
                        at(beat - (BEFORE < 3), COPY2 if BEFORE < 3 else COPY_OUT, copy_out, m, kp, GS[m // 2])
                        copies.append(beat - 1)
                        if kp == GS[m // 2] - 1:
                            at(beat, GPSIMD, scale_plain, m, GS[m // 2])
                    else:
                        at(beat, SCALE, scale_out, m, kp)
                banks = banks[here:]
            closes[r] = len(count) - 1
            at(closes[r], LAY if r == GROUPS - 1 else CLOSE, quantise_group, r)
        supplied = len(count)
        count.extend(LAST)

        for r in range(4, GROUPS):
            job, pieces = tuple(pieces[: JOB[r]]), pieces[JOB[r] :]
            at(opens[r] - 3, LOAD, load_job, job)
            at(opens[r] - 1, GPSIMD, run_job, job)
            for size in EXTRA[r]:
                others, pieces = tuple(pieces[:size]), pieces[size:]
                at(opens[r] - 2, LOAD, load_pieces, others)
                for x in range(len(others)):
                    at(opens[r] - 1, GPSIMD, lay_gpsimd, others, x)
                at(closes[r], CLOSE, quantise_pieces, others)
            if SLAY[r]:
                his, pieces = tuple(pieces[: SLAY[r]]), pieces[SLAY[r] :]
                at(opens[r] - 2, LOAD, load_pieces, his)
                for x in range(len(his)):
                    at(opens[r] + 2 * x + SOFF, WIDEN, lay, his, x, nc.scalar.copy)
                at(closes[r], CLOSE, quantise_pieces, his)
            if VLAY[r]:
                mine, pieces = tuple(pieces[: VLAY[r]]), pieces[VLAY[r] :]
                at(opens[r], LOAD, load_pieces, mine)
                for x in range(len(mine)):
                    at(closes[r], BACKS, lay, mine, x, nc.vector.tensor_copy)
                at(closes[r], CLOSE, quantise_pieces, mine)
            at(closes[r], CLOSE, quantise_pieces, job)
        beat = supplied - 1
        last_job = None
        while pieces:
            job, pieces = tuple(pieces[:SETS]), pieces[SETS:]
            at(beat - 2, LOAD, load_job, job)
            at(beat, GPSIMD if beat < supplied else RELU, run_job, job)
            beat = beat + PA_GAP
            if pieces or not Q_TAIL:
                at(beat, CLAMP, quantise_pieces, job)
            else:
                last_job = job
        at(supplied, LOAD, load_out_bias)
        set_ready = {0: -2, 1: -2}
        for c in range(2, SETS):
            set_ready[c] = closes[c + 1] + 2 + TERMS_LATE
            at(closes[c + 1] + 1 + TERMS_LATE, TERMS_RANK, term_products, c)
            at(closes[c + 1] + 1 + TERMS_LATE, TERMS_COPY, copy_terms, c)
        if clamped:
            at(closes[BACKS_AT], BACKS, backs, sorted(clamped))

        units = [(g, q) for h in range(2) for g in range(GROUPS) for q in range(4 * h, 4 * h + 4) if g > 1 or q > 3]
        beat = 0
        last_sum = [0, 0]
        waiting = [(0, 1, 2), (0, 1, 3)]
        while units:
            ready = [(g, q) for g, q in units if max(closes[g] + 1, set_ready[q // 2]) < beat]
            ready += [(g, q) for g, q in units if max(closes[g] + 1, set_ready[q // 2]) == beat]
            burst = ready[: count[beat]]
            for n, (g, q) in enumerate(burst):
                units = [unit for unit in units if unit != (g, q)]
                inside = q in clamped and clamped[q][0] <= g < clamped[q][1]
                lag = SUM_LAG + (n >= SUM_SPLIT)
                if inside and q in ZFROM:
                    at(closes[g - 1] + 1, GPSIMD, build_floor, g, q)
                    at(beat, MULTIPLY, product, g, q, False)
                    at(beat, ADD, clamp_floor, g, q)
                elif inside and q in DRANGE:
                    at(beat, MULTIPLY, product, g, q, True)
                    at(beat, ADD, clamp_senders, g, q, True)
                elif inside and beat >= supplied:
                    at(beat, MULTIPLY, product, g, q, False)
                    at(beat, ADD, add_receivers, g, q)
                    lag = 99
                elif inside:
                    at(beat, MULTIPLY, product, g, q, False)
                    at(beat, ADD, add_receivers, g, q, True)
                    lag = min([closes[r] for r in closes if closes[r] >= beat] + [supplied - 1 + PA_GAP]) - beat
                    at(beat + lag, BACKS if beat < supplied else RELU, clamp_senders, g, q, False)
                    lag = lag + 1
                else:
                    folded = n < NFOLD.get(beat, 0)
                    at(beat, MULTIPLY, product, g, q, folded)
                    if not folded:
                        at(beat, ADD, add_receivers, g, q)
                    late = n >= RELU_SPLIT and not folded
                    at(beat + late, (LATER if beat + 1 in copies and n >= BEFORE else LATE) if late else RELU, relu_senders, g, q, folded, SENDERS // 2 if len(units) < SHARE_LAST else 0)
                waiting.append((beat + lag, g, q))
            beat = beat + 1
        when = 0
        while when < beat:
            due = [entry for entry in sorted(waiting) if entry[0] <= when][: SUMS + (when >= supplied - 1)]
            for entry in due:
                waiting.remove(entry)
                at(when, SUM, sum_senders, entry[1], entry[2])
            when = when + 1

        for place in sorted(plan):
            for fn, args in plan[place]:
                fn(*args)

        last = GROUPS - 1
        for q in TAILQ:
            clamp_senders(last, q, False)
        round_agg(0)
        final_pass("o", 0)
        for entry in sorted(waiting):
            sum_senders(entry[1], entry[2])
        round_agg(1)
        turn_agg(0)
        lay_agg(0)
        quantise_agg(0)
        quantise_pieces(last_job)
        final_pass("o", 1)
        turn_agg(1)
        lay_agg(1)
        quantise_agg(1)
        final_pass("a", 0)
        final_pass("a", 1)
        for n in range(OUT_PARTS):
            finish(n)
